import numpy as np
import ml_dtypes


def mxq(x, axis, fmt="e4m3"):
    dtype, down = {"e4m3": (ml_dtypes.float8_e4m3fn, 7), "e5m2": (ml_dtypes.float8_e5m2, 14)}[fmt]
    v = np.moveaxis(np.asarray(x, np.float32).astype(ml_dtypes.bfloat16).astype(np.float64), axis, -1)
    blocks = v.reshape(v.shape[:-1] + (-1, 32))
    amax = np.abs(blocks).max(-1, keepdims=True)
    byte = np.maximum(np.where(amax > 0, np.frexp(amax)[1] - 1 + 127, 0) - down, 1)
    scale = np.exp2(byte - 127.0)
    codes = (blocks / scale).astype(np.float32).astype(dtype).astype(np.float64)
    return np.moveaxis((codes * scale).reshape(v.shape), -1, axis)


WIDE = False


def mx_kscale(k):
    if not WIDE:
        return np.ones(k)
    levels = np.array([10, -10, 5, -5, 0])
    a = np.random.permutation(np.resize(levels, k // 512 * 4)).reshape(k // 512, 4)
    idx = np.arange(k)
    return np.exp2(a[idx // 512, idx % 128 // 32])


BF16 = ml_dtypes.bfloat16


def bf(x):
    return np.asarray(x, np.float32).astype(BF16)


def f64(x):
    return np.asarray(x).astype(np.float64)


N, D, F, DEG = 4096, 512, 128, 32


def gcn_norm(adjacency):
    n = adjacency.shape[0]
    ahat = adjacency + np.eye(n)
    deg = ahat.sum(axis=0)
    dinv = np.where(deg > 0, deg ** -0.5, 0.0)
    return dinv[:, None] * ahat * dinv[None, :]


def setup_inputs():
    s = mx_kscale(D)
    adjacency = (np.random.uniform(size=(N, N)) < DEG / N) * (1.0 - np.eye(N))
    return {"x": bf(np.random.standard_normal((N, D)) * s),
            "adjacency": bf(adjacency),
            "w": bf(np.random.standard_normal((D, F)) * np.sqrt(DEG / D) / s[:, None]),
            "b": bf(np.random.standard_normal(F) * 0.3)}


def reference(x, adjacency, w, b):
    an = gcn_norm(f64(adjacency))
    xw = mxq(f64(x), 1, "e4m3") @ mxq(f64(w), 0, "e4m3")
    agg = mxq(an.T, 1, "e4m3") @ mxq(xw, 0, "e4m3")
    return np.maximum(agg + f64(b), 0.0)

@@ -1,0 +1,244 @@
+from contextlib import ExitStack
+
+import concourse.bass as bass
+import concourse.mybir as mybir
+import concourse.tile as tile
+from concourse.masks import make_identity
+
+F32 = mybir.dt.float32
+BF16 = mybir.dt.bfloat16
+U32 = mybir.dt.uint32
+U8 = mybir.dt.uint8
+FP8X4 = mybir.dt.float8_e4m3fn_x4
+ALU = mybir.AluOpType
+ACT = mybir.ActivationFunctionType
+AX = mybir.AxisListType
+
+P = 128
+N = 4096
+D = 512
+F = 128
+PANEL = 1024
+NPAN = N // PANEL
+NPASS = N // 512
+UNIT_BUFS = 16
+LOOKAHEAD = 6
+TINY = 1e-30
+
+FLOPS = 2 * N * D * F + 2 * N * N * F
+
+
+def tile_simplegcn_pa_t_kernel(tc, x, adjacency, w, b, out):
+    nc = tc.nc
+    with ExitStack() as ctx:
+        const = ctx.enter_context(tc.tile_pool(name="const", bufs=1))
+        units = ctx.enter_context(tc.tile_pool(name="units", bufs=UNIT_BUFS))
+        grp = ctx.enter_context(tc.tile_pool(name="grp", bufs=3))
+        cod = ctx.enter_context(tc.tile_pool(name="cod", bufs=3))
+        small = ctx.enter_context(tc.tile_pool(name="small", bufs=2))
+        outp = ctx.enter_context(tc.tile_pool(name="outp", bufs=2))
+        accp = ctx.enter_context(tc.psum_pool(name="accp", bufs=4))
+        csp = ctx.enter_context(tc.psum_pool(name="csp", bufs=1))
+        vbp = ctx.enter_context(tc.psum_pool(name="vbp", bufs=1))
+        tpp = ctx.enter_context(tc.psum_pool(name="tpp", bufs=2))
+
+        ident_f = const.tile([P, P], F32)
+        make_identity(nc, ident_f[:])
+        ident_b = const.tile([P, P], BF16)
+        nc.vector.tensor_copy(out=ident_b[:], in_=ident_f[:])
+        ones = const.tile([P, 2], BF16)
+        nc.vector.memset(ones[:], 1.0)
+        warm = const.tile([P, 1], F32)
+        nc.vector.memset(warm[:], 1.0)
+        warm2 = const.tile([P, 1], F32)
+        nc.scalar.activation(out=warm2[:], in_=warm[:], func=ACT.Sqrt)
+
+        w_raw = const.tile([P, 4, F], BF16)
+        nc.sync.dma_start(
+            out=w_raw[:].rearrange("q (u e) f -> q u e f", u=2),
+            in_=w.rearrange("(u q e) f -> q u e f", u=2, e=2),
+        )
+        xunits = []
+        for g in range(4):
+            xu = units.tile([P, 8, D], BF16, tag="unit", name="xu%d" % g)
+            nc.sync.dma_start(out=xu[:], in_=x[1024 * g:1024 * (g + 1), :].rearrange("(r p) d -> p r d", p=P))
+            xunits.append(xu)
+        b_raw = const.tile([P, 1], BF16)
+        nc.sync.dma_start(out=b_raw[:], in_=b.rearrange("(p o) -> p o", o=1))
+        b_f = const.tile([P, 1], F32)
+        nc.vector.tensor_copy(out=b_f[:], in_=b_raw[:])
+
+        def load_unit(J, c):
+            u = units.tile([P, 4, PANEL], BF16, tag="unit", name="u%d_%d" % (J, c))
+            nc.sync.dma_start(
+                out=u[:],
+                in_=adjacency[512 * c:512 * (c + 1), PANEL * J:PANEL * (J + 1)].rearrange("(t p) w -> p t w", p=P),
+            )
+            return u
+
+        def load_panel(J):
+            cs = csp.tile([P, 8, NPASS], F32, tag="cs")
+            keep = {}
+            for c in range(NPASS):
+                u = load_unit(J, c)
+                if c // 2 == J:
+                    b0 = 4 * (c - 2 * J)
+                    blk = u[:].rearrange("p t (n k) -> p (t n) k", k=P)[:, b0:b0 + 28:9, :]
+                    nc.vector.tensor_tensor(out=blk, in0=blk, in1=ident_b[:].unsqueeze(1).to_broadcast([P, 4, P]), op=ALU.add)
+                for m in range(8):
+                    for t in range(4):
+                        nc.tensor.matmul(out=cs[:, m, c:c + 1], lhsT=u[:, t, P * m:P * (m + 1)], rhs=ones[:, 0:1],
+                                         start=(t == 0), stop=(t == 3))
+                if c < 2 * J + 2:
+                    keep[c] = u
+            return cs, keep
+
+        dinv = {}
+        vb = {}
+
+        def chain(J, cs):
+            deg = small.tile([P, 8], F32, tag="deg")
+            nc.vector.tensor_reduce(out=deg[:], in_=cs[:], axis=AX.X, op=ALU.add)
+            dcl = small.tile([P, 8], F32, tag="dcl")
+            nc.vector.tensor_scalar_max(out=dcl[:], in0=deg[:], scalar1=TINY)
+            sq = small.tile([P, 8], F32, tag="sq")
+            nc.scalar.activation(out=sq[:], in_=dcl[:], func=ACT.Sqrt)
+            rc = small.tile([P, 8], F32, tag="rc")
+            nc.vector.reciprocal(out=rc[:], in_=sq[:])
+            dv = const.tile([P, 8], F32, name="dinv%d" % J)
+            nc.vector.scalar_tensor_tensor(out=dv[:], in0=deg[:], scalar=0.0, in1=rc[:], op0=ALU.is_gt, op1=ALU.mult)
+            vbt = const.tile([P, PANEL], F32, name="vb%d" % J)
+            for h in range(2):
+                vps = vbp.tile([P, 512], F32, tag="vps")
+                for m in range(4):
+                    nc.tensor.matmul(out=vps[:, P * m:P * (m + 1)], lhsT=dv[:, 4 * h + m:4 * h + m + 1].to_broadcast([P, P]),
+                                     rhs=ident_f[:], start=True, stop=True)
+                nc.scalar.copy(out=vbt[:, 512 * h:512 * (h + 1)], in_=vps[:])
+            dinv[J] = dv
+            vb[J] = vbt
+
+        cs0, keep0 = load_panel(0)
+        kept = {0: keep0}
+
+        w_g = const.tile([P, F, 4], BF16, align_bytes=64)
+        nc.vector.tensor_copy(out=w_g[:], in_=w_raw[:].rearrange("q t f -> q f t"))
+        w_c = const.tile([P, F], U32, align_bytes=64)
+        w_s = const.tile([P, F], U8, align_bytes=64)
+        nc.vector.quantize_mx(out=w_c[:].bitcast(FP8X4), scales=w_s[:], in_=w_g[:].rearrange("q f t -> q (f t)"))
+
+        xw_c = const.tile([P, NPASS * F], U32, align_bytes=64)
+        xw_s = const.tile([P, NPASS * F], U8, align_bytes=64)
+        xw_g = grp.tile([P, 4 * PANEL], BF16, tag="ag", align_bytes=64)
+        xw_gv = xw_g[:].rearrange("p (c f t) -> p c f t", c=NPASS, t=4)
+        for g in range(4):
+            xu = xunits[g]
+            xg = grp.tile([P, 4 * PANEL], BF16, tag="ag", align_bytes=64)
+            xg32 = xg[:].bitcast(F32).rearrange("p (r i u) -> p r i u", r=8, u=2)
+            for k in range(4):
+                tp = tpp.tile([P, 2, 2, P], F32, tag="tp")
+                for r2 in range(2):
+                    xr = xu[:, 2 * k + r2, :].bitcast(F32)
+                    for u2 in range(2):
+                        nc.tensor.transpose(out=tp[:, r2, u2, :], in_=xr[:, P * u2:P * (u2 + 1)], identity=ident_f[:])
+                if k % 2 == 0:
+                    nc.vector.tensor_copy(out=xg32[:, 2 * k:2 * k + 2], in_=tp[:].rearrange("p r u i -> p r i u"))
+                else:
+                    nc.scalar.copy(out=xg32[:, 2 * k:2 * k + 2], in_=tp[:].rearrange("p r u i -> p r i u"))
+            xc = cod.tile([P, PANEL], U32, tag="cd", align_bytes=64)
+            xs = cod.tile([P, PANEL], U8, tag="sc", align_bytes=64)
+            nc.vector.quantize_mx(out=xc[:].bitcast(FP8X4), scales=xs[:], in_=xg[:])
+            for cc in range(2):
+                c = 2 * g + cc
+                xwp = tpp.tile([P, 4, F], F32, tag="tp")
+                for t in range(4):
+                    r = 4 * cc + t
+                    nc.tensor.matmul_mx(out=xwp[:, t, :], lhsT=xc[:, P * r:P * (r + 1)].bitcast(FP8X4),
+                                        lhsT_scale=xs[:, P * r:P * (r + 1)], rhs=w_c[:].bitcast(FP8X4), rhs_scale=w_s[:],
+                                        start=True, stop=True)
+                nc.scalar.copy(out=xw_gv[:, c], in_=xwp[:].rearrange("p t f -> p f t"))
+            if g % 2 == 1:
+                hh = g // 2
+                nc.vector.quantize_mx(out=xw_c[:, 512 * hh:512 * (hh + 1)].bitcast(FP8X4), scales=xw_s[:, 512 * hh:512 * (hh + 1)],
+                                      in_=xw_g[:, 2048 * hh:2048 * (hh + 1)])
+
+        def process(J, c, u, accs, first, last):
+            dv = dinv[c // 2]
+            for t in range(4):
+                k = (4 * c + t) % 8
+                nc.vector.scalar_tensor_tensor(out=u[:, t, :], in0=u[:, t, :], scalar=dv[:, k:k + 1], in1=vb[J][:],
+                                               op0=ALU.mult, op1=ALU.mult)
+            ag = grp.tile([P, 4 * PANEL], BF16, tag="ag", align_bytes=64)
+            nc.scalar.copy(out=ag[:].rearrange("p (n i t) -> p n t i", i=4, t=4),
+                           in_=u[:].rearrange("p t (n i) -> p n t i", i=4))
+            cd = cod.tile([P, PANEL], U32, tag="cd", align_bytes=64)
+            sc = cod.tile([P, PANEL], U8, tag="sc", align_bytes=64)
+            nc.vector.quantize_mx(out=cd[:].bitcast(FP8X4), scales=sc[:], in_=ag[:])
+            for h in range(2):
+                nc.tensor.matmul_mx(out=accs[h][:], lhsT=xw_c[:, F * c:F * (c + 1)].bitcast(FP8X4),
+                                    lhsT_scale=xw_s[:, F * c:F * (c + 1)],
+                                    rhs=cd[:, 512 * h:512 * (h + 1)].bitcast(FP8X4), rhs_scale=sc[:, 512 * h:512 * (h + 1)],
+                                    start=first, stop=last)
+
+        def new_accs():
+            acc0 = accp.tile([P, 512], F32, tag="acc")
+            acc1 = accp.tile([P, 512], F32, tag="acc")
+            return [acc0, acc1]
+
+        parts = {}
+
+        def park(J, accs):
+            part = const.tile([P, PANEL], F32, name="part%d" % J)
+            for h in range(2):
+                nc.scalar.copy(out=part[:, 512 * h:512 * (h + 1)], in_=accs[h][:])
+            parts[J] = part
+
+        def finish(J, accs):
+            res = outp.tile([P, PANEL], F32, tag="res")
+            for h in range(2):
+                sl = slice(512 * h, 512 * (h + 1))
+                if J in parts:
+                    nc.vector.tensor_tensor(out=res[:, sl], in0=accs[h][:], in1=parts[J][:, sl], op=ALU.add)
+                    nc.scalar.activation(out=res[:, sl], in_=res[:, sl], func=ACT.Relu, bias=b_f[:, 0:1], scale=1.0)
+                else:
+                    nc.scalar.activation(out=res[:, sl], in_=accs[h][:], func=ACT.Relu, bias=b_f[:, 0:1], scale=1.0)
+            ot = outp.tile([P, 8, F], F32, tag="ot")
+            for h in range(2):
+                tq = tpp.tile([P, 4, F], F32, tag="tp")
+                for m in range(4):
+                    nc.tensor.transpose(out=tq[:, m, :], in_=res[:, 512 * h + P * m:512 * h + P * (m + 1)], identity=ident_f[:])
+                nc.scalar.copy(out=ot[:, 4 * h:4 * h + 4, :], in_=tq[:])
+            nc.sync.dma_start(out=out[PANEL * J:PANEL * (J + 1), :].rearrange("(m p) f -> p m f", p=P), in_=ot[:])
+
+        def upper(J):
+            accs = new_accs()
+            last_c = 2 * J + 1
+            for c in range(last_c + 1):
+                process(J, c, kept[J][c], accs, c == 0, c == last_c)
+            return accs
+
+        chain(0, cs0)
+        for J in range(1, NPAN):
+            csJ, keepJ = load_panel(J)
+            kept[J] = keepJ
+            chain(J, csJ)
+            park(J - 1, upper(J - 1))
+
+        tail = [(NPAN - 1, c) for c in range(NPASS)]
+        for J in (2, 1, 0):
+            tail.extend([(J, c) for c in range(2 * J + 2, NPASS)])
+        loaded = {}
+        for c in range(NPASS):
+            loaded[(NPAN - 1, c)] = kept[NPAN - 1][c]
+        accs = None
+        for idx in range(len(tail)):
+            for q in range(idx, min(idx + LOOKAHEAD + 1, len(tail))):
+                if tail[q] not in loaded:
+                    loaded[tail[q]] = load_unit(tail[q][0], tail[q][1])
+            J, c = tail[idx]
+            first = idx == 0 or tail[idx - 1][0] != J
+            last = idx == len(tail) - 1 or tail[idx + 1][0] != J
+            if first:
+                accs = new_accs()
+            process(J, c, loaded[(J, c)], accs, first, last)
+            if last:
+                finish(J, accs)

@@ -37,9 +37,9 @@ def tile_simplegcn_pa_t_kernel(tc, x, adjacency, w, b, out):
         cod = ctx.enter_context(tc.tile_pool(name="cod", bufs=3))
         small = ctx.enter_context(tc.tile_pool(name="small", bufs=2))
         outp = ctx.enter_context(tc.tile_pool(name="outp", bufs=2))
-        accp = ctx.enter_context(tc.psum_pool(name="accp", bufs=4))
-        csp = ctx.enter_context(tc.psum_pool(name="csp", bufs=1))
-        vbp = ctx.enter_context(tc.psum_pool(name="vbp", bufs=1))
+        gtmp = ctx.enter_context(tc.tile_pool(name="gtmp", bufs=2))
+        accp = ctx.enter_context(tc.psum_pool(name="accp", bufs=2))
+        vbp = ctx.enter_context(tc.psum_pool(name="vbp", bufs=4))
         tpp = ctx.enter_context(tc.psum_pool(name="tpp", bufs=2))
 
         ident_f = const.tile([P, P], F32)
@@ -77,7 +77,7 @@ def tile_simplegcn_pa_t_kernel(tc, x, adjacency, w, b, out):
             return u
 
         def load_panel(J):
-            cs = csp.tile([P, 8, NPASS], F32, tag="cs")
+            cs = tpp.tile([P, 8, NPASS], F32, tag="tp")
             keep = {}
             for c in range(NPASS):
                 u = load_unit(J, c)
@@ -95,6 +95,17 @@ def tile_simplegcn_pa_t_kernel(tc, x, adjacency, w, b, out):
 
         dinv = {}
         vb = {}
+        vbps = {}
+
+        def broadcast(J):
+            banks = []
+            for h in range(2):
+                vps = vbp.tile([P, 512], F32, tag="vps", name="vps%d_%d" % (J, h))
+                for m in range(4):
+                    nc.tensor.matmul(out=vps[:, P * m:P * (m + 1)], lhsT=dinv[J][:, 4 * h + m:4 * h + m + 1].to_broadcast([P, P]),
+                                     rhs=ident_f[:], start=True, stop=True)
+                banks.append(vps)
+            vbps[J] = banks
 
         def chain(J, cs):
             deg = small.tile([P, 8], F32, tag="deg")
@@ -107,14 +118,11 @@ def tile_simplegcn_pa_t_kernel(tc, x, adjacency, w, b, out):
             nc.vector.reciprocal(out=rc[:], in_=sq[:])
             dv = const.tile([P, 8], F32, name="dinv%d" % J)
             nc.vector.scalar_tensor_tensor(out=dv[:], in0=deg[:], scalar=0.0, in1=rc[:], op0=ALU.is_gt, op1=ALU.mult)
+            dinv[J] = dv
+            broadcast(J)
             vbt = const.tile([P, PANEL], F32, name="vb%d" % J)
             for h in range(2):
-                vps = vbp.tile([P, 512], F32, tag="vps")
-                for m in range(4):
-                    nc.tensor.matmul(out=vps[:, P * m:P * (m + 1)], lhsT=dv[:, 4 * h + m:4 * h + m + 1].to_broadcast([P, P]),
-                                     rhs=ident_f[:], start=True, stop=True)
-                nc.scalar.copy(out=vbt[:, 512 * h:512 * (h + 1)], in_=vps[:])
-            dinv[J] = dv
+                nc.scalar.copy(out=vbt[:, 512 * h:512 * (h + 1)], in_=vbps[J][h][:])
             vb[J] = vbt
 
         cs0, keep0 = load_panel(0)
@@ -163,10 +171,16 @@ def tile_simplegcn_pa_t_kernel(tc, x, adjacency, w, b, out):
 
         def process(J, c, u, accs, first, last):
             dv = dinv[c // 2]
-            for t in range(4):
+            k3 = (4 * c + 3) % 8
+            tmp = gtmp.tile([P, PANEL], F32, tag="gt")
+            nc.gpsimd.tensor_scalar(out=tmp[:], in0=u[:, 3, :], scalar1=dv[:, k3:k3 + 1], scalar2=0.0, op0=ALU.mult, op1=ALU.add)
+            nc.gpsimd.tensor_tensor(out=u[:, 3, :], in0=tmp[:], in1=vb[J][:], op=ALU.mult)
+            for t in range(3):
                 k = (4 * c + t) % 8
-                nc.vector.scalar_tensor_tensor(out=u[:, t, :], in0=u[:, t, :], scalar=dv[:, k:k + 1], in1=vb[J][:],
-                                               op0=ALU.mult, op1=ALU.mult)
+                for h in range(2):
+                    sl = slice(512 * h, 512 * (h + 1))
+                    nc.vector.scalar_tensor_tensor(out=u[:, t, sl], in0=u[:, t, sl], scalar=dv[:, k:k + 1], in1=vbps[J][h][:],
+                                                   op0=ALU.mult, op1=ALU.mult)
             ag = grp.tile([P, 4 * PANEL], BF16, tag="ag", align_bytes=64)
             nc.scalar.copy(out=ag[:].rearrange("p (n i t) -> p n t i", i=4, t=4),
                            in_=u[:].rearrange("p t (n i) -> p n t i", i=4))
@@ -221,14 +235,16 @@ def tile_simplegcn_pa_t_kernel(tc, x, adjacency, w, b, out):
             csJ, keepJ = load_panel(J)
             kept[J] = keepJ
             chain(J, csJ)
-            park(J - 1, upper(J - 1))
+            if J < NPAN - 1:
+                park(J - 1, upper(J - 1))
 
-        tail = [(NPAN - 1, c) for c in range(NPASS)]
-        for J in (2, 1, 0):
+        tail = [(2, c) for c in range(NPASS)] + [(3, c) for c in range(NPASS)]
+        for J in (1, 0):
             tail.extend([(J, c) for c in range(2 * J + 2, NPASS)])
         loaded = {}
-        for c in range(NPASS):
-            loaded[(NPAN - 1, c)] = kept[NPAN - 1][c]
+        for J in (2, 3):
+            for c in kept[J]:
+                loaded[(J, c)] = kept[J][c]
         accs = None
         for idx in range(len(tail)):
             for q in range(idx, min(idx + LOOKAHEAD + 1, len(tail))):
@@ -239,6 +255,10 @@ def tile_simplegcn_pa_t_kernel(tc, x, adjacency, w, b, out):
             last = idx == len(tail) - 1 or tail[idx + 1][0] != J
             if first:
                 accs = new_accs()
+                if J == 3:
+                    broadcast(1)
+                if J == 1:
+                    broadcast(0)
             process(J, c, loaded[(J, c)], accs, first, last)
             if last:
                 finish(J, accs)

@@ -1,8 +1,6 @@
 from contextlib import ExitStack
 
-import concourse.bass as bass
 import concourse.mybir as mybir
-import concourse.tile as tile
 from concourse.masks import make_identity
 
 F32 = mybir.dt.float32
@@ -21,8 +19,9 @@ F = 128
 PANEL = 1024
 NPAN = N // PANEL
 NPASS = N // 512
-UNIT_BUFS = 16
-LOOKAHEAD = 6
+UNIT_BUFS = 15
+COD_BUFS = 8
+LOOKAHEAD = 5
 TINY = 1e-30
 
 FLOPS = 2 * N * D * F + 2 * N * N * F
@@ -34,12 +33,10 @@ def tile_simplegcn_pa_t_kernel(tc, x, adjacency, w, b, out):
         const = ctx.enter_context(tc.tile_pool(name="const", bufs=1))
         units = ctx.enter_context(tc.tile_pool(name="units", bufs=UNIT_BUFS))
         grp = ctx.enter_context(tc.tile_pool(name="grp", bufs=3))
-        cod = ctx.enter_context(tc.tile_pool(name="cod", bufs=3))
+        cod = ctx.enter_context(tc.tile_pool(name="cod", bufs=COD_BUFS))
         small = ctx.enter_context(tc.tile_pool(name="small", bufs=2))
         outp = ctx.enter_context(tc.tile_pool(name="outp", bufs=2))
-        gtmp = ctx.enter_context(tc.tile_pool(name="gtmp", bufs=2))
-        accp = ctx.enter_context(tc.psum_pool(name="accp", bufs=2))
-        vbp = ctx.enter_context(tc.psum_pool(name="vbp", bufs=4))
+        accp = ctx.enter_context(tc.psum_pool(name="accp", bufs=6))
         tpp = ctx.enter_context(tc.psum_pool(name="tpp", bufs=2))
 
         ident_f = const.tile([P, P], F32)
@@ -58,11 +55,6 @@ def tile_simplegcn_pa_t_kernel(tc, x, adjacency, w, b, out):
             out=w_raw[:].rearrange("q (u e) f -> q u e f", u=2),
             in_=w.rearrange("(u q e) f -> q u e f", u=2, e=2),
         )
-        xunits = []
-        for g in range(4):
-            xu = units.tile([P, 8, D], BF16, tag="unit", name="xu%d" % g)
-            nc.sync.dma_start(out=xu[:], in_=x[1024 * g:1024 * (g + 1), :].rearrange("(r p) d -> p r d", p=P))
-            xunits.append(xu)
         b_raw = const.tile([P, 1], BF16)
         nc.sync.dma_start(out=b_raw[:], in_=b.rearrange("(p o) -> p o", o=1))
         b_f = const.tile([P, 1], F32)
@@ -77,7 +69,7 @@ def tile_simplegcn_pa_t_kernel(tc, x, adjacency, w, b, out):
             return u
 
         def load_panel(J):
-            cs = tpp.tile([P, 8, NPASS], F32, tag="tp")
+            cs = tpp.tile([P, 8, NPASS], F32, tag="tp", name="cs%d" % J)
             keep = {}
             for c in range(NPASS):
                 u = load_unit(J, c)
@@ -95,17 +87,6 @@ def tile_simplegcn_pa_t_kernel(tc, x, adjacency, w, b, out):
 
         dinv = {}
         vb = {}
-        vbps = {}
-
-        def broadcast(J):
-            banks = []
-            for h in range(2):
-                vps = vbp.tile([P, 512], F32, tag="vps", name="vps%d_%d" % (J, h))
-                for m in range(4):
-                    nc.tensor.matmul(out=vps[:, P * m:P * (m + 1)], lhsT=dinv[J][:, 4 * h + m:4 * h + m + 1].to_broadcast([P, P]),
-                                     rhs=ident_f[:], start=True, stop=True)
-                banks.append(vps)
-            vbps[J] = banks
 
         def chain(J, cs):
             deg = small.tile([P, 8], F32, tag="deg")
@@ -118,24 +99,90 @@ def tile_simplegcn_pa_t_kernel(tc, x, adjacency, w, b, out):
             nc.vector.reciprocal(out=rc[:], in_=sq[:])
             dv = const.tile([P, 8], F32, name="dinv%d" % J)
             nc.vector.scalar_tensor_tensor(out=dv[:], in0=deg[:], scalar=0.0, in1=rc[:], op0=ALU.is_gt, op1=ALU.mult)
-            dinv[J] = dv
-            broadcast(J)
             vbt = const.tile([P, PANEL], F32, name="vb%d" % J)
             for h in range(2):
-                nc.scalar.copy(out=vbt[:, 512 * h:512 * (h + 1)], in_=vbps[J][h][:])
+                vps = tpp.tile([P, 512], F32, tag="tp", name="vps%d_%d" % (J, h))
+                for m in range(4):
+                    k = 4 * h + m
+                    nc.tensor.transpose(out=vps[:, P * m:P * (m + 1)], in_=dv[:, k:k + 1].to_broadcast([P, P]), identity=ident_f[:])
+                if h == 0:
+                    nc.vector.tensor_copy(out=vbt[:, 0:512], in_=vps[:])
+                else:
+                    nc.scalar.copy(out=vbt[:, 512:1024], in_=vps[:])
+            dinv[J] = dv
             vb[J] = vbt
 
-        cs0, keep0 = load_panel(0)
-        kept = {0: keep0}
+        xw_c = const.tile([P, NPASS * F], U32, align_bytes=64)
+        xw_s = const.tile([P, NPASS * F], U8, align_bytes=64)
 
+        def scale(J, c, u, cols):
+            dv = dinv[c // 2]
+            for t in range(4):
+                k = (4 * c + t) % 8
+                nc.vector.scalar_tensor_tensor(out=u[:, t, cols], in0=u[:, t, cols], scalar=dv[:, k:k + 1], in1=vb[J][:, cols],
+                                               op0=ALU.mult, op1=ALU.mult)
+
+        def quantise(u, cols, width):
+            ag = grp.tile([P, 4 * width], BF16, tag="ag", align_bytes=64)
+            nc.scalar.copy(out=ag[:].rearrange("p (n i t) -> p n t i", i=4, t=4),
+                           in_=u[:, :, cols].rearrange("p t (n i) -> p n t i", i=4))
+            cd = cod.tile([P, width], U32, tag="cd", align_bytes=64)
+            sc = cod.tile([P, width], U8, tag="sc", align_bytes=64)
+            nc.vector.quantize_mx(out=cd[:].bitcast(FP8X4), scales=sc[:], in_=ag[:])
+            return cd, sc
+
+        acc = {}
+        seen = {}
+
+        def multiply(J, c, h, cd, sc, off):
+            if (J, h) not in acc:
+                acc[(J, h)] = accp.tile([P, 512], F32, tag="acc", name="acc%d_%d" % (J, h))
+                seen[(J, h)] = 0
+            seen[(J, h)] += 1
+            nc.tensor.matmul_mx(out=acc[(J, h)][:], lhsT=xw_c[:, F * c:F * (c + 1)].bitcast(FP8X4),
+                                lhsT_scale=xw_s[:, F * c:F * (c + 1)],
+                                rhs=cd[:, off:off + 512].bitcast(FP8X4), rhs_scale=sc[:, off:off + 512],
+                                start=(seen[(J, h)] == 1), stop=(seen[(J, h)] == NPASS))
+
+        def finish(J, h):
+            res = outp.tile([P, 512], F32, tag="res")
+            nc.scalar.activation(out=res[:], in_=acc[(J, h)][:], func=ACT.Relu, bias=b_f[:, 0:1], scale=1.0)
+            tq = tpp.tile([P, 4, F], F32, tag="tp")
+            for m in range(4):
+                nc.tensor.transpose(out=tq[:, m, :], in_=res[:, P * m:P * (m + 1)], identity=ident_f[:])
+            ot = outp.tile([P, 4, F], F32, tag="ot")
+            nc.scalar.copy(out=ot[:], in_=tq[:])
+            r0 = PANEL * J + 512 * h
+            nc.sync.dma_start(out=out[r0:r0 + 512, :].rearrange("(m p) f -> p m f", p=P), in_=ot[:])
+
+        ALLC = slice(0, PANEL)
+
+        kept = {}
+        cs0, kept[0] = load_panel(0)
         w_g = const.tile([P, F, 4], BF16, align_bytes=64)
         nc.vector.tensor_copy(out=w_g[:], in_=w_raw[:].rearrange("q t f -> q f t"))
         w_c = const.tile([P, F], U32, align_bytes=64)
         w_s = const.tile([P, F], U8, align_bytes=64)
         nc.vector.quantize_mx(out=w_c[:].bitcast(FP8X4), scales=w_s[:], in_=w_g[:].rearrange("q f t -> q (f t)"))
+        chain(0, cs0)
+        cs1, kept[1] = load_panel(1)
+        chain(1, cs1)
+        xunits = []
+        for g in range(4):
+            xu = units.tile([P, 8, D], BF16, tag="unit", name="xu%d" % g)
+            nc.sync.dma_start(out=xu[:], in_=x[1024 * g:1024 * (g + 1), :].rearrange("(r p) d -> p r d", p=P))
+            xunits.append(xu)
 
-        xw_c = const.tile([P, NPASS * F], U32, align_bytes=64)
-        xw_s = const.tile([P, NPASS * F], U8, align_bytes=64)
+        waiting = []
+        for c in range(2):
+            scale(0, c, kept[0][c], ALLC)
+            waiting.append((0, c, quantise(kept[0][c], ALLC, PANEL)))
+        cs2, kept[2] = load_panel(2)
+        chain(2, cs2)
+        for c in range(4):
+            scale(1, c, kept[1][c], ALLC)
+            waiting.append((1, c, quantise(kept[1][c], ALLC, PANEL)))
+
         xw_g = grp.tile([P, 4 * PANEL], BF16, tag="ag", align_bytes=64)
         xw_gv = xw_g[:].rearrange("p (c f t) -> p c f t", c=NPASS, t=4)
         for g in range(4):
@@ -143,21 +190,18 @@ def tile_simplegcn_pa_t_kernel(tc, x, adjacency, w, b, out):
             xg = grp.tile([P, 4 * PANEL], BF16, tag="ag", align_bytes=64)
             xg32 = xg[:].bitcast(F32).rearrange("p (r i u) -> p r i u", r=8, u=2)
             for k in range(4):
-                tp = tpp.tile([P, 2, 2, P], F32, tag="tp")
+                tp = accp.tile([P, 2, 2, P], F32, tag="acc", name="xt%d_%d" % (g, k))
                 for r2 in range(2):
                     xr = xu[:, 2 * k + r2, :].bitcast(F32)
                     for u2 in range(2):
                         nc.tensor.transpose(out=tp[:, r2, u2, :], in_=xr[:, P * u2:P * (u2 + 1)], identity=ident_f[:])
-                if k % 2 == 0:
-                    nc.vector.tensor_copy(out=xg32[:, 2 * k:2 * k + 2], in_=tp[:].rearrange("p r u i -> p r i u"))
-                else:
-                    nc.scalar.copy(out=xg32[:, 2 * k:2 * k + 2], in_=tp[:].rearrange("p r u i -> p r i u"))
+                nc.scalar.copy(out=xg32[:, 2 * k:2 * k + 2], in_=tp[:].rearrange("p r u i -> p r i u"))
             xc = cod.tile([P, PANEL], U32, tag="cd", align_bytes=64)
             xs = cod.tile([P, PANEL], U8, tag="sc", align_bytes=64)
             nc.vector.quantize_mx(out=xc[:].bitcast(FP8X4), scales=xs[:], in_=xg[:])
             for cc in range(2):
                 c = 2 * g + cc
-                xwp = tpp.tile([P, 4, F], F32, tag="tp")
+                xwp = accp.tile([P, 4, F], F32, tag="acc", name="xwp%d" % c)
                 for t in range(4):
                     r = 4 * cc + t
                     nc.tensor.matmul_mx(out=xwp[:, t, :], lhsT=xc[:, P * r:P * (r + 1)].bitcast(FP8X4),
@@ -169,74 +213,12 @@ def tile_simplegcn_pa_t_kernel(tc, x, adjacency, w, b, out):
                 nc.vector.quantize_mx(out=xw_c[:, 512 * hh:512 * (hh + 1)].bitcast(FP8X4), scales=xw_s[:, 512 * hh:512 * (hh + 1)],
                                       in_=xw_g[:, 2048 * hh:2048 * (hh + 1)])
 
-        def process(J, c, u, accs, first, last):
-            dv = dinv[c // 2]
-            k3 = (4 * c + 3) % 8
-            tmp = gtmp.tile([P, PANEL], F32, tag="gt")
-            nc.gpsimd.tensor_scalar(out=tmp[:], in0=u[:, 3, :], scalar1=dv[:, k3:k3 + 1], scalar2=0.0, op0=ALU.mult, op1=ALU.add)
-            nc.gpsimd.tensor_tensor(out=u[:, 3, :], in0=tmp[:], in1=vb[J][:], op=ALU.mult)
-            for t in range(3):
-                k = (4 * c + t) % 8
-                for h in range(2):
-                    sl = slice(512 * h, 512 * (h + 1))
-                    nc.vector.scalar_tensor_tensor(out=u[:, t, sl], in0=u[:, t, sl], scalar=dv[:, k:k + 1], in1=vbps[J][h][:],
-                                                   op0=ALU.mult, op1=ALU.mult)
-            ag = grp.tile([P, 4 * PANEL], BF16, tag="ag", align_bytes=64)
-            nc.scalar.copy(out=ag[:].rearrange("p (n i t) -> p n t i", i=4, t=4),
-                           in_=u[:].rearrange("p t (n i) -> p n t i", i=4))
-            cd = cod.tile([P, PANEL], U32, tag="cd", align_bytes=64)
-            sc = cod.tile([P, PANEL], U8, tag="sc", align_bytes=64)
-            nc.vector.quantize_mx(out=cd[:].bitcast(FP8X4), scales=sc[:], in_=ag[:])
+        for J, c, pair in waiting:
             for h in range(2):
-                nc.tensor.matmul_mx(out=accs[h][:], lhsT=xw_c[:, F * c:F * (c + 1)].bitcast(FP8X4),
-                                    lhsT_scale=xw_s[:, F * c:F * (c + 1)],
-                                    rhs=cd[:, 512 * h:512 * (h + 1)].bitcast(FP8X4), rhs_scale=sc[:, 512 * h:512 * (h + 1)],
-                                    start=first, stop=last)
+                multiply(J, c, h, pair[0], pair[1], 512 * h)
 
-        def new_accs():
-            acc0 = accp.tile([P, 512], F32, tag="acc")
-            acc1 = accp.tile([P, 512], F32, tag="acc")
-            return [acc0, acc1]
-
-        parts = {}
-
-        def park(J, accs):
-            part = const.tile([P, PANEL], F32, name="part%d" % J)
-            for h in range(2):
-                nc.scalar.copy(out=part[:, 512 * h:512 * (h + 1)], in_=accs[h][:])
-            parts[J] = part
-
-        def finish(J, accs):
-            res = outp.tile([P, PANEL], F32, tag="res")
-            for h in range(2):
-                sl = slice(512 * h, 512 * (h + 1))
-                if J in parts:
-                    nc.vector.tensor_tensor(out=res[:, sl], in0=accs[h][:], in1=parts[J][:, sl], op=ALU.add)
-                    nc.scalar.activation(out=res[:, sl], in_=res[:, sl], func=ACT.Relu, bias=b_f[:, 0:1], scale=1.0)
-                else:
-                    nc.scalar.activation(out=res[:, sl], in_=accs[h][:], func=ACT.Relu, bias=b_f[:, 0:1], scale=1.0)
-            ot = outp.tile([P, 8, F], F32, tag="ot")
-            for h in range(2):
-                tq = tpp.tile([P, 4, F], F32, tag="tp")
-                for m in range(4):
-                    nc.tensor.transpose(out=tq[:, m, :], in_=res[:, 512 * h + P * m:512 * h + P * (m + 1)], identity=ident_f[:])
-                nc.scalar.copy(out=ot[:, 4 * h:4 * h + 4, :], in_=tq[:])
-            nc.sync.dma_start(out=out[PANEL * J:PANEL * (J + 1), :].rearrange("(m p) f -> p m f", p=P), in_=ot[:])
-
-        def upper(J):
-            accs = new_accs()
-            last_c = 2 * J + 1
-            for c in range(last_c + 1):
-                process(J, c, kept[J][c], accs, c == 0, c == last_c)
-            return accs
-
-        chain(0, cs0)
-        for J in range(1, NPAN):
-            csJ, keepJ = load_panel(J)
-            kept[J] = keepJ
-            chain(J, csJ)
-            if J < NPAN - 1:
-                park(J - 1, upper(J - 1))
+        cs3, kept[3] = load_panel(3)
+        chain(3, cs3)
 
         tail = [(2, c) for c in range(NPASS)] + [(3, c) for c in range(NPASS)]
         for J in (1, 0):
@@ -245,20 +227,23 @@ def tile_simplegcn_pa_t_kernel(tc, x, adjacency, w, b, out):
         for J in (2, 3):
             for c in kept[J]:
                 loaded[(J, c)] = kept[J][c]
-        accs = None
         for idx in range(len(tail)):
             for q in range(idx, min(idx + LOOKAHEAD + 1, len(tail))):
                 if tail[q] not in loaded:
                     loaded[tail[q]] = load_unit(tail[q][0], tail[q][1])
             J, c = tail[idx]
-            first = idx == 0 or tail[idx - 1][0] != J
-            last = idx == len(tail) - 1 or tail[idx + 1][0] != J
-            if first:
-                accs = new_accs()
-                if J == 3:
-                    broadcast(1)
-                if J == 1:
-                    broadcast(0)
-            process(J, c, loaded[(J, c)], accs, first, last)
-            if last:
-                finish(J, accs)
+            u = loaded[(J, c)]
+            if idx < len(tail) - 1:
+                scale(J, c, u, ALLC)
+                cd, sc = quantise(u, ALLC, PANEL)
+                for h in range(2):
+                    multiply(J, c, h, cd, sc, 512 * h)
+                    if seen[(J, h)] == NPASS:
+                        finish(J, h)
+            else:
+                for h in range(2):
+                    scale(J, c, u, slice(512 * h, 512 * (h + 1)))
+                for h in range(2):
+                    cd, sc = quantise(u, slice(512 * h, 512 * (h + 1)), 512)
+                    multiply(J, c, h, cd, sc, 0)
+                    finish(J, h)

@@ -19,8 +19,8 @@ F = 128
 PANEL = 1024
 NPAN = N // PANEL
 NPASS = N // 512
-UNIT_BUFS = 15
-COD_BUFS = 8
+UNIT_BUFS = 14
+COD_BUFS = 7
 LOOKAHEAD = 5
 TINY = 1e-30
 
@@ -36,7 +36,9 @@ def tile_simplegcn_pa_t_kernel(tc, x, adjacency, w, b, out):
         cod = ctx.enter_context(tc.tile_pool(name="cod", bufs=COD_BUFS))
         small = ctx.enter_context(tc.tile_pool(name="small", bufs=2))
         outp = ctx.enter_context(tc.tile_pool(name="outp", bufs=2))
-        accp = ctx.enter_context(tc.psum_pool(name="accp", bufs=6))
+        gtmp = ctx.enter_context(tc.tile_pool(name="gtmp", bufs=2))
+        accp = ctx.enter_context(tc.psum_pool(name="accp", bufs=4))
+        vbp = ctx.enter_context(tc.psum_pool(name="vbp", bufs=2))
         tpp = ctx.enter_context(tc.psum_pool(name="tpp", bufs=2))
 
         ident_f = const.tile([P, P], F32)
@@ -115,12 +117,31 @@ def tile_simplegcn_pa_t_kernel(tc, x, adjacency, w, b, out):
         xw_c = const.tile([P, NPASS * F], U32, align_bytes=64)
         xw_s = const.tile([P, NPASS * F], U8, align_bytes=64)
 
-        def scale(J, c, u, cols):
+        vbk = {}
+
+        def broadcast(J):
+            for h in range(2):
+                bank = vbp.tile([P, 512], F32, tag="vbk", name="vbk%d_%d" % (J, h))
+                for m in range(4):
+                    k = 4 * h + m
+                    nc.tensor.transpose(out=bank[:, P * m:P * (m + 1)], in_=dinv[J][:, k:k + 1].to_broadcast([P, P]), identity=ident_f[:])
+                vbk[h] = bank
+
+        def scale(J, c, u, use_g):
             dv = dinv[c // 2]
-            for t in range(4):
-                k = (4 * c + t) % 8
-                nc.vector.scalar_tensor_tensor(out=u[:, t, cols], in0=u[:, t, cols], scalar=dv[:, k:k + 1], in1=vb[J][:, cols],
-                                               op0=ALU.mult, op1=ALU.mult)
+            rows = 4
+            if use_g:
+                rows = 3
+                k3 = (4 * c + 3) % 8
+                gx = gtmp.tile([P, PANEL], F32, tag="gx")
+                nc.vector.tensor_scalar_mul(out=gx[:], in0=u[:, 3, :], scalar1=dv[:, k3:k3 + 1])
+                nc.gpsimd.tensor_tensor(out=u[:, 3, :], in0=gx[:], in1=vb[J][:], op=ALU.mult)
+            for h in range(2):
+                cols = slice(512 * h, 512 * (h + 1))
+                for t in range(rows):
+                    k = (4 * c + t) % 8
+                    nc.vector.scalar_tensor_tensor(out=u[:, t, cols], in0=u[:, t, cols], scalar=dv[:, k:k + 1], in1=vbk[h][:],
+                                                   op0=ALU.mult, op1=ALU.mult)
 
         def quantise(u, cols, width):
             ag = grp.tile([P, 4 * width], BF16, tag="ag", align_bytes=64)
@@ -133,20 +154,28 @@ def tile_simplegcn_pa_t_kernel(tc, x, adjacency, w, b, out):
 
         acc = {}
         seen = {}
+        part0 = const.tile([P, PANEL], F32)
 
         def multiply(J, c, h, cd, sc, off):
-            if (J, h) not in acc:
+            if acc.get((J, h)) is None:
                 acc[(J, h)] = accp.tile([P, 512], F32, tag="acc", name="acc%d_%d" % (J, h))
-                seen[(J, h)] = 0
-            seen[(J, h)] += 1
+            seen[(J, h)] = seen.get((J, h), 0) + 1
+            n = seen[(J, h)]
             nc.tensor.matmul_mx(out=acc[(J, h)][:], lhsT=xw_c[:, F * c:F * (c + 1)].bitcast(FP8X4),
                                 lhsT_scale=xw_s[:, F * c:F * (c + 1)],
                                 rhs=cd[:, off:off + 512].bitcast(FP8X4), rhs_scale=sc[:, off:off + 512],
-                                start=(seen[(J, h)] == 1), stop=(seen[(J, h)] == NPASS))
+                                start=(n == 1 or (J == 0 and n == 3)), stop=(n == NPASS or (J == 0 and n == 2)))
+            if J == 0 and n == 2:
+                nc.scalar.copy(out=part0[:, 512 * h:512 * (h + 1)], in_=acc[(J, h)][:])
+                acc[(J, h)] = None
 
         def finish(J, h):
             res = outp.tile([P, 512], F32, tag="res")
-            nc.scalar.activation(out=res[:], in_=acc[(J, h)][:], func=ACT.Relu, bias=b_f[:, 0:1], scale=1.0)
+            if J == 0:
+                nc.vector.tensor_tensor(out=res[:], in0=acc[(J, h)][:], in1=part0[:, 512 * h:512 * (h + 1)], op=ALU.add)
+                nc.scalar.activation(out=res[:], in_=res[:], func=ACT.Relu, bias=b_f[:, 0:1], scale=1.0)
+            else:
+                nc.scalar.activation(out=res[:], in_=acc[(J, h)][:], func=ACT.Relu, bias=b_f[:, 0:1], scale=1.0)
             tq = tpp.tile([P, 4, F], F32, tag="tp")
             for m in range(4):
                 nc.tensor.transpose(out=tq[:, m, :], in_=res[:, P * m:P * (m + 1)], identity=ident_f[:])
@@ -174,13 +203,15 @@ def tile_simplegcn_pa_t_kernel(tc, x, adjacency, w, b, out):
             xunits.append(xu)
 
         waiting = []
+        broadcast(0)
         for c in range(2):
-            scale(0, c, kept[0][c], ALLC)
+            scale(0, c, kept[0][c], True)
             waiting.append((0, c, quantise(kept[0][c], ALLC, PANEL)))
         cs2, kept[2] = load_panel(2)
         chain(2, cs2)
+        broadcast(1)
         for c in range(4):
-            scale(1, c, kept[1][c], ALLC)
+            scale(1, c, kept[1][c], True)
             waiting.append((1, c, quantise(kept[1][c], ALLC, PANEL)))
 
         xw_g = grp.tile([P, 4 * PANEL], BF16, tag="ag", align_bytes=64)
@@ -233,16 +264,17 @@ def tile_simplegcn_pa_t_kernel(tc, x, adjacency, w, b, out):
                     loaded[tail[q]] = load_unit(tail[q][0], tail[q][1])
             J, c = tail[idx]
             u = loaded[(J, c)]
+            if idx == 0 or tail[idx - 1][0] != J:
+                broadcast(J)
             if idx < len(tail) - 1:
-                scale(J, c, u, ALLC)
+                scale(J, c, u, True)
                 cd, sc = quantise(u, ALLC, PANEL)
                 for h in range(2):
                     multiply(J, c, h, cd, sc, 512 * h)
                     if seen[(J, h)] == NPASS:
                         finish(J, h)
             else:
-                for h in range(2):
-                    scale(J, c, u, slice(512 * h, 512 * (h + 1)))
+                scale(J, c, u, False)
                 for h in range(2):
                     cd, sc = quantise(u, slice(512 * h, 512 * (h + 1)), 512)
                     multiply(J, c, h, cd, sc, 0)

@@ -17,10 +17,10 @@ N = 4096
 D = 512
 F = 128
 PANEL = 1024
-NPAN = N // PANEL
-NPASS = N // 512
-UNIT_BUFS = 14
-COD_BUFS = 7
+BLK = 512
+NPASS = N // BLK
+UNIT_BUFS = 15
+COD_BUFS = 16
 LOOKAHEAD = 5
 TINY = 1e-30
 
@@ -36,9 +36,7 @@ def tile_simplegcn_pa_t_kernel(tc, x, adjacency, w, b, out):
         cod = ctx.enter_context(tc.tile_pool(name="cod", bufs=COD_BUFS))
         small = ctx.enter_context(tc.tile_pool(name="small", bufs=2))
         outp = ctx.enter_context(tc.tile_pool(name="outp", bufs=2))
-        gtmp = ctx.enter_context(tc.tile_pool(name="gtmp", bufs=2))
-        accp = ctx.enter_context(tc.psum_pool(name="accp", bufs=4))
-        vbp = ctx.enter_context(tc.psum_pool(name="vbp", bufs=2))
+        accp = ctx.enter_context(tc.psum_pool(name="accp", bufs=6))
         tpp = ctx.enter_context(tc.psum_pool(name="tpp", bufs=2))
 
         ident_f = const.tile([P, P], F32)
@@ -52,169 +50,151 @@ def tile_simplegcn_pa_t_kernel(tc, x, adjacency, w, b, out):
         warm2 = const.tile([P, 1], F32)
         nc.scalar.activation(out=warm2[:], in_=warm[:], func=ACT.Sqrt)
 
-        w_raw = const.tile([P, 4, F], BF16)
-        nc.sync.dma_start(
-            out=w_raw[:].rearrange("q (u e) f -> q u e f", u=2),
-            in_=w.rearrange("(u q e) f -> q u e f", u=2, e=2),
-        )
-        b_raw = const.tile([P, 1], BF16)
-        nc.sync.dma_start(out=b_raw[:], in_=b.rearrange("(p o) -> p o", o=1))
-        b_f = const.tile([P, 1], F32)
-        nc.vector.tensor_copy(out=b_f[:], in_=b_raw[:])
-
-        def load_unit(J, c):
-            u = units.tile([P, 4, PANEL], BF16, tag="unit", name="u%d_%d" % (J, c))
+        def load_unit(col0, width, c):
+            u = units.tile([P, 4, width], BF16, tag="unit", name="u%d_%d" % (col0, c))
             nc.sync.dma_start(
                 out=u[:],
-                in_=adjacency[512 * c:512 * (c + 1), PANEL * J:PANEL * (J + 1)].rearrange("(t p) w -> p t w", p=P),
+                in_=adjacency[BLK * c:BLK * (c + 1), col0:col0 + width].rearrange("(t p) w -> p t w", p=P),
             )
             return u
 
-        def load_panel(J):
-            cs = tpp.tile([P, 8, NPASS], F32, tag="tp", name="cs%d" % J)
+        def load_cols(col0, width, keep_below):
+            nb = width // P
+            cs = tpp.tile([P, nb, NPASS], F32, tag="tp", name="cs%d" % col0)
             keep = {}
             for c in range(NPASS):
-                u = load_unit(J, c)
-                if c // 2 == J:
-                    b0 = 4 * (c - 2 * J)
-                    blk = u[:].rearrange("p t (n k) -> p (t n) k", k=P)[:, b0:b0 + 28:9, :]
+                u = load_unit(col0, width, c)
+                b0 = (BLK * c - col0) // P
+                if 0 <= b0 and b0 + 3 < nb:
+                    blk = u[:].rearrange("p t (n k) -> p (t n) k", k=P)[:, b0:b0 + 3 * (nb + 1) + 1:nb + 1, :]
                     nc.vector.tensor_tensor(out=blk, in0=blk, in1=ident_b[:].unsqueeze(1).to_broadcast([P, 4, P]), op=ALU.add)
-                for m in range(8):
+                for m in range(nb):
                     for t in range(4):
                         nc.tensor.matmul(out=cs[:, m, c:c + 1], lhsT=u[:, t, P * m:P * (m + 1)], rhs=ones[:, 0:1],
                                          start=(t == 0), stop=(t == 3))
-                if c < 2 * J + 2:
+                if c < keep_below:
                     keep[c] = u
             return cs, keep
 
         dinv = {}
         vb = {}
+        for J in range(4):
+            dinv[J] = const.tile([P, 8], F32, name="dinv%d" % J)
+            vb[J] = const.tile([P, PANEL], F32, name="vb%d" % J)
 
-        def chain(J, cs):
-            deg = small.tile([P, 8], F32, tag="deg")
+        def chain(J, m0, nm, cs):
+            deg = small.tile([P, nm], F32, tag="deg")
             nc.vector.tensor_reduce(out=deg[:], in_=cs[:], axis=AX.X, op=ALU.add)
-            dcl = small.tile([P, 8], F32, tag="dcl")
+            dcl = small.tile([P, nm], F32, tag="dcl")
             nc.vector.tensor_scalar_max(out=dcl[:], in0=deg[:], scalar1=TINY)
-            sq = small.tile([P, 8], F32, tag="sq")
+            sq = small.tile([P, nm], F32, tag="sq")
             nc.scalar.activation(out=sq[:], in_=dcl[:], func=ACT.Sqrt)
-            rc = small.tile([P, 8], F32, tag="rc")
+            rc = small.tile([P, nm], F32, tag="rc")
             nc.vector.reciprocal(out=rc[:], in_=sq[:])
-            dv = const.tile([P, 8], F32, name="dinv%d" % J)
-            nc.vector.scalar_tensor_tensor(out=dv[:], in0=deg[:], scalar=0.0, in1=rc[:], op0=ALU.is_gt, op1=ALU.mult)
-            vbt = const.tile([P, PANEL], F32, name="vb%d" % J)
-            for h in range(2):
-                vps = tpp.tile([P, 512], F32, tag="tp", name="vps%d_%d" % (J, h))
+            nc.vector.scalar_tensor_tensor(out=dinv[J][:, m0:m0 + nm], in0=deg[:], scalar=0.0, in1=rc[:], op0=ALU.is_gt, op1=ALU.mult)
+            for h in range(nm // 4):
+                vps = tpp.tile([P, BLK], F32, tag="tp", name="vps%d_%d" % (J, m0 + 4 * h))
                 for m in range(4):
-                    k = 4 * h + m
-                    nc.tensor.transpose(out=vps[:, P * m:P * (m + 1)], in_=dv[:, k:k + 1].to_broadcast([P, P]), identity=ident_f[:])
+                    k = m0 + 4 * h + m
+                    nc.tensor.transpose(out=vps[:, P * m:P * (m + 1)], in_=dinv[J][:, k:k + 1].to_broadcast([P, P]), identity=ident_f[:])
+                dst = vb[J][:, P * (m0 + 4 * h):P * (m0 + 4 * h) + BLK]
                 if h == 0:
-                    nc.vector.tensor_copy(out=vbt[:, 0:512], in_=vps[:])
+                    nc.vector.tensor_copy(out=dst, in_=vps[:])
                 else:
-                    nc.scalar.copy(out=vbt[:, 512:1024], in_=vps[:])
-            dinv[J] = dv
-            vb[J] = vbt
+                    nc.scalar.copy(out=dst, in_=vps[:])
 
         xw_c = const.tile([P, NPASS * F], U32, align_bytes=64)
         xw_s = const.tile([P, NPASS * F], U8, align_bytes=64)
 
-        vbk = {}
-
-        def broadcast(J):
-            for h in range(2):
-                bank = vbp.tile([P, 512], F32, tag="vbk", name="vbk%d_%d" % (J, h))
-                for m in range(4):
-                    k = 4 * h + m
-                    nc.tensor.transpose(out=bank[:, P * m:P * (m + 1)], in_=dinv[J][:, k:k + 1].to_broadcast([P, P]), identity=ident_f[:])
-                vbk[h] = bank
-
-        def scale(J, c, u, use_g):
+        def scale(u, col0, width, c, step):
+            J = col0 // PANEL
             dv = dinv[c // 2]
-            rows = 4
-            if use_g:
-                rows = 3
-                k3 = (4 * c + 3) % 8
-                gx = gtmp.tile([P, PANEL], F32, tag="gx")
-                nc.vector.tensor_scalar_mul(out=gx[:], in0=u[:, 3, :], scalar1=dv[:, k3:k3 + 1])
-                nc.gpsimd.tensor_tensor(out=u[:, 3, :], in0=gx[:], in1=vb[J][:], op=ALU.mult)
-            for h in range(2):
-                cols = slice(512 * h, 512 * (h + 1))
-                for t in range(rows):
+            for s0 in range(0, width, step):
+                v0 = col0 - PANEL * J + s0
+                for t in range(4):
                     k = (4 * c + t) % 8
-                    nc.vector.scalar_tensor_tensor(out=u[:, t, cols], in0=u[:, t, cols], scalar=dv[:, k:k + 1], in1=vbk[h][:],
-                                                   op0=ALU.mult, op1=ALU.mult)
+                    nc.vector.scalar_tensor_tensor(out=u[:, t, s0:s0 + step], in0=u[:, t, s0:s0 + step], scalar=dv[:, k:k + 1],
+                                                   in1=vb[J][:, v0:v0 + step], op0=ALU.mult, op1=ALU.mult)
 
-        def quantise(u, cols, width):
-            ag = grp.tile([P, 4 * width], BF16, tag="ag", align_bytes=64)
-            nc.scalar.copy(out=ag[:].rearrange("p (n i t) -> p n t i", i=4, t=4),
-                           in_=u[:, :, cols].rearrange("p t (n i) -> p n t i", i=4))
-            cd = cod.tile([P, width], U32, tag="cd", align_bytes=64)
-            sc = cod.tile([P, width], U8, tag="sc", align_bytes=64)
-            nc.vector.quantize_mx(out=cd[:].bitcast(FP8X4), scales=sc[:], in_=ag[:])
-            return cd, sc
+        def quantise(u, width, step):
+            pairs = []
+            for s0 in range(0, width, step):
+                ag = grp.tile([P, 4 * step], BF16, tag="ag", align_bytes=64)
+                nc.scalar.copy(out=ag[:].rearrange("p (n i t) -> p n t i", i=4, t=4),
+                               in_=u[:, :, s0:s0 + step].rearrange("p t (n i) -> p n t i", i=4))
+                for q0 in range(0, step, BLK):
+                    cd = cod.tile([P, BLK], U32, tag="cd", align_bytes=64)
+                    sc = cod.tile([P, BLK], U8, tag="sc", align_bytes=64)
+                    nc.vector.quantize_mx(out=cd[:].bitcast(FP8X4), scales=sc[:], in_=ag[:, 4 * q0:4 * (q0 + BLK)])
+                    pairs.append((cd, sc))
+            return pairs
 
         acc = {}
         seen = {}
-        part0 = const.tile([P, PANEL], F32)
 
-        def multiply(J, c, h, cd, sc, off):
-            if acc.get((J, h)) is None:
-                acc[(J, h)] = accp.tile([P, 512], F32, tag="acc", name="acc%d_%d" % (J, h))
-            seen[(J, h)] = seen.get((J, h), 0) + 1
-            n = seen[(J, h)]
-            nc.tensor.matmul_mx(out=acc[(J, h)][:], lhsT=xw_c[:, F * c:F * (c + 1)].bitcast(FP8X4),
-                                lhsT_scale=xw_s[:, F * c:F * (c + 1)],
-                                rhs=cd[:, off:off + 512].bitcast(FP8X4), rhs_scale=sc[:, off:off + 512],
-                                start=(n == 1 or (J == 0 and n == 3)), stop=(n == NPASS or (J == 0 and n == 2)))
-            if J == 0 and n == 2:
-                nc.scalar.copy(out=part0[:, 512 * h:512 * (h + 1)], in_=acc[(J, h)][:])
-                acc[(J, h)] = None
-
-        def finish(J, h):
-            res = outp.tile([P, 512], F32, tag="res")
-            if J == 0:
-                nc.vector.tensor_tensor(out=res[:], in0=acc[(J, h)][:], in1=part0[:, 512 * h:512 * (h + 1)], op=ALU.add)
-                nc.scalar.activation(out=res[:], in_=res[:], func=ACT.Relu, bias=b_f[:, 0:1], scale=1.0)
-            else:
-                nc.scalar.activation(out=res[:], in_=acc[(J, h)][:], func=ACT.Relu, bias=b_f[:, 0:1], scale=1.0)
+        def finish(B):
+            res = outp.tile([P, BLK], F32, tag="res")
+            nc.scalar.activation(out=res[:], in_=acc[B][:], func=ACT.Relu, bias=b_f[:, 0:1], scale=1.0)
             tq = tpp.tile([P, 4, F], F32, tag="tp")
             for m in range(4):
                 nc.tensor.transpose(out=tq[:, m, :], in_=res[:, P * m:P * (m + 1)], identity=ident_f[:])
             ot = outp.tile([P, 4, F], F32, tag="ot")
             nc.scalar.copy(out=ot[:], in_=tq[:])
-            r0 = PANEL * J + 512 * h
-            nc.sync.dma_start(out=out[r0:r0 + 512, :].rearrange("(m p) f -> p m f", p=P), in_=ot[:])
+            nc.sync.dma_start(out=out[BLK * B:BLK * (B + 1), :].rearrange("(m p) f -> p m f", p=P), in_=ot[:])
 
-        ALLC = slice(0, PANEL)
+        def multiply(B, c, pair):
+            if B not in acc:
+                acc[B] = accp.tile([P, BLK], F32, tag="acc", name="acc%d" % B)
+                seen[B] = 0
+            seen[B] += 1
+            nc.tensor.matmul_mx(out=acc[B][:], lhsT=xw_c[:, F * c:F * (c + 1)].bitcast(FP8X4),
+                                lhsT_scale=xw_s[:, F * c:F * (c + 1)],
+                                rhs=pair[0][:].bitcast(FP8X4), rhs_scale=pair[1][:],
+                                start=(seen[B] == 1), stop=(seen[B] == NPASS))
+            if seen[B] == NPASS:
+                finish(B)
 
-        kept = {}
-        cs0, kept[0] = load_panel(0)
-        w_g = const.tile([P, F, 4], BF16, align_bytes=64)
-        nc.vector.tensor_copy(out=w_g[:], in_=w_raw[:].rearrange("q t f -> q f t"))
-        w_c = const.tile([P, F], U32, align_bytes=64)
-        w_s = const.tile([P, F], U8, align_bytes=64)
-        nc.vector.quantize_mx(out=w_c[:].bitcast(FP8X4), scales=w_s[:], in_=w_g[:].rearrange("q f t -> q (f t)"))
-        chain(0, cs0)
-        cs1, kept[1] = load_panel(1)
-        chain(1, cs1)
+        def work(u, col0, width, c, fine):
+            step = BLK if fine else width
+            scale(u, col0, width, c, step)
+            pairs = quantise(u, width, step)
+            return [(col0 // BLK + n, c, pairs[n]) for n in range(len(pairs))]
+
+        cs0, keep0 = load_cols(0, PANEL, 4)
+        chain(0, 0, 8, cs0)
+        cs1a, keep1a = load_cols(PANEL, BLK, 4)
+        chain(1, 0, 4, cs1a)
+        cs1b, keep1b = load_cols(PANEL + BLK, BLK, 4)
+        chain(1, 4, 4, cs1b)
+
+        w_raw = const.tile([P, 4, F], BF16)
+        nc.sync.dma_start(
+            out=w_raw[:].rearrange("q (u e) f -> q u e f", u=2),
+            in_=w.rearrange("(u q e) f -> q u e f", u=2, e=2),
+        )
         xunits = []
         for g in range(4):
             xu = units.tile([P, 8, D], BF16, tag="unit", name="xu%d" % g)
             nc.sync.dma_start(out=xu[:], in_=x[1024 * g:1024 * (g + 1), :].rearrange("(r p) d -> p r d", p=P))
             xunits.append(xu)
+        b_raw = const.tile([P, 1], BF16)
+        nc.sync.dma_start(out=b_raw[:], in_=b.rearrange("(p o) -> p o", o=1))
+        b_f = const.tile([P, 1], F32)
+        nc.vector.tensor_copy(out=b_f[:], in_=b_raw[:])
 
         waiting = []
-        broadcast(0)
         for c in range(2):
-            scale(0, c, kept[0][c], True)
-            waiting.append((0, c, quantise(kept[0][c], ALLC, PANEL)))
-        cs2, kept[2] = load_panel(2)
-        chain(2, cs2)
-        broadcast(1)
-        for c in range(4):
-            scale(1, c, kept[1][c], True)
-            waiting.append((1, c, quantise(kept[1][c], ALLC, PANEL)))
+            waiting.extend(work(keep0[c], 0, PANEL, c, False))
 
-        xw_g = grp.tile([P, 4 * PANEL], BF16, tag="ag", align_bytes=64)
+        cs2, keep2 = load_cols(2 * PANEL, PANEL, 6)
+        chain(2, 0, 8, cs2)
+
+        w_g = const.tile([P, F, 4], BF16, align_bytes=64)
+        nc.vector.tensor_copy(out=w_g[:], in_=w_raw[:].rearrange("q t f -> q f t"))
+        w_c = const.tile([P, F], U32, align_bytes=64)
+        w_s = const.tile([P, F], U8, align_bytes=64)
+        nc.vector.quantize_mx(out=w_c[:].bitcast(FP8X4), scales=w_s[:], in_=w_g[:].rearrange("q f t -> q (f t)"))
+        xw_g = const.tile([P, 4 * PANEL], BF16, align_bytes=64)
         xw_gv = xw_g[:].rearrange("p (c f t) -> p c f t", c=NPASS, t=4)
         for g in range(4):
             xu = xunits[g]
@@ -227,16 +207,15 @@ def tile_simplegcn_pa_t_kernel(tc, x, adjacency, w, b, out):
                     for u2 in range(2):
                         nc.tensor.transpose(out=tp[:, r2, u2, :], in_=xr[:, P * u2:P * (u2 + 1)], identity=ident_f[:])
                 nc.scalar.copy(out=xg32[:, 2 * k:2 * k + 2], in_=tp[:].rearrange("p r u i -> p r i u"))
-            xc = cod.tile([P, PANEL], U32, tag="cd", align_bytes=64)
-            xs = cod.tile([P, PANEL], U8, tag="sc", align_bytes=64)
-            nc.vector.quantize_mx(out=xc[:].bitcast(FP8X4), scales=xs[:], in_=xg[:])
             for cc in range(2):
                 c = 2 * g + cc
+                xc = cod.tile([P, BLK], U32, tag="cd", align_bytes=64)
+                xs = cod.tile([P, BLK], U8, tag="sc", align_bytes=64)
+                nc.vector.quantize_mx(out=xc[:].bitcast(FP8X4), scales=xs[:], in_=xg[:, 2048 * cc:2048 * (cc + 1)])
                 xwp = accp.tile([P, 4, F], F32, tag="acc", name="xwp%d" % c)
                 for t in range(4):
-                    r = 4 * cc + t
-                    nc.tensor.matmul_mx(out=xwp[:, t, :], lhsT=xc[:, P * r:P * (r + 1)].bitcast(FP8X4),
-                                        lhsT_scale=xs[:, P * r:P * (r + 1)], rhs=w_c[:].bitcast(FP8X4), rhs_scale=w_s[:],
+                    nc.tensor.matmul_mx(out=xwp[:, t, :], lhsT=xc[:, P * t:P * (t + 1)].bitcast(FP8X4),
+                                        lhsT_scale=xs[:, P * t:P * (t + 1)], rhs=w_c[:].bitcast(FP8X4), rhs_scale=w_s[:],
                                         start=True, stop=True)
                 nc.scalar.copy(out=xw_gv[:, c], in_=xwp[:].rearrange("p t f -> p f t"))
             if g % 2 == 1:
@@ -244,38 +223,35 @@ def tile_simplegcn_pa_t_kernel(tc, x, adjacency, w, b, out):
                 nc.vector.quantize_mx(out=xw_c[:, 512 * hh:512 * (hh + 1)].bitcast(FP8X4), scales=xw_s[:, 512 * hh:512 * (hh + 1)],
                                       in_=xw_g[:, 2048 * hh:2048 * (hh + 1)])
 
-        for J, c, pair in waiting:
-            for h in range(2):
-                multiply(J, c, h, pair[0], pair[1], 512 * h)
+        def run(u, col0, width, c, fine):
+            for B, cc, pair in work(u, col0, width, c, fine):
+                multiply(B, cc, pair)
 
-        cs3, kept[3] = load_panel(3)
-        chain(3, cs3)
+        for B, c, pair in waiting:
+            multiply(B, c, pair)
+
+        for c in range(3):
+            run(keep1a[c], PANEL, BLK, c, False)
+        run(keep0[2], 0, PANEL, 2, False)
+        for c in range(4):
+            run(keep1b[c], PANEL + BLK, BLK, c, False)
+        run(keep1a[3], PANEL, BLK, 3, False)
+        run(keep0[3], 0, PANEL, 3, False)
+
+        cs3, keep3 = load_cols(3 * PANEL, PANEL, NPASS)
+        chain(3, 0, 8, cs3)
 
         tail = [(2, c) for c in range(NPASS)] + [(3, c) for c in range(NPASS)]
         for J in (1, 0):
-            tail.extend([(J, c) for c in range(2 * J + 2, NPASS)])
+            tail.extend([(J, c) for c in range(4, NPASS)])
         loaded = {}
-        for J in (2, 3):
-            for c in kept[J]:
-                loaded[(J, c)] = kept[J][c]
+        for c in keep2:
+            loaded[(2, c)] = keep2[c]
+        for c in keep3:
+            loaded[(3, c)] = keep3[c]
         for idx in range(len(tail)):
             for q in range(idx, min(idx + LOOKAHEAD + 1, len(tail))):
                 if tail[q] not in loaded:
-                    loaded[tail[q]] = load_unit(tail[q][0], tail[q][1])
+                    loaded[tail[q]] = load_unit(PANEL * tail[q][0], PANEL, tail[q][1])
             J, c = tail[idx]
-            u = loaded[(J, c)]
-            if idx == 0 or tail[idx - 1][0] != J:
-                broadcast(J)
-            if idx < len(tail) - 1:
-                scale(J, c, u, True)
-                cd, sc = quantise(u, ALLC, PANEL)
-                for h in range(2):
-                    multiply(J, c, h, cd, sc, 512 * h)
-                    if seen[(J, h)] == NPASS:
-                        finish(J, h)
-            else:
-                scale(J, c, u, False)
-                for h in range(2):
-                    cd, sc = quantise(u, slice(512 * h, 512 * (h + 1)), 512)
-                    multiply(J, c, h, cd, sc, 0)
-                    finish(J, h)
+            run(loaded[(J, c)], PANEL * J, PANEL, c, idx == len(tail) - 1)

@@ -22,6 +22,8 @@ NPASS = N // BLK
 UNIT_BUFS = 15
 COD_BUFS = 16
 LOOKAHEAD = 5
+R_OF = 3
+R_TAKE = 2
 TINY = 1e-30
 
 FLOPS = 2 * N * D * F + 2 * N * N * F
@@ -36,6 +38,7 @@ def tile_simplegcn_pa_t_kernel(tc, x, adjacency, w, b, out):
         cod = ctx.enter_context(tc.tile_pool(name="cod", bufs=COD_BUFS))
         small = ctx.enter_context(tc.tile_pool(name="small", bufs=2))
         outp = ctx.enter_context(tc.tile_pool(name="outp", bufs=2))
+        rowp = ctx.enter_context(tc.tile_pool(name="rowp", bufs=2))
         accp = ctx.enter_context(tc.psum_pool(name="accp", bufs=6))
         tpp = ctx.enter_context(tc.psum_pool(name="tpp", bufs=2))
 
@@ -82,7 +85,7 @@ def tile_simplegcn_pa_t_kernel(tc, x, adjacency, w, b, out):
             dinv[J] = const.tile([P, 8], F32, name="dinv%d" % J)
             vb[J] = const.tile([P, PANEL], F32, name="vb%d" % J)
 
-        def chain(J, m0, nm, cs):
+        def chain(J, m0, nm, cs, urgent):
             deg = small.tile([P, nm], F32, tag="deg")
             nc.vector.tensor_reduce(out=deg[:], in_=cs[:], axis=AX.X, op=ALU.add)
             dcl = small.tile([P, nm], F32, tag="dcl")
@@ -98,20 +101,30 @@ def tile_simplegcn_pa_t_kernel(tc, x, adjacency, w, b, out):
                     k = m0 + 4 * h + m
                     nc.tensor.transpose(out=vps[:, P * m:P * (m + 1)], in_=dinv[J][:, k:k + 1].to_broadcast([P, P]), identity=ident_f[:])
                 dst = vb[J][:, P * (m0 + 4 * h):P * (m0 + 4 * h) + BLK]
-                if h == 0:
+                if h == 0 and urgent:
                     nc.vector.tensor_copy(out=dst, in_=vps[:])
                 else:
                     nc.scalar.copy(out=dst, in_=vps[:])
 
+        count = [0]
         xw_c = const.tile([P, NPASS * F], U32, align_bytes=64)
         xw_s = const.tile([P, NPASS * F], U8, align_bytes=64)
 
         def scale(u, col0, width, c, step):
             J = col0 // PANEL
             dv = dinv[c // 2]
+            rows = 4
+            if step == PANEL:
+                count[0] += 1
+                if count[0] % R_OF < R_TAKE:
+                    rows = 3
+                    k3 = (4 * c + 3) % 8
+                    rr = rowp.tile([P, PANEL], BF16, tag="rr")
+                    nc.scalar.activation(out=rr[:], in_=vb[J][:], func=ACT.Copy, scale=dv[:, k3:k3 + 1])
+                    nc.vector.tensor_tensor(out=u[:, 3, :], in0=u[:, 3, :], in1=rr[:], op=ALU.mult)
             for s0 in range(0, width, step):
                 v0 = col0 - PANEL * J + s0
-                for t in range(4):
+                for t in range(rows):
                     k = (4 * c + t) % 8
                     nc.vector.scalar_tensor_tensor(out=u[:, t, s0:s0 + step], in0=u[:, t, s0:s0 + step], scalar=dv[:, k:k + 1],
                                                    in1=vb[J][:, v0:v0 + step], op0=ALU.mult, op1=ALU.mult)
@@ -120,8 +133,12 @@ def tile_simplegcn_pa_t_kernel(tc, x, adjacency, w, b, out):
             pairs = []
             for s0 in range(0, width, step):
                 ag = grp.tile([P, 4 * step], BF16, tag="ag", align_bytes=64)
-                nc.scalar.copy(out=ag[:].rearrange("p (n i t) -> p n t i", i=4, t=4),
-                               in_=u[:, :, s0:s0 + step].rearrange("p t (n i) -> p n t i", i=4))
+                if step < width and s0 + step == width:
+                    nc.vector.tensor_copy(out=ag[:].rearrange("p (n i t) -> p n t i", i=4, t=4),
+                                          in_=u[:, :, s0:s0 + step].rearrange("p t (n i) -> p n t i", i=4))
+                else:
+                    nc.scalar.copy(out=ag[:].rearrange("p (n i t) -> p n t i", i=4, t=4),
+                                   in_=u[:, :, s0:s0 + step].rearrange("p t (n i) -> p n t i", i=4))
                 for q0 in range(0, step, BLK):
                     cd = cod.tile([P, BLK], U32, tag="cd", align_bytes=64)
                     sc = cod.tile([P, BLK], U8, tag="sc", align_bytes=64)
@@ -161,11 +178,9 @@ def tile_simplegcn_pa_t_kernel(tc, x, adjacency, w, b, out):
             return [(col0 // BLK + n, c, pairs[n]) for n in range(len(pairs))]
 
         cs0, keep0 = load_cols(0, PANEL, 4)
-        chain(0, 0, 8, cs0)
+        chain(0, 0, 8, cs0, True)
         cs1a, keep1a = load_cols(PANEL, BLK, 4)
-        chain(1, 0, 4, cs1a)
-        cs1b, keep1b = load_cols(PANEL + BLK, BLK, 4)
-        chain(1, 4, 4, cs1b)
+        chain(1, 0, 4, cs1a, True)
 
         w_raw = const.tile([P, 4, F], BF16)
         nc.sync.dma_start(
@@ -181,13 +196,15 @@ def tile_simplegcn_pa_t_kernel(tc, x, adjacency, w, b, out):
         nc.sync.dma_start(out=b_raw[:], in_=b.rearrange("(p o) -> p o", o=1))
         b_f = const.tile([P, 1], F32)
         nc.vector.tensor_copy(out=b_f[:], in_=b_raw[:])
+        cs1b, keep1b = load_cols(PANEL + BLK, BLK, 4)
+        chain(1, 4, 4, cs1b, False)
 
         waiting = []
         for c in range(2):
             waiting.extend(work(keep0[c], 0, PANEL, c, False))
 
         cs2, keep2 = load_cols(2 * PANEL, PANEL, 6)
-        chain(2, 0, 8, cs2)
+        chain(2, 0, 8, cs2, False)
 
         w_g = const.tile([P, F, 4], BF16, align_bytes=64)
         nc.vector.tensor_copy(out=w_g[:], in_=w_raw[:].rearrange("q t f -> q f t"))
@@ -239,7 +256,7 @@ def tile_simplegcn_pa_t_kernel(tc, x, adjacency, w, b, out):
         run(keep0[3], 0, PANEL, 3, False)
 
         cs3, keep3 = load_cols(3 * PANEL, PANEL, NPASS)
-        chain(3, 0, 8, cs3)
+        chain(3, 0, 8, cs3, False)
 
         tail = [(2, c) for c in range(NPASS)] + [(3, c) for c in range(NPASS)]
         for J in (1, 0):

@@ -22,8 +22,8 @@ NPASS = N // BLK
 UNIT_BUFS = 15
 COD_BUFS = 16
 LOOKAHEAD = 5
-R_OF = 3
-R_TAKE = 2
+R_OF = 2
+R_TAKE = 1
 TINY = 1e-30
 
 FLOPS = 2 * N * D * F + 2 * N * N * F
@@ -192,10 +192,6 @@ def tile_simplegcn_pa_t_kernel(tc, x, adjacency, w, b, out):
             xu = units.tile([P, 8, D], BF16, tag="unit", name="xu%d" % g)
             nc.sync.dma_start(out=xu[:], in_=x[1024 * g:1024 * (g + 1), :].rearrange("(r p) d -> p r d", p=P))
             xunits.append(xu)
-        b_raw = const.tile([P, 1], BF16)
-        nc.sync.dma_start(out=b_raw[:], in_=b.rearrange("(p o) -> p o", o=1))
-        b_f = const.tile([P, 1], F32)
-        nc.vector.tensor_copy(out=b_f[:], in_=b_raw[:])
         cs1b, keep1b = load_cols(PANEL + BLK, BLK, 4)
         chain(1, 4, 4, cs1b, False)
 
@@ -257,6 +253,10 @@ def tile_simplegcn_pa_t_kernel(tc, x, adjacency, w, b, out):
 
         cs3, keep3 = load_cols(3 * PANEL, PANEL, NPASS)
         chain(3, 0, 8, cs3, False)
+        b_raw = const.tile([P, 1], BF16)
+        nc.sync.dma_start(out=b_raw[:], in_=b.rearrange("(p o) -> p o", o=1))
+        b_f = const.tile([P, 1], F32)
+        nc.vector.tensor_copy(out=b_f[:], in_=b_raw[:])
 
         tail = [(2, c) for c in range(NPASS)] + [(3, c) for c in range(NPASS)]
         for J in (1, 0):

@@ -18,12 +18,10 @@ D = 512
 F = 128
 PANEL = 1024
 BLK = 512
-NPASS = N // BLK
-UNIT_BUFS = 15
-COD_BUFS = 16
-LOOKAHEAD = 5
-R_OF = 2
-R_TAKE = 1
+NBLK = N // BLK
+UNIT_BUFS = 16
+COD_BUFS = 8
+V_COPY = 4
 TINY = 1e-30
 
 FLOPS = 2 * N * D * F + 2 * N * N * F
@@ -34,13 +32,16 @@ def tile_simplegcn_pa_t_kernel(tc, x, adjacency, w, b, out):
     with ExitStack() as ctx:
         const = ctx.enter_context(tc.tile_pool(name="const", bufs=1))
         units = ctx.enter_context(tc.tile_pool(name="units", bufs=UNIT_BUFS))
-        grp = ctx.enter_context(tc.tile_pool(name="grp", bufs=3))
+        grp = ctx.enter_context(tc.tile_pool(name="grp", bufs=4))
+        rpool = ctx.enter_context(tc.tile_pool(name="rpool", bufs=2))
+        tpool = ctx.enter_context(tc.tile_pool(name="tpool", bufs=3))
         cod = ctx.enter_context(tc.tile_pool(name="cod", bufs=COD_BUFS))
         small = ctx.enter_context(tc.tile_pool(name="small", bufs=2))
         outp = ctx.enter_context(tc.tile_pool(name="outp", bufs=2))
-        rowp = ctx.enter_context(tc.tile_pool(name="rowp", bufs=2))
-        accp = ctx.enter_context(tc.psum_pool(name="accp", bufs=6))
-        tpp = ctx.enter_context(tc.psum_pool(name="tpp", bufs=2))
+        t1p = ctx.enter_context(tc.psum_pool(name="t1p", bufs=2))
+        t2p = ctx.enter_context(tc.psum_pool(name="t2p", bufs=2))
+        csp = ctx.enter_context(tc.psum_pool(name="csp", bufs=1))
+        accp = ctx.enter_context(tc.psum_pool(name="accp", bufs=3))
 
         ident_f = const.tile([P, P], F32)
         make_identity(nc, ident_f[:])
@@ -53,39 +54,45 @@ def tile_simplegcn_pa_t_kernel(tc, x, adjacency, w, b, out):
         warm2 = const.tile([P, 1], F32)
         nc.scalar.activation(out=warm2[:], in_=warm[:], func=ACT.Sqrt)
 
-        def load_unit(col0, width, c):
-            u = units.tile([P, 4, width], BF16, tag="unit", name="u%d_%d" % (col0, c))
-            nc.sync.dma_start(
-                out=u[:],
-                in_=adjacency[BLK * c:BLK * (c + 1), col0:col0 + width].rearrange("(t p) w -> p t w", p=P),
-            )
+        vb = const.tile([P, N], F32)
+        dinv = const.tile([P, 4 * NBLK], F32)
+        xw_c = const.tile([P, NBLK * F], U32, align_bytes=64)
+        xw_s = const.tile([P, NBLK * F], U8, align_bytes=64)
+
+        unit = {}
+
+        def load(J, c, w0, width, again=False):
+            if again or (J, c) not in unit:
+                unit[(J, c)] = units.tile([P, 4, PANEL], BF16, tag="unit", name="u%d_%d_%d" % (J, c, int(again)))
+            u = unit[(J, c)]
+            src = adjacency[BLK * c:BLK * (c + 1), PANEL * J + w0:PANEL * J + w0 + width]
+            if c < 2 * J:
+                for h in range(2):
+                    nc.sync.dma_start(out=u[:, 2 * h:2 * h + 2, w0:w0 + width],
+                                      in_=src[256 * h:256 * (h + 1), :].rearrange("(p e) w -> p e w", e=2))
+            else:
+                nc.sync.dma_start(out=u[:, :, w0:w0 + width], in_=src.rearrange("(t p) w -> p t w", p=P))
             return u
 
-        def load_cols(col0, width, keep_below):
-            nb = width // P
-            cs = tpp.tile([P, nb, NPASS], F32, tag="tp", name="cs%d" % col0)
-            keep = {}
-            for c in range(NPASS):
-                u = load_unit(col0, width, c)
-                b0 = (BLK * c - col0) // P
-                if 0 <= b0 and b0 + 3 < nb:
-                    blk = u[:].rearrange("p t (n k) -> p (t n) k", k=P)[:, b0:b0 + 3 * (nb + 1) + 1:nb + 1, :]
-                    nc.vector.tensor_tensor(out=blk, in0=blk, in1=ident_b[:].unsqueeze(1).to_broadcast([P, 4, P]), op=ALU.add)
-                for m in range(nb):
+        def degrees(J, w0, width, pause=(None, None)):
+            nb = width // BLK
+            b0 = (PANEL * J + w0) // BLK
+            cs = csp.tile([P, 4 * nb, NBLK], F32, tag="cs", name="cs%d" % b0)
+            for c in range(NBLK):
+                if c == pause[0]:
+                    pause[1]()
+                u = load(J, c, w0, width)
+                if b0 <= c < b0 + nb:
                     for t in range(4):
-                        nc.tensor.matmul(out=cs[:, m, c:c + 1], lhsT=u[:, t, P * m:P * (m + 1)], rhs=ones[:, 0:1],
+                        d0 = BLK * c - PANEL * J + P * t
+                        nc.vector.tensor_tensor(out=u[:, t, d0:d0 + P], in0=u[:, t, d0:d0 + P], in1=ident_b[:], op=ALU.add)
+                for m in range(4 * nb):
+                    s = w0 + 256 * (m // 2)
+                    for t in range(4):
+                        nc.tensor.matmul(out=cs[:, m, c:c + 1], lhsT=u[:, t, s + m % 2:s + 256:2], rhs=ones[:, 0:1],
                                          start=(t == 0), stop=(t == 3))
-                if c < keep_below:
-                    keep[c] = u
-            return cs, keep
-
-        dinv = {}
-        vb = {}
-        for J in range(4):
-            dinv[J] = const.tile([P, 8], F32, name="dinv%d" % J)
-            vb[J] = const.tile([P, PANEL], F32, name="vb%d" % J)
-
-        def chain(J, m0, nm, cs, urgent):
+            nm = 4 * nb
+            k0 = 4 * b0
             deg = small.tile([P, nm], F32, tag="deg")
             nc.vector.tensor_reduce(out=deg[:], in_=cs[:], axis=AX.X, op=ALU.add)
             dcl = small.tile([P, nm], F32, tag="dcl")
@@ -94,181 +101,212 @@ def tile_simplegcn_pa_t_kernel(tc, x, adjacency, w, b, out):
             nc.scalar.activation(out=sq[:], in_=dcl[:], func=ACT.Sqrt)
             rc = small.tile([P, nm], F32, tag="rc")
             nc.vector.reciprocal(out=rc[:], in_=sq[:])
-            nc.vector.scalar_tensor_tensor(out=dinv[J][:, m0:m0 + nm], in0=deg[:], scalar=0.0, in1=rc[:], op0=ALU.is_gt, op1=ALU.mult)
-            for h in range(nm // 4):
-                vps = tpp.tile([P, BLK], F32, tag="tp", name="vps%d_%d" % (J, m0 + 4 * h))
+            nc.vector.scalar_tensor_tensor(out=dinv[:, k0:k0 + nm], in0=deg[:], scalar=0.0, in1=rc[:], op0=ALU.is_gt, op1=ALU.mult)
+            for n in range(nb):
+                vps = t2p.tile([P, 4, P], F32, tag="t2", name="vps%d" % (b0 + n))
                 for m in range(4):
-                    k = m0 + 4 * h + m
-                    nc.tensor.transpose(out=vps[:, P * m:P * (m + 1)], in_=dinv[J][:, k:k + 1].to_broadcast([P, P]), identity=ident_f[:])
-                dst = vb[J][:, P * (m0 + 4 * h):P * (m0 + 4 * h) + BLK]
-                if h == 0 and urgent:
-                    nc.vector.tensor_copy(out=dst, in_=vps[:])
-                else:
-                    nc.scalar.copy(out=dst, in_=vps[:])
-
-        count = [0]
-        xw_c = const.tile([P, NPASS * F], U32, align_bytes=64)
-        xw_s = const.tile([P, NPASS * F], U8, align_bytes=64)
-
-        def scale(u, col0, width, c, step):
-            J = col0 // PANEL
-            dv = dinv[c // 2]
-            rows = 4
-            if step == PANEL:
-                count[0] += 1
-                if count[0] % R_OF < R_TAKE:
-                    rows = 3
-                    k3 = (4 * c + 3) % 8
-                    rr = rowp.tile([P, PANEL], BF16, tag="rr")
-                    nc.scalar.activation(out=rr[:], in_=vb[J][:], func=ACT.Copy, scale=dv[:, k3:k3 + 1])
-                    nc.vector.tensor_tensor(out=u[:, 3, :], in0=u[:, 3, :], in1=rr[:], op=ALU.mult)
-            for s0 in range(0, width, step):
-                v0 = col0 - PANEL * J + s0
-                for t in range(rows):
-                    k = (4 * c + t) % 8
-                    nc.vector.scalar_tensor_tensor(out=u[:, t, s0:s0 + step], in0=u[:, t, s0:s0 + step], scalar=dv[:, k:k + 1],
-                                                   in1=vb[J][:, v0:v0 + step], op0=ALU.mult, op1=ALU.mult)
-
-        def quantise(u, width, step):
-            pairs = []
-            for s0 in range(0, width, step):
-                ag = grp.tile([P, 4 * step], BF16, tag="ag", align_bytes=64)
-                if step < width and s0 + step == width:
-                    nc.vector.tensor_copy(out=ag[:].rearrange("p (n i t) -> p n t i", i=4, t=4),
-                                          in_=u[:, :, s0:s0 + step].rearrange("p t (n i) -> p n t i", i=4))
-                else:
-                    nc.scalar.copy(out=ag[:].rearrange("p (n i t) -> p n t i", i=4, t=4),
-                                   in_=u[:, :, s0:s0 + step].rearrange("p t (n i) -> p n t i", i=4))
-                for q0 in range(0, step, BLK):
-                    cd = cod.tile([P, BLK], U32, tag="cd", align_bytes=64)
-                    sc = cod.tile([P, BLK], U8, tag="sc", align_bytes=64)
-                    nc.vector.quantize_mx(out=cd[:].bitcast(FP8X4), scales=sc[:], in_=ag[:, 4 * q0:4 * (q0 + BLK)])
-                    pairs.append((cd, sc))
-            return pairs
+                    k = k0 + 4 * n + m
+                    nc.tensor.transpose(out=vps[:, m, :], in_=dinv[:, k:k + 1].to_broadcast([P, P]), identity=ident_f[:])
+                nc.vector.tensor_copy(out=vb[:, BLK * (b0 + n):BLK * (b0 + n + 1)].rearrange("p (u k e) -> p u k e", u=2, e=2),
+                                      in_=vps[:].rearrange("p (u e) k -> p u k e", u=2))
 
         acc = {}
-        seen = {}
+        sums = {}
+        b_f = const.tile([P, 1], F32)
 
-        def finish(B):
-            res = outp.tile([P, BLK], F32, tag="res")
-            nc.scalar.activation(out=res[:], in_=acc[B][:], func=ACT.Relu, bias=b_f[:, 0:1], scale=1.0)
-            tq = tpp.tile([P, 4, F], F32, tag="tp")
-            for m in range(4):
-                nc.tensor.transpose(out=tq[:, m, :], in_=res[:, P * m:P * (m + 1)], identity=ident_f[:])
-            ot = outp.tile([P, 4, F], F32, tag="ot")
-            nc.scalar.copy(out=ot[:], in_=tq[:])
-            nc.sync.dma_start(out=out[BLK * B:BLK * (B + 1), :].rearrange("(m p) f -> p m f", p=P), in_=ot[:])
+        def start_group(B, passes):
+            acc[B] = [None, passes, 0]
 
-        def multiply(B, c, pair):
-            if B not in acc:
-                acc[B] = accp.tile([P, BLK], F32, tag="acc", name="acc%d" % B)
-                seen[B] = 0
-            seen[B] += 1
-            nc.tensor.matmul_mx(out=acc[B][:], lhsT=xw_c[:, F * c:F * (c + 1)].bitcast(FP8X4),
-                                lhsT_scale=xw_s[:, F * c:F * (c + 1)],
-                                rhs=pair[0][:].bitcast(FP8X4), rhs_scale=pair[1][:],
-                                start=(seen[B] == 1), stop=(seen[B] == NPASS))
-            if seen[B] == NPASS:
-                finish(B)
+        def multiply(B, c, pair, last):
+            a = acc[B]
+            if a[2] == 0:
+                a[0] = accp.tile([P, BLK], F32, tag="acc", name="acc%d_%d" % (B, c))
+            a[2] += 1
+            nc.tensor.matmul_mx(out=a[0][:], lhsT=xw_c[:, F * c:F * (c + 1)].bitcast(FP8X4), lhsT_scale=xw_s[:, F * c:F * (c + 1)],
+                                rhs=pair[0][:].bitcast(FP8X4), rhs_scale=pair[1][:], start=(a[2] == 1), stop=(a[2] == a[1]))
+            if a[2] == a[1]:
+                close(B, a[0], last)
 
-        def work(u, col0, width, c, fine):
-            step = BLK if fine else width
-            scale(u, col0, width, c, step)
-            pairs = quantise(u, width, step)
-            return [(col0 // BLK + n, c, pairs[n]) for n in range(len(pairs))]
+        def close(B, ps, last):
+            if B in sums:
+                if last:
+                    res = outp.tile([P, BLK], F32, tag="res")
+                else:
+                    res = sums[B]
+                nc.vector.tensor_tensor(out=res[:], in0=ps[:], in1=sums[B][:], op=ALU.add)
+            else:
+                if last:
+                    res = outp.tile([P, BLK], F32, tag="res")
+                else:
+                    res = const.tile([P, BLK], F32, name="sum%d" % B)
+                    sums[B] = res
+                nc.scalar.activation(out=res[:], in_=ps[:], func=ACT.Identity, bias=b_f[:, 0:1], scale=1.0)
+            if last:
+                tq = t2p.tile([P, 4, F], F32, tag="t2")
+                for m in range(4):
+                    nc.tensor.transpose(out=tq[:, m, :], in_=res[:, P * m:P * (m + 1)], identity=ident_f[:])
+                ot = outp.tile([P, 4, F], F32, tag="ot")
+                nc.scalar.activation(out=ot[:], in_=tq[:], func=ACT.Relu)
+                nc.sync.dma_start(out=out[BLK * B:BLK * (B + 1), :].rearrange("(m p) f -> p m f", p=P), in_=ot[:])
 
-        cs0, keep0 = load_cols(0, PANEL, 4)
-        chain(0, 0, 8, cs0, True)
-        cs1a, keep1a = load_cols(PANEL, BLK, 4)
-        chain(1, 0, 4, cs1a, True)
+        def quantise(ag):
+            cd = cod.tile([P, BLK], U32, tag="cd", align_bytes=64)
+            sc = cod.tile([P, BLK], U8, tag="sc", align_bytes=64)
+            nc.vector.quantize_mx(out=cd[:].bitcast(FP8X4), scales=sc[:], in_=ag[:])
+            return cd, sc
 
-        w_raw = const.tile([P, 4, F], BF16)
-        nc.sync.dma_start(
-            out=w_raw[:].rearrange("q (u e) f -> q u e f", u=2),
-            in_=w.rearrange("(u q e) f -> q u e f", u=2, e=2),
-        )
-        xunits = []
-        for g in range(4):
-            xu = units.tile([P, 8, D], BF16, tag="unit", name="xu%d" % g)
-            nc.sync.dma_start(out=xu[:], in_=x[1024 * g:1024 * (g + 1), :].rearrange("(r p) d -> p r d", p=P))
-            xunits.append(xu)
-        cs1b, keep1b = load_cols(PANEL + BLK, BLK, 4)
-        chain(1, 4, 4, cs1b, False)
+        def turned(u, w0, b, c, rt, r0):
+            ag = grp.tile([P, 4 * BLK], BF16, tag="ag", align_bytes=64)
+            for h in range(2):
+                tp = t1p.tile([P, 2, BLK], BF16, tag="t1")
+                for e in range(2):
+                    s = w0 + 256 * h
+                    for t in range(4):
+                        nc.tensor.transpose(out=tp[:, e, P * t:P * (t + 1)], in_=u[:, t, s + e:s + 256:2], identity=ident_b[:])
+                at = tpool.tile([P, 2, BLK], BF16, tag="at", align_bytes=64)
+                if rt is None:
+                    for e in range(2):
+                        k = 4 * b + 2 * h + e
+                        nc.vector.scalar_tensor_tensor(out=at[:, e, :], in0=tp[:, e, :], scalar=dinv[:, k:k + 1],
+                                                       in1=vb[:, BLK * c:BLK * (c + 1)], op0=ALU.mult, op1=ALU.mult)
+                else:
+                    nc.vector.tensor_tensor(out=at[:], in0=tp[:], in1=rt[:, 2 * h:2 * h + 2, r0:r0 + BLK], op=ALU.mult)
+                words = at[:].rearrange("p e i -> p (e i)").bitcast(F32)
+                tq = t2p.tile([P, 2, 2, P], F32, tag="t2")
+                for v in range(2):
+                    for e in range(2):
+                        s = 256 * e + P * v
+                        nc.tensor.transpose(out=tq[:, v, e, :], in_=words[:, s:s + P], identity=ident_f[:])
+                agw = ag[:].bitcast(F32)
+                nc.scalar.copy(out=agw[:, BLK * h:BLK * (h + 1)].rearrange("p (k e v) -> p k e v", e=2, v=2),
+                               in_=tq[:].rearrange("p v e k -> p k e v"))
+            return quantise(ag)
+
+        count = [0]
+
+        def straight(u, w0, rt, r0):
+            nc.vector.tensor_tensor(out=u[:, :, w0:w0 + BLK], in0=u[:, :, w0:w0 + BLK], in1=rt[:, :, r0:r0 + BLK], op=ALU.mult)
+            ag = grp.tile([P, 4 * BLK], BF16, tag="ag", align_bytes=64)
+            dst = ag[:].rearrange("p (n i t) -> p n t i", i=4, t=4)
+            src = u[:, :, w0:w0 + BLK].rearrange("p t (n i) -> p n t i", i=4)
+            count[0] += 1
+            if count[0] % V_COPY == 0:
+                nc.vector.tensor_copy(out=dst, in_=src)
+            else:
+                nc.scalar.copy(out=dst, in_=src)
+            return quantise(ag)
+
+        def table(a, col0, width):
+            rt = rpool.tile([P, 4, PANEL], BF16, tag="rt")
+            for k in range(4):
+                nc.scalar.activation(out=rt[:, k, 0:width], in_=vb[:, col0:col0 + width], func=ACT.Copy, scale=dinv[:, 4 * a + k:4 * a + k + 1])
+            return rt
 
         waiting = []
-        for c in range(2):
-            waiting.extend(work(keep0[c], 0, PANEL, c, False))
 
-        cs2, keep2 = load_cols(2 * PANEL, PANEL, 6)
-        chain(2, 0, 8, cs2, False)
+        def emit(B, c, pair, last=False):
+            waiting.append((B, c, pair, last))
 
-        w_g = const.tile([P, F, 4], BF16, align_bytes=64)
-        nc.vector.tensor_copy(out=w_g[:], in_=w_raw[:].rearrange("q t f -> q f t"))
-        w_c = const.tile([P, F], U32, align_bytes=64)
-        w_s = const.tile([P, F], U8, align_bytes=64)
-        nc.vector.quantize_mx(out=w_c[:].bitcast(FP8X4), scales=w_s[:], in_=w_g[:].rearrange("q f t -> q (f t)"))
-        xw_g = const.tile([P, 4 * PANEL], BF16, align_bytes=64)
-        xw_gv = xw_g[:].rearrange("p (c f t) -> p c f t", c=NPASS, t=4)
-        for g in range(4):
-            xu = xunits[g]
-            xg = grp.tile([P, 4 * PANEL], BF16, tag="ag", align_bytes=64)
-            xg32 = xg[:].bitcast(F32).rearrange("p (r i u) -> p r i u", r=8, u=2)
-            for k in range(4):
-                tp = accp.tile([P, 2, 2, P], F32, tag="acc", name="xt%d_%d" % (g, k))
-                for r2 in range(2):
-                    xr = xu[:, 2 * k + r2, :].bitcast(F32)
-                    for u2 in range(2):
-                        nc.tensor.transpose(out=tp[:, r2, u2, :], in_=xr[:, P * u2:P * (u2 + 1)], identity=ident_f[:])
-                nc.scalar.copy(out=xg32[:, 2 * k:2 * k + 2], in_=tp[:].rearrange("p r u i -> p r i u"))
-            for cc in range(2):
-                c = 2 * g + cc
-                xc = cod.tile([P, BLK], U32, tag="cd", align_bytes=64)
-                xs = cod.tile([P, BLK], U8, tag="sc", align_bytes=64)
-                nc.vector.quantize_mx(out=xc[:].bitcast(FP8X4), scales=xs[:], in_=xg[:, 2048 * cc:2048 * (cc + 1)])
-                xwp = accp.tile([P, 4, F], F32, tag="acc", name="xwp%d" % c)
-                for t in range(4):
-                    nc.tensor.matmul_mx(out=xwp[:, t, :], lhsT=xc[:, P * t:P * (t + 1)].bitcast(FP8X4),
-                                        lhsT_scale=xs[:, P * t:P * (t + 1)], rhs=w_c[:].bitcast(FP8X4), rhs_scale=w_s[:],
-                                        start=True, stop=True)
-                nc.scalar.copy(out=xw_gv[:, c], in_=xwp[:].rearrange("p t f -> p f t"))
-            if g % 2 == 1:
-                hh = g // 2
-                nc.vector.quantize_mx(out=xw_c[:, 512 * hh:512 * (hh + 1)].bitcast(FP8X4), scales=xw_s[:, 512 * hh:512 * (hh + 1)],
-                                      in_=xw_g[:, 2048 * hh:2048 * (hh + 1)])
+        def flush():
+            for B, c, pair, last in waiting:
+                multiply(B, c, pair, last)
+            waiting.clear()
 
-        def run(u, col0, width, c, fine):
-            for B, cc, pair in work(u, col0, width, c, fine):
-                multiply(B, cc, pair)
+        def features():
+            w_raw = const.tile([P, 4, F], BF16)
+            nc.sync.dma_start(out=w_raw[:].rearrange("q (u e) f -> q u e f", u=2), in_=w.rearrange("(u q e) f -> q u e f", u=2, e=2))
+            xunits = []
+            for g in range(4):
+                xu = units.tile([P, 4, 2, D], BF16, tag="unit", name="xu%d" % g)
+                nc.sync.dma_start(out=xu[:].rearrange("p r e d -> p r (e d)"),
+                                  in_=x[1024 * g:1024 * (g + 1), :].rearrange("(r p e) d -> p r (e d)", p=P, e=2))
+                xunits.append(xu)
+            b_raw = const.tile([P, 1], BF16)
+            nc.sync.dma_start(out=b_raw[:], in_=b.rearrange("(p o) -> p o", o=1))
+            nc.vector.tensor_copy(out=b_f[:], in_=b_raw[:])
+            w_g = const.tile([P, F, 4], BF16, align_bytes=64)
+            nc.vector.tensor_copy(out=w_g[:], in_=w_raw[:].rearrange("q t f -> q f t"))
+            w_c = const.tile([P, F], U32, align_bytes=64)
+            w_s = const.tile([P, F], U8, align_bytes=64)
+            nc.vector.quantize_mx(out=w_c[:].bitcast(FP8X4), scales=w_s[:], in_=w_g[:].rearrange("q f t -> q (f t)"))
+            for hh in range(2):
+                xw_g = grp.tile([P, 4 * BLK], BF16, tag="ag", align_bytes=64)
+                xw_v = xw_g[:].rearrange("p (c f t) -> p c f t", c=4, t=4)
+                for cc in range(4):
+                    c = 4 * hh + cc
+                    xu = xunits[c // 2]
+                    xg = grp.tile([P, 4 * BLK], BF16, tag="ag", align_bytes=64)
+                    xg32 = xg[:].bitcast(F32).rearrange("p (r i u) -> p r i u", r=4, u=2)
+                    for k in range(2):
+                        tp = t2p.tile([P, 2, 2, P], F32, tag="t2", name="xt%d_%d" % (c, k))
+                        for e in range(2):
+                            xr = xu[:, 2 * (c % 2) + k, e, :].bitcast(F32)
+                            for u2 in range(2):
+                                nc.tensor.transpose(out=tp[:, e, u2, :], in_=xr[:, P * u2:P * (u2 + 1)], identity=ident_f[:])
+                        nc.scalar.copy(out=xg32[:, 2 * k:2 * k + 2], in_=tp[:].rearrange("p e u i -> p e i u"))
+                    xc, xs = quantise(xg)
+                    xwp = accp.tile([P, 4, F], F32, tag="acc", name="xwp%d" % c)
+                    for t in range(4):
+                        nc.tensor.matmul_mx(out=xwp[:, t, :], lhsT=xc[:, P * t:P * (t + 1)].bitcast(FP8X4),
+                                            lhsT_scale=xs[:, P * t:P * (t + 1)], rhs=w_c[:].bitcast(FP8X4), rhs_scale=w_s[:],
+                                            start=True, stop=True)
+                    nc.scalar.copy(out=xw_v[:, cc], in_=xwp[:].rearrange("p t f -> p f t"))
+                nc.vector.quantize_mx(out=xw_c[:, BLK * hh:BLK * (hh + 1)].bitcast(FP8X4), scales=xw_s[:, BLK * hh:BLK * (hh + 1)], in_=xw_g[:])
 
-        for B, c, pair in waiting:
-            multiply(B, c, pair)
+        def own(b, c):
+            return turned(unit[(b // 2, c)], BLK * (b % 2), b, c, None, 0)
 
-        for c in range(3):
-            run(keep1a[c], PANEL, BLK, c, False)
-        run(keep0[2], 0, PANEL, 2, False)
-        for c in range(4):
-            run(keep1b[c], PANEL + BLK, BLK, c, False)
-        run(keep1a[3], PANEL, BLK, 3, False)
-        run(keep0[3], 0, PANEL, 3, False)
+        def pairs(a, cols, last):
+            rt = table(a, BLK * cols[0], BLK * len(cols))
+            J = cols[0] // 2
+            ready = []
+            for n in range(len(cols)):
+                ready.append((cols[n], a, straight(unit[(J, a)], BLK * (cols[n] % 2), rt, BLK * n), False))
+                ready.append((a, cols[n], turned(unit[(a // 2, cols[n])], BLK * (a % 2), a, cols[n], rt, BLK * n), last))
+            return ready
 
-        cs3, keep3 = load_cols(3 * PANEL, PANEL, NPASS)
-        chain(3, 0, 8, cs3, False)
-        b_raw = const.tile([P, 1], BF16)
-        nc.sync.dma_start(out=b_raw[:], in_=b.rearrange("(p o) -> p o", o=1))
-        b_f = const.tile([P, 1], F32)
-        nc.vector.tensor_copy(out=b_f[:], in_=b_raw[:])
+        degrees(0, 0, BLK)
+        start_group(0, 2)
+        start_group(1, 2)
+        emit(0, 0, own(0, 0))
+        features()
+        degrees(0, BLK, BLK)
+        degrees(1, 0, BLK)
+        for bb, cc in ((1, 0), (0, 1), (1, 1)):
+            emit(bb, cc, own(bb, cc))
+        flush()
 
-        tail = [(2, c) for c in range(NPASS)] + [(3, c) for c in range(NPASS)]
-        for J in (1, 0):
-            tail.extend([(J, c) for c in range(4, NPASS)])
-        loaded = {}
-        for c in keep2:
-            loaded[(2, c)] = keep2[c]
-        for c in keep3:
-            loaded[(3, c)] = keep3[c]
-        for idx in range(len(tail)):
-            for q in range(idx, min(idx + LOOKAHEAD + 1, len(tail))):
-                if tail[q] not in loaded:
-                    loaded[tail[q]] = load_unit(PANEL * tail[q][0], PANEL, tail[q][1])
-            J, c = tail[idx]
-            run(loaded[(J, c)], PANEL * J, PANEL, c, idx == len(tail) - 1)
+        degrees(1, BLK, BLK)
+        start_group(2, 4)
+        emit(2, 2, own(2, 2))
+        flush()
+        start_group(3, 4)
+        for a in range(2):
+            start_group(a, 2)
+            for n in (2, 3):
+                for B, c, pair, last in pairs(a, [n], False):
+                    multiply(B, c, pair, last)
+        for bb, cc in ((3, 2), (2, 3), (3, 3)):
+            multiply(bb, cc, own(bb, cc), False)
+
+        def diagonal(J):
+            start_group(2 * J, 2 * J + 2)
+            start_group(2 * J + 1, 2 * J + 2)
+            for bb, cc in ((2 * J, 2 * J), (2 * J + 1, 2 * J), (2 * J, 2 * J + 1), (2 * J + 1, 2 * J + 1)):
+                multiply(bb, cc, own(bb, cc), False)
+
+        def mirror(J, rows):
+            for a in rows:
+                start_group(a, 2)
+                for B, c, pair, last in pairs(a, [2 * J, 2 * J + 1], J == 3):
+                    multiply(B, c, pair, J == 3)
+
+        degrees(2, 0, PANEL)
+        diagonal(2)
+        degrees(3, 0, PANEL, (6, lambda: mirror(2, (0, 1))))
+        mirror(2, (2, 3))
+        for I in range(2):
+            for c in (6, 7):
+                load(I, c, 0, PANEL, True)
+        diagonal(3)
+        mirror(3, range(6))

@@ -19,9 +19,11 @@ F = 128
 PANEL = 1024
 BLK = 512
 NBLK = N // BLK
-UNIT_BUFS = 16
-COD_BUFS = 8
-V_COPY = 4
+UNIT_BUFS = 17
+AG_BUFS = 5
+COD_BUFS = 6
+LAG = 6
+LAG_D = 4
 TINY = 1e-30
 
 FLOPS = 2 * N * D * F + 2 * N * N * F
@@ -32,16 +34,16 @@ def tile_simplegcn_pa_t_kernel(tc, x, adjacency, w, b, out):
     with ExitStack() as ctx:
         const = ctx.enter_context(tc.tile_pool(name="const", bufs=1))
         units = ctx.enter_context(tc.tile_pool(name="units", bufs=UNIT_BUFS))
-        grp = ctx.enter_context(tc.tile_pool(name="grp", bufs=4))
+        grp = ctx.enter_context(tc.tile_pool(name="grp", bufs=AG_BUFS))
         rpool = ctx.enter_context(tc.tile_pool(name="rpool", bufs=2))
-        tpool = ctx.enter_context(tc.tile_pool(name="tpool", bufs=3))
+        plain = ctx.enter_context(tc.tile_pool(name="plain", bufs=3))
         cod = ctx.enter_context(tc.tile_pool(name="cod", bufs=COD_BUFS))
         small = ctx.enter_context(tc.tile_pool(name="small", bufs=2))
         outp = ctx.enter_context(tc.tile_pool(name="outp", bufs=2))
         t1p = ctx.enter_context(tc.psum_pool(name="t1p", bufs=2))
-        t2p = ctx.enter_context(tc.psum_pool(name="t2p", bufs=2))
+        t2p = ctx.enter_context(tc.psum_pool(name="t2p", bufs=1))
         csp = ctx.enter_context(tc.psum_pool(name="csp", bufs=1))
-        accp = ctx.enter_context(tc.psum_pool(name="accp", bufs=3))
+        accp = ctx.enter_context(tc.psum_pool(name="accp", bufs=4))
 
         ident_f = const.tile([P, P], F32)
         make_identity(nc, ident_f[:])
@@ -54,100 +56,112 @@ def tile_simplegcn_pa_t_kernel(tc, x, adjacency, w, b, out):
         warm2 = const.tile([P, 1], F32)
         nc.scalar.activation(out=warm2[:], in_=warm[:], func=ACT.Sqrt)
 
-        vb = const.tile([P, N], F32)
+        vb = const.tile([P, 2 * PANEL], F32)
         dinv = const.tile([P, 4 * NBLK], F32)
         xw_c = const.tile([P, NBLK * F], U32, align_bytes=64)
         xw_s = const.tile([P, NBLK * F], U8, align_bytes=64)
+        b_f = const.tile([P, 1], F32)
+
+        later = []
+        step = [0]
+
+        def after(steps, action):
+            later.append((step[0] + steps, action))
+
+        def tick():
+            step[0] += 1
+            for item in list(later):
+                if item[0] <= step[0]:
+                    later.remove(item)
+                    item[1]()
 
         unit = {}
+        loops = {}
 
-        def load(J, c, w0, width, again=False):
-            if again or (J, c) not in unit:
-                unit[(J, c)] = units.tile([P, 4, PANEL], BF16, tag="unit", name="u%d_%d_%d" % (J, c, int(again)))
-            u = unit[(J, c)]
-            src = adjacency[BLK * c:BLK * (c + 1), PANEL * J + w0:PANEL * J + w0 + width]
-            if c < 2 * J:
+        def load(J, c, halves):
+            tile = units.tile([P, 4, PANEL], BF16, tag="unit", name="u%d_%d_%d" % (J, c, len(unit)))
+            rows = adjacency[BLK * c:BLK * (c + 1), PANEL * J:PANEL * (J + 1)].rearrange("(t p) w -> p t w", p=P)
+            if halves:
+                two = tile[:].rearrange("p t w -> p (t w)").rearrange("p (h t w) -> p h t w", h=2, t=4)
                 for h in range(2):
-                    nc.sync.dma_start(out=u[:, 2 * h:2 * h + 2, w0:w0 + width],
-                                      in_=src[256 * h:256 * (h + 1), :].rearrange("(p e) w -> p e w", e=2))
-            else:
-                nc.sync.dma_start(out=u[:, :, w0:w0 + width], in_=src.rearrange("(t p) w -> p t w", p=P))
-            return u
+                    unit[(2 * J + h, c)] = two[:, h]
+                    loops[(2 * J + h, c)] = two[:, h].rearrange("p t (n k) -> p (t n) k", k=P)[:, 0:16:5, :]
+                return lambda h: nc.sync.dma_start(out=two[:, h], in_=rows[:, :, BLK * h:BLK * (h + 1)])
+            for h in range(2):
+                unit[(2 * J + h, c)] = tile[:, :, BLK * h:BLK * (h + 1)]
+                loops[(2 * J + h, c)] = tile[:].rearrange("p t (n k) -> p (t n) k", k=P)[:, 4 * h:4 * h + 28:9, :]
+            nc.sync.dma_start(out=tile[:], in_=rows)
+            return None
 
-        def degrees(J, w0, width, pause=(None, None)):
-            nb = width // BLK
-            b0 = (PANEL * J + w0) // BLK
-            cs = csp.tile([P, 4 * nb, NBLK], F32, tag="cs", name="cs%d" % b0)
-            for c in range(NBLK):
-                if c == pause[0]:
-                    pause[1]()
-                u = load(J, c, w0, width)
-                if b0 <= c < b0 + nb:
-                    for t in range(4):
-                        d0 = BLK * c - PANEL * J + P * t
-                        nc.vector.tensor_tensor(out=u[:, t, d0:d0 + P], in0=u[:, t, d0:d0 + P], in1=ident_b[:], op=ALU.add)
-                for m in range(4 * nb):
-                    s = w0 + 256 * (m // 2)
-                    for t in range(4):
-                        nc.tensor.matmul(out=cs[:, m, c:c + 1], lhsT=u[:, t, s + m % 2:s + 256:2], rhs=ones[:, 0:1],
-                                         start=(t == 0), stop=(t == 3))
-            nm = 4 * nb
-            k0 = 4 * b0
-            deg = small.tile([P, nm], F32, tag="deg")
-            nc.vector.tensor_reduce(out=deg[:], in_=cs[:], axis=AX.X, op=ALU.add)
-            dcl = small.tile([P, nm], F32, tag="dcl")
-            nc.vector.tensor_scalar_max(out=dcl[:], in0=deg[:], scalar1=TINY)
-            sq = small.tile([P, nm], F32, tag="sq")
-            nc.scalar.activation(out=sq[:], in_=dcl[:], func=ACT.Sqrt)
-            rc = small.tile([P, nm], F32, tag="rc")
-            nc.vector.reciprocal(out=rc[:], in_=sq[:])
-            nc.vector.scalar_tensor_tensor(out=dinv[:, k0:k0 + nm], in0=deg[:], scalar=0.0, in1=rc[:], op0=ALU.is_gt, op1=ALU.mult)
-            for n in range(nb):
-                vps = t2p.tile([P, 4, P], F32, tag="t2", name="vps%d" % (b0 + n))
+        cs = {}
+
+        def count(b0, nb, c):
+            if c == 0:
+                cs[b0] = csp.tile([P, 4 * nb, NBLK], F32, tag="cs", name="cs%d" % b0)
+            for m in range(4 * nb):
+                u = unit[(b0 + m // 4, c)]
+                s = P * (m % 4)
+                for t in range(4):
+                    nc.tensor.matmul(out=cs[b0][:, m, c:c + 1], lhsT=u[:, t, s:s + P], rhs=ones[:, 0:1], start=(t == 0), stop=(t == 3))
+
+        deg = {}
+        sq = {}
+
+        def root(b0, nb):
+            deg[b0] = small.tile([P, 4 * nb], F32, tag="deg", name="deg%d" % b0)
+            nc.vector.tensor_reduce(out=deg[b0][:], in_=cs[b0][:], axis=AX.X, op=ALU.add)
+            dcl = small.tile([P, 4 * nb], F32, tag="dcl")
+            nc.vector.tensor_scalar(out=dcl[:], in0=deg[b0][:], scalar1=1.0, scalar2=TINY, op0=ALU.add, op1=ALU.max)
+            sq[b0] = small.tile([P, 4 * nb], F32, tag="sq", name="sq%d" % b0)
+            nc.scalar.activation(out=sq[b0][:], in_=dcl[:], func=ACT.Sqrt)
+
+        def spread(b0, nb):
+            rc = small.tile([P, 4 * nb], F32, tag="rc")
+            nc.vector.reciprocal(out=rc[:], in_=sq[b0][:])
+            nc.vector.scalar_tensor_tensor(out=dinv[:, 4 * b0:4 * (b0 + nb)], in0=deg[b0][:], scalar=-1.0, in1=rc[:], op0=ALU.is_gt, op1=ALU.mult)
+            for n in range(b0, b0 + nb):
+                vps = t2p.tile([P, BLK], F32, tag="t2", name="vps%d" % n)
                 for m in range(4):
-                    k = k0 + 4 * n + m
-                    nc.tensor.transpose(out=vps[:, m, :], in_=dinv[:, k:k + 1].to_broadcast([P, P]), identity=ident_f[:])
-                nc.vector.tensor_copy(out=vb[:, BLK * (b0 + n):BLK * (b0 + n + 1)].rearrange("p (u k e) -> p u k e", u=2, e=2),
-                                      in_=vps[:].rearrange("p (u e) k -> p u k e", u=2))
+                    nc.tensor.transpose(out=vps[:, P * m:P * (m + 1)], in_=dinv[:, 4 * n + m:4 * n + m + 1].to_broadcast([P, P]), identity=ident_f[:])
+                nc.scalar.copy(out=vb[:, BLK * (n % 4):BLK * (n % 4 + 1)], in_=vps[:])
 
         acc = {}
         sums = {}
-        b_f = const.tile([P, 1], F32)
 
-        def start_group(B, passes):
-            acc[B] = [None, passes, 0]
-
-        def multiply(B, c, pair, last):
-            a = acc[B]
-            if a[2] == 0:
-                a[0] = accp.tile([P, BLK], F32, tag="acc", name="acc%d_%d" % (B, c))
-            a[2] += 1
+        def multiply(B, c, pair):
+            J = max(B, c) // 2
+            passes = 2 * J + 2 if J == B // 2 else 2
+            if (B, J) not in acc:
+                acc[(B, J)] = [accp.tile([P, BLK], F32, tag="acc", name="acc%d_%d" % (B, J)), 0]
+            a = acc[(B, J)]
+            a[1] += 1
             nc.tensor.matmul_mx(out=a[0][:], lhsT=xw_c[:, F * c:F * (c + 1)].bitcast(FP8X4), lhsT_scale=xw_s[:, F * c:F * (c + 1)],
-                                rhs=pair[0][:].bitcast(FP8X4), rhs_scale=pair[1][:], start=(a[2] == 1), stop=(a[2] == a[1]))
-            if a[2] == a[1]:
-                close(B, a[0], last)
+                                rhs=pair[0][:].bitcast(FP8X4), rhs_scale=pair[1][:], start=(a[1] == 1), stop=(a[1] == passes))
+            if a[1] == passes:
+                after(1, lambda: close(B, a[0], J == 3))
 
         def close(B, ps, last):
+            if last:
+                res = outp.tile([P, BLK], F32, tag="res")
+            elif B in sums:
+                res = sums[B]
+            else:
+                res = const.tile([P, BLK], F32, name="sum%d" % B)
             if B in sums:
-                if last:
-                    res = outp.tile([P, BLK], F32, tag="res")
-                else:
-                    res = sums[B]
                 nc.vector.tensor_tensor(out=res[:], in0=ps[:], in1=sums[B][:], op=ALU.add)
             else:
-                if last:
-                    res = outp.tile([P, BLK], F32, tag="res")
-                else:
-                    res = const.tile([P, BLK], F32, name="sum%d" % B)
-                    sums[B] = res
                 nc.scalar.activation(out=res[:], in_=ps[:], func=ACT.Identity, bias=b_f[:, 0:1], scale=1.0)
+                sums[B] = res
             if last:
-                tq = t2p.tile([P, 4, F], F32, tag="t2")
-                for m in range(4):
-                    nc.tensor.transpose(out=tq[:, m, :], in_=res[:, P * m:P * (m + 1)], identity=ident_f[:])
-                ot = outp.tile([P, 4, F], F32, tag="ot")
-                nc.scalar.activation(out=ot[:], in_=tq[:], func=ACT.Relu)
-                nc.sync.dma_start(out=out[BLK * B:BLK * (B + 1), :].rearrange("(m p) f -> p m f", p=P), in_=ot[:])
+                after(1, lambda: store(B, res))
+
+        def store(B, res):
+            tq = t2p.tile([P, 4, F], F32, tag="t2")
+            for m in range(4):
+                nc.tensor.transpose(out=tq[:, m, :], in_=res[:, P * m:P * (m + 1)], identity=ident_f[:])
+            ot = outp.tile([P, 4, F], F32, tag="ot")
+            nc.scalar.activation(out=ot[:], in_=tq[:], func=ACT.Relu)
+            nc.sync.dma_start(out=out[BLK * B:BLK * (B + 1), :].rearrange("(m p) f -> p m f", p=P), in_=ot[:])
 
         def quantise(ag):
             cd = cod.tile([P, BLK], U32, tag="cd", align_bytes=64)
@@ -155,158 +169,276 @@ def tile_simplegcn_pa_t_kernel(tc, x, adjacency, w, b, out):
             nc.vector.quantize_mx(out=cd[:].bitcast(FP8X4), scales=sc[:], in_=ag[:])
             return cd, sc
 
-        def turned(u, w0, b, c, rt, r0):
-            ag = grp.tile([P, 4 * BLK], BF16, tag="ag", align_bytes=64)
-            for h in range(2):
-                tp = t1p.tile([P, 2, BLK], BF16, tag="t1")
-                for e in range(2):
-                    s = w0 + 256 * h
-                    for t in range(4):
-                        nc.tensor.transpose(out=tp[:, e, P * t:P * (t + 1)], in_=u[:, t, s + e:s + 256:2], identity=ident_b[:])
-                at = tpool.tile([P, 2, BLK], BF16, tag="at", align_bytes=64)
-                if rt is None:
-                    for e in range(2):
-                        k = 4 * b + 2 * h + e
-                        nc.vector.scalar_tensor_tensor(out=at[:, e, :], in0=tp[:, e, :], scalar=dinv[:, k:k + 1],
-                                                       in1=vb[:, BLK * c:BLK * (c + 1)], op0=ALU.mult, op1=ALU.mult)
-                else:
-                    nc.vector.tensor_tensor(out=at[:], in0=tp[:], in1=rt[:, 2 * h:2 * h + 2, r0:r0 + BLK], op=ALU.mult)
-                words = at[:].rearrange("p e i -> p (e i)").bitcast(F32)
-                tq = t2p.tile([P, 2, 2, P], F32, tag="t2")
-                for v in range(2):
-                    for e in range(2):
-                        s = 256 * e + P * v
-                        nc.tensor.transpose(out=tq[:, v, e, :], in_=words[:, s:s + P], identity=ident_f[:])
-                agw = ag[:].bitcast(F32)
-                nc.scalar.copy(out=agw[:, BLK * h:BLK * (h + 1)].rearrange("p (k e v) -> p k e v", e=2, v=2),
-                               in_=tq[:].rearrange("p v e k -> p k e v"))
-            return quantise(ag)
+        def finish(B, c, ag):
+            pair = quantise(ag)
+            after(1, lambda: multiply(B, c, pair))
 
-        count = [0]
+        def columns(ap):
+            return ap.rearrange("p t (n i) -> p n t i", i=4)
 
-        def straight(u, w0, rt, r0):
-            nc.vector.tensor_tensor(out=u[:, :, w0:w0 + BLK], in0=u[:, :, w0:w0 + BLK], in1=rt[:, :, r0:r0 + BLK], op=ALU.mult)
-            ag = grp.tile([P, 4 * BLK], BF16, tag="ag", align_bytes=64)
-            dst = ag[:].rearrange("p (n i t) -> p n t i", i=4, t=4)
-            src = u[:, :, w0:w0 + BLK].rearrange("p t (n i) -> p n t i", i=4)
-            count[0] += 1
-            if count[0] % V_COPY == 0:
-                nc.vector.tensor_copy(out=dst, in_=src)
-            else:
-                nc.scalar.copy(out=dst, in_=src)
-            return quantise(ag)
+        def grouped(ap):
+            return ap.rearrange("p (n i t) -> p n t i", i=4, t=4)
 
-        def table(a, col0, width):
-            rt = rpool.tile([P, 4, PANEL], BF16, tag="rt")
+        def group_tile(B, c):
+            return grp.tile([P, 4 * BLK], BF16, tag="ag", align_bytes=64, name="ag%d_%d" % (B, c))
+
+        tables = {}
+
+        def table(job):
+            a, cols = job
+            rt = rpool.tile([P, 4, PANEL], BF16, tag="rt", name="rt%d_%d" % (a, cols[0]))
+            tables[job] = rt
+            col0 = BLK * (cols[0] % 4)
+            width = BLK * len(cols)
             for k in range(4):
-                nc.scalar.activation(out=rt[:, k, 0:width], in_=vb[:, col0:col0 + width], func=ACT.Copy, scale=dinv[:, 4 * a + k:4 * a + k + 1])
-            return rt
+                dv = dinv[:, 4 * a + k:4 * a + k + 1]
+                nc.scalar.activation(out=rt[:, k, 0:width], in_=vb[:, col0:col0 + width], func=ACT.Copy, scale=dv)
 
-        waiting = []
+        turned = {}
 
-        def emit(B, c, pair, last=False):
-            waiting.append((B, c, pair, last))
+        def turn(half):
+            job, n, h = half
+            rt = tables[job]
+            tp = t1p.tile([P, 4, 256], BF16, tag="t1", name="tp%d_%d_%d" % (job[0], job[1][n], h))
+            for t in range(4):
+                for m in range(2):
+                    s = BLK * n + P * t
+                    nc.tensor.transpose(out=tp[:, t, P * m:P * (m + 1)], in_=rt[:, 2 * h + m, s:s + P], identity=ident_b[:])
+            turned[half] = tp
 
-        def flush():
-            for B, c, pair, last in waiting:
-                multiply(B, c, pair, last)
-            waiting.clear()
+        ag_m = {}
+
+        def mirrored(half):
+            job, n, h = half
+            a, cols = job
+            c = cols[n]
+            if h == 0:
+                ag_m[(a, c)] = group_tile(a, c)
+            ag = ag_m[(a, c)]
+            u = unit[(a, c)][:, :, 256 * h:256 * (h + 1)]
+            dst = grouped(ag[:, PANEL * h:PANEL * (h + 1)])
+            nc.vector.tensor_tensor(out=dst, in0=columns(u), in1=columns(turned[half][:]), op=ALU.mult)
+            if h == 1:
+                after(2, lambda: finish(a, c, ag))
+
+        planes = {}
+
+        def straight(job, n):
+            a, cols = job
+            B = cols[n]
+            pl = plain.tile([P, 4, BLK], BF16, tag="pl", name="pl%d_%d" % (B, a))
+            planes[(B, a)] = pl
+            nc.vector.tensor_tensor(out=pl[:], in0=unit[(B, a)], in1=tables[job][:, :, BLK * n:BLK * (n + 1)], op=ALU.mult)
+
+        def interleave(job, n, steps):
+            a, cols = job
+            B = cols[n]
+            ag = group_tile(B, a)
+            nc.scalar.copy(out=grouped(ag[:]), in_=columns(planes[(B, a)][:]))
+            after(steps, lambda: finish(B, a, ag))
+
+        def diagonal(a):
+            u = unit[(a, a)]
+            nc.gpsimd.tensor_tensor(out=loops[(a, a)], in0=loops[(a, a)], in1=ident_b[:].unsqueeze(1).to_broadcast([P, 4, P]), op=ALU.add)
+            pl = plain.tile([P, 4, BLK], BF16, tag="pl", name="pl%d_%d" % (a, a))
+            v0 = BLK * (a % 4)
+            for t in range(4):
+                nc.vector.scalar_tensor_tensor(out=pl[:, t, :], in0=u[:, t, :], scalar=dinv[:, 4 * a + t:4 * a + t + 1],
+                                               in1=vb[:, v0:v0 + BLK], op0=ALU.mult, op1=ALU.mult)
+            ag = group_tile(a, a)
+            nc.scalar.copy(out=grouped(ag[:]), in_=columns(pl[:]))
+            after(LAG_D, lambda: finish(a, a, ag))
+
+        def halves(job):
+            a, cols = job
+            return [] if cols == (a,) else [(job, n, h) for n in range(len(cols)) for h in range(2)]
+
+        def run(jobs, fill):
+            queue = []
+            for job in jobs:
+                queue.extend(halves(job))
+            turns = [0]
+
+            def turn_next(hs):
+                if turns[0] < len(queue) and queue[turns[0]] in hs:
+                    turn(queue[turns[0]])
+                    turns[0] += 1
+
+            for i in range(len(jobs)):
+                job = jobs[i]
+                a, cols = job
+                extra = list(fill.get(job, []))
+                nxt = jobs[i + 1] if i + 1 < len(jobs) else None
+
+                def early():
+                    if nxt is not None and nxt[1] != (nxt[0],) and nxt not in tables and BLK * nxt[1][-1] < ready[0]:
+                        table(nxt)
+
+                def done():
+                    tick()
+                    if extra:
+                        e = extra[0]
+                        extra.remove(e)
+                        e()
+                    early()
+
+                early()
+                if cols == (a,):
+                    diagonal(a)
+                    done()
+                else:
+                    hs = halves(job)
+                    turn_next(hs[0:2])
+                    turn_next(hs[0:2])
+                    straight(job, 0)
+                    interleave(job, 0, LAG)
+                    done()
+                    mirrored(hs[0])
+                    turn_next(hs)
+                    done()
+                    if len(cols) == 2:
+                        straight(job, 1)
+                        interleave(job, 1, LAG)
+                        done()
+                    for q in range(1, len(hs)):
+                        mirrored(hs[q])
+                        turn_next(hs)
+                        done()
+                for e in list(extra):
+                    e()
+                    early()
+
+        ready = [0]
+
+        def degrees_done(b0, nb):
+            spread(b0, nb)
+            ready[0] = BLK * (b0 + nb)
+
+        def degrees(b):
+            for c in range(NBLK):
+                count(b, 1, c)
+            root(b, 1)
+            degrees_done(b, 1)
 
         def features():
-            w_raw = const.tile([P, 4, F], BF16)
-            nc.sync.dma_start(out=w_raw[:].rearrange("q (u e) f -> q u e f", u=2), in_=w.rearrange("(u q e) f -> q u e f", u=2, e=2))
-            xunits = []
-            for g in range(4):
-                xu = units.tile([P, 4, 2, D], BF16, tag="unit", name="xu%d" % g)
-                nc.sync.dma_start(out=xu[:].rearrange("p r e d -> p r (e d)"),
-                                  in_=x[1024 * g:1024 * (g + 1), :].rearrange("(r p e) d -> p r (e d)", p=P, e=2))
-                xunits.append(xu)
-            b_raw = const.tile([P, 1], BF16)
-            nc.sync.dma_start(out=b_raw[:], in_=b.rearrange("(p o) -> p o", o=1))
-            nc.vector.tensor_copy(out=b_f[:], in_=b_raw[:])
             w_g = const.tile([P, F, 4], BF16, align_bytes=64)
             nc.vector.tensor_copy(out=w_g[:], in_=w_raw[:].rearrange("q t f -> q f t"))
             w_c = const.tile([P, F], U32, align_bytes=64)
             w_s = const.tile([P, F], U8, align_bytes=64)
             nc.vector.quantize_mx(out=w_c[:].bitcast(FP8X4), scales=w_s[:], in_=w_g[:].rearrange("q f t -> q (f t)"))
-            for hh in range(2):
-                xw_g = grp.tile([P, 4 * BLK], BF16, tag="ag", align_bytes=64)
-                xw_v = xw_g[:].rearrange("p (c f t) -> p c f t", c=4, t=4)
-                for cc in range(4):
-                    c = 4 * hh + cc
-                    xu = xunits[c // 2]
-                    xg = grp.tile([P, 4 * BLK], BF16, tag="ag", align_bytes=64)
-                    xg32 = xg[:].bitcast(F32).rearrange("p (r i u) -> p r i u", r=4, u=2)
-                    for k in range(2):
-                        tp = t2p.tile([P, 2, 2, P], F32, tag="t2", name="xt%d_%d" % (c, k))
-                        for e in range(2):
-                            xr = xu[:, 2 * (c % 2) + k, e, :].bitcast(F32)
-                            for u2 in range(2):
-                                nc.tensor.transpose(out=tp[:, e, u2, :], in_=xr[:, P * u2:P * (u2 + 1)], identity=ident_f[:])
-                        nc.scalar.copy(out=xg32[:, 2 * k:2 * k + 2], in_=tp[:].rearrange("p e u i -> p e i u"))
-                    xc, xs = quantise(xg)
-                    xwp = accp.tile([P, 4, F], F32, tag="acc", name="xwp%d" % c)
-                    for t in range(4):
-                        nc.tensor.matmul_mx(out=xwp[:, t, :], lhsT=xc[:, P * t:P * (t + 1)].bitcast(FP8X4),
-                                            lhsT_scale=xs[:, P * t:P * (t + 1)], rhs=w_c[:].bitcast(FP8X4), rhs_scale=w_s[:],
-                                            start=True, stop=True)
-                    nc.scalar.copy(out=xw_v[:, cc], in_=xwp[:].rearrange("p t f -> p f t"))
-                nc.vector.quantize_mx(out=xw_c[:, BLK * hh:BLK * (hh + 1)].bitcast(FP8X4), scales=xw_s[:, BLK * hh:BLK * (hh + 1)], in_=xw_g[:])
+            nc.vector.tensor_copy(out=b_f[:], in_=b_raw[:])
+            xw_g = [grp.tile([P, 4 * BLK], BF16, tag="ag", align_bytes=64, name="xw%d" % hh) for hh in range(2)]
+            codes = {}
+            sums_x = {}
 
-        def own(b, c):
-            return turned(unit[(b // 2, c)], BLK * (b % 2), b, c, None, 0)
+            def regroup(c):
+                xg = grp.tile([P, 4 * BLK], BF16, tag="ag", align_bytes=64, name="xg%d" % c)
+                xg32 = xg[:].bitcast(F32).rearrange("p (r i u) -> p r i u", r=4, u=2)
+                for k in range(2):
+                    tp = accp.tile([P, 2, 2, P], F32, tag="acc", name="xt%d_%d" % (c, k))
+                    for e in range(2):
+                        xr = xunits[c // 2][:, 4 * (c % 2) + 2 * k + e, :].bitcast(F32)
+                        for u2 in range(2):
+                            nc.tensor.transpose(out=tp[:, e, u2, :], in_=xr[:, P * u2:P * (u2 + 1)], identity=ident_f[:])
+                    if k == 0:
+                        nc.scalar.copy(out=xg32[:, 0:2], in_=tp[:].rearrange("p e u i -> p e i u"))
+                    else:
+                        nc.vector.tensor_copy(out=xg32[:, 2:4], in_=tp[:].rearrange("p e u i -> p e i u"))
+                codes[c] = xg
 
-        def pairs(a, cols, last):
-            rt = table(a, BLK * cols[0], BLK * len(cols))
-            J = cols[0] // 2
-            ready = []
-            for n in range(len(cols)):
-                ready.append((cols[n], a, straight(unit[(J, a)], BLK * (cols[n] % 2), rt, BLK * n), False))
-                ready.append((a, cols[n], turned(unit[(a // 2, cols[n])], BLK * (a % 2), a, cols[n], rt, BLK * n), last))
-            return ready
+            def times_w(c):
+                xc, xs = codes[c]
+                xwp = t1p.tile([P, 4, F], F32, tag="t1", name="xwp%d" % c)
+                for t in range(4):
+                    nc.tensor.matmul_mx(out=xwp[:, t, :], lhsT=xc[:, P * t:P * (t + 1)].bitcast(FP8X4),
+                                        lhsT_scale=xs[:, P * t:P * (t + 1)], rhs=w_c[:].bitcast(FP8X4), rhs_scale=w_s[:],
+                                        start=True, stop=True)
+                sums_x[c] = xwp
 
-        degrees(0, 0, BLK)
-        start_group(0, 2)
-        start_group(1, 2)
-        emit(0, 0, own(0, 0))
+            def collect(c):
+                dst = xw_g[c // 4][:].rearrange("p (c f t) -> p c f t", c=4, t=4)[:, c % 4]
+                nc.scalar.copy(out=dst, in_=sums_x[c][:].rearrange("p t f -> p f t"))
+                if c % 4 == 3:
+                    hh = c // 4
+                    nc.vector.quantize_mx(out=xw_c[:, BLK * hh:BLK * (hh + 1)].bitcast(FP8X4), scales=xw_s[:, BLK * hh:BLK * (hh + 1)], in_=xw_g[hh][:])
+
+            for i in range(NBLK + 3):
+                if i == 3:
+                    diagonal(0)
+                if i < NBLK:
+                    regroup(i)
+                if 1 <= i < NBLK + 1:
+                    codes[i - 1] = quantise(codes[i - 1])
+                if 2 <= i < NBLK + 2:
+                    times_w(i - 2)
+                if i >= 3:
+                    collect(i - 3)
+                if 2 <= i < NBLK + 2:
+                    count(1, 1, i - 2)
+                if i == NBLK + 1:
+                    root(1, 1)
+                    degrees_done(1, 1)
+
+        parts = [load(0, c, True) for c in range(NBLK)]
+        for part in parts:
+            part(0)
+        w_raw = const.tile([P, 4, F], BF16)
+        nc.sync.dma_start(out=w_raw[:].rearrange("q (u e) f -> q u e f", u=2), in_=w.rearrange("(u q e) f -> q u e f", u=2, e=2))
+        b_raw = const.tile([P, 1], BF16)
+        nc.sync.dma_start(out=b_raw[:], in_=b.rearrange("(p o) -> p o", o=1))
+        xunits = []
+        for g in range(4):
+            xu = units.tile([P, 8, D], BF16, tag="unit", name="xu%d" % g)
+            nc.sync.dma_start(out=xu[:], in_=x[1024 * g:1024 * (g + 1), :].rearrange("(r p) d -> p r d", p=P))
+            xunits.append(xu)
+        for part in parts:
+            part(1)
+        parts = [load(1, c, True) for c in range(NBLK)]
+        for h in range(2):
+            for part in parts:
+                part(h)
+
+        degrees(0)
         features()
-        degrees(0, BLK, BLK)
-        degrees(1, 0, BLK)
-        for bb, cc in ((1, 0), (0, 1), (1, 1)):
-            emit(bb, cc, own(bb, cc))
-        flush()
+        tick()
 
-        degrees(1, BLK, BLK)
-        start_group(2, 4)
-        emit(2, 2, own(2, 2))
-        flush()
-        start_group(3, 4)
-        for a in range(2):
-            start_group(a, 2)
-            for n in (2, 3):
-                for B, c, pair, last in pairs(a, [n], False):
-                    multiply(B, c, pair, last)
-        for bb, cc in ((3, 2), (2, 3), (3, 3)):
-            multiply(bb, cc, own(bb, cc), False)
+        def counts(b0, nb, rows):
+            def go():
+                for c in rows:
+                    count(b0, nb, c)
+            return go
 
-        def diagonal(J):
-            start_group(2 * J, 2 * J + 2)
-            start_group(2 * J + 1, 2 * J + 2)
-            for bb, cc in ((2 * J, 2 * J), (2 * J + 1, 2 * J), (2 * J, 2 * J + 1), (2 * J + 1, 2 * J + 1)):
-                multiply(bb, cc, own(bb, cc), False)
+        def nothing():
+            return None
 
-        def mirror(J, rows):
-            for a in rows:
-                start_group(a, 2)
-                for B, c, pair, last in pairs(a, [2 * J, 2 * J + 1], J == 3):
-                    multiply(B, c, pair, J == 3)
+        for J in (2, 3):
+            for c in range(NBLK):
+                load(J, c, False)
 
-        degrees(2, 0, PANEL)
-        diagonal(2)
-        degrees(3, 0, PANEL, (6, lambda: mirror(2, (0, 1))))
-        mirror(2, (2, 3))
-        for I in range(2):
-            for c in (6, 7):
-                load(I, c, 0, PANEL, True)
-        diagonal(3)
-        mirror(3, range(6))
+        def reload(J, rows):
+            def go():
+                for c in rows:
+                    load(J, c, False)
+            return go
+
+        run([(1, (1,)), (0, (1,)),
+             (2, (2,)), (0, (2,)), (1, (2,)),
+             (3, (3,)), (0, (3,)), (1, (3,)), (2, (3,)),
+             (4, (4,)), (5, (5,)), (4, (5,))] + [(a, (4, 5)) for a in range(4)]
+            + [(6, (6,)), (7, (7,)), (6, (7,))] + [(a, (6, 7)) for a in (4, 5, 0, 1, 2, 3)],
+            {(1, (1,)): [counts(2, 1, (0, 1, 2, 3))],
+             (0, (1,)): [counts(2, 1, (4, 5)), counts(2, 1, (6, 7)), lambda: root(2, 1), lambda: degrees_done(2, 1)],
+             (2, (2,)): [counts(3, 1, (0, 1))],
+             (0, (2,)): [counts(3, 1, (2, 3, 4)), counts(3, 1, (5, 6, 7)), lambda: root(3, 1)],
+             (1, (2,)): [lambda: degrees_done(3, 1)],
+             (0, (3,)): [counts(4, 2, (0,)), counts(4, 2, (1,)), counts(4, 2, (2,))],
+             (1, (3,)): [counts(4, 2, (3,)), counts(4, 2, (4,)), counts(4, 2, (5,))],
+             (2, (3,)): [counts(4, 2, (6,)), counts(4, 2, (7,)), lambda: root(4, 2), lambda: degrees_done(4, 2)],
+             (4, (4,)): [reload(1, (4, 5))],
+             (5, (5,)): [reload(0, (6, 7))],
+             (4, (5,)): [counts(6, 2, (0,)), nothing, counts(6, 2, (1,)), reload(1, (6, 7))],
+             (0, (4, 5)): [nothing, counts(6, 2, (2,)), counts(6, 2, (3,)), nothing, counts(6, 2, (4,)), counts(6, 2, (5,))],
+             (1, (4, 5)): [counts(6, 2, (6,)), nothing, counts(6, 2, (7,)), nothing, lambda: root(6, 2)],
+             (2, (4, 5)): [lambda: degrees_done(6, 2)]})
+        for q in range(12):
+            tick()

@@ -19,11 +19,11 @@ F = 128
 PANEL = 1024
 BLK = 512
 NBLK = N // BLK
-UNIT_BUFS = 17
+UNIT_BUFS = 27
+RAW_BUFS = 7
 AG_BUFS = 5
 COD_BUFS = 6
-LAG = 6
-LAG_D = 4
+LAG = 5
 TINY = 1e-30
 
 FLOPS = 2 * N * D * F + 2 * N * N * F
@@ -34,6 +34,7 @@ def tile_simplegcn_pa_t_kernel(tc, x, adjacency, w, b, out):
     with ExitStack() as ctx:
         const = ctx.enter_context(tc.tile_pool(name="const", bufs=1))
         units = ctx.enter_context(tc.tile_pool(name="units", bufs=UNIT_BUFS))
+        raws = ctx.enter_context(tc.tile_pool(name="raws", bufs=RAW_BUFS))
         grp = ctx.enter_context(tc.tile_pool(name="grp", bufs=AG_BUFS))
         rpool = ctx.enter_context(tc.tile_pool(name="rpool", bufs=2))
         plain = ctx.enter_context(tc.tile_pool(name="plain", bufs=3))
@@ -76,22 +77,15 @@ def tile_simplegcn_pa_t_kernel(tc, x, adjacency, w, b, out):
                     item[1]()
 
         unit = {}
-        loops = {}
 
-        def load(J, c, halves):
-            tile = units.tile([P, 4, PANEL], BF16, tag="unit", name="u%d_%d_%d" % (J, c, len(unit)))
-            rows = adjacency[BLK * c:BLK * (c + 1), PANEL * J:PANEL * (J + 1)].rearrange("(t p) w -> p t w", p=P)
-            if halves:
-                two = tile[:].rearrange("p t w -> p (t w)").rearrange("p (h t w) -> p h t w", h=2, t=4)
-                for h in range(2):
-                    unit[(2 * J + h, c)] = two[:, h]
-                    loops[(2 * J + h, c)] = two[:, h].rearrange("p t (n k) -> p (t n) k", k=P)[:, 0:16:5, :]
-                return lambda h: nc.sync.dma_start(out=two[:, h], in_=rows[:, :, BLK * h:BLK * (h + 1)])
-            for h in range(2):
-                unit[(2 * J + h, c)] = tile[:, :, BLK * h:BLK * (h + 1)]
-                loops[(2 * J + h, c)] = tile[:].rearrange("p t (n k) -> p (t n) k", k=P)[:, 4 * h:4 * h + 28:9, :]
-            nc.sync.dma_start(out=tile[:], in_=rows)
-            return None
+        def rows_of(c, col0, width, u):
+            return adjacency[BLK * c + 256 * u:BLK * c + 256 * (u + 1), col0:col0 + width].rearrange("(p e) w -> p e w", e=2)
+
+        def load(b, c):
+            tile = units.tile([P, 4, BLK], BF16, tag="unit", align_bytes=64, name="u%d_%d_%d" % (b, c, len(unit)))
+            unit[(b, c)] = tile[:]
+            for u in range(2):
+                nc.sync.dma_start(out=tile[:, 2 * u:2 * u + 2, :], in_=rows_of(c, BLK * b, BLK, u))
 
         cs = {}
 
@@ -100,9 +94,9 @@ def tile_simplegcn_pa_t_kernel(tc, x, adjacency, w, b, out):
                 cs[b0] = csp.tile([P, 4 * nb, NBLK], F32, tag="cs", name="cs%d" % b0)
             for m in range(4 * nb):
                 u = unit[(b0 + m // 4, c)]
-                s = P * (m % 4)
+                s = 256 * (m % 4 // 2) + m % 2
                 for t in range(4):
-                    nc.tensor.matmul(out=cs[b0][:, m, c:c + 1], lhsT=u[:, t, s:s + P], rhs=ones[:, 0:1], start=(t == 0), stop=(t == 3))
+                    nc.tensor.matmul(out=cs[b0][:, m, c:c + 1], lhsT=u[:, t, s:s + 255:2], rhs=ones[:, 0:1], start=(t == 0), stop=(t == 3))
 
         deg = {}
         sq = {}
@@ -115,15 +109,20 @@ def tile_simplegcn_pa_t_kernel(tc, x, adjacency, w, b, out):
             sq[b0] = small.tile([P, 4 * nb], F32, tag="sq", name="sq%d" % b0)
             nc.scalar.activation(out=sq[b0][:], in_=dcl[:], func=ACT.Sqrt)
 
+        ready = [0]
+
         def spread(b0, nb):
             rc = small.tile([P, 4 * nb], F32, tag="rc")
             nc.vector.reciprocal(out=rc[:], in_=sq[b0][:])
             nc.vector.scalar_tensor_tensor(out=dinv[:, 4 * b0:4 * (b0 + nb)], in0=deg[b0][:], scalar=-1.0, in1=rc[:], op0=ALU.is_gt, op1=ALU.mult)
             for n in range(b0, b0 + nb):
-                vps = t2p.tile([P, BLK], F32, tag="t2", name="vps%d" % n)
+                vps = t2p.tile([P, 4, P], F32, tag="t2", name="vps%d" % n)
                 for m in range(4):
-                    nc.tensor.transpose(out=vps[:, P * m:P * (m + 1)], in_=dinv[:, 4 * n + m:4 * n + m + 1].to_broadcast([P, P]), identity=ident_f[:])
-                nc.scalar.copy(out=vb[:, BLK * (n % 4):BLK * (n % 4 + 1)], in_=vps[:])
+                    nc.tensor.transpose(out=vps[:, m, :], in_=dinv[:, 4 * n + m:4 * n + m + 1].to_broadcast([P, P]), identity=ident_f[:])
+                nc.scalar.copy(out=vb[:, BLK * (n % 4):BLK * (n % 4 + 1)].rearrange("p (u k e) -> p u k e", u=2, e=2),
+                               in_=vps[:].rearrange("p (u e) k -> p u k e", u=2))
+                self_loops(n)
+            ready[0] = b0 + nb
 
         acc = {}
         sums = {}
@@ -182,6 +181,16 @@ def tile_simplegcn_pa_t_kernel(tc, x, adjacency, w, b, out):
         def group_tile(B, c):
             return grp.tile([P, 4 * BLK], BF16, tag="ag", align_bytes=64, name="ag%d_%d" % (B, c))
 
+        raw = {}
+
+        def regroup_early(B, c, engine):
+            t = raws.tile([P, 4 * BLK], BF16, tag="raw", align_bytes=64, name="raw%d_%d" % (B, c))
+            if engine == 0:
+                nc.vector.tensor_copy(out=grouped(t[:]), in_=columns(unit[(B, c)]))
+            else:
+                nc.scalar.copy(out=grouped(t[:]), in_=columns(unit[(B, c)]))
+            raw[(B, c)] = t
+
         tables = {}
 
         def table(job):
@@ -191,19 +200,19 @@ def tile_simplegcn_pa_t_kernel(tc, x, adjacency, w, b, out):
             col0 = BLK * (cols[0] % 4)
             width = BLK * len(cols)
             for k in range(4):
-                dv = dinv[:, 4 * a + k:4 * a + k + 1]
-                nc.scalar.activation(out=rt[:, k, 0:width], in_=vb[:, col0:col0 + width], func=ACT.Copy, scale=dv)
+                nc.scalar.activation(out=rt[:, k, 0:width], in_=vb[:, col0:col0 + width], func=ACT.Copy, scale=dinv[:, 4 * a + k:4 * a + k + 1])
 
         turned = {}
 
         def turn(half):
             job, n, h = half
             rt = tables[job]
-            tp = t1p.tile([P, 4, 256], BF16, tag="t1", name="tp%d_%d_%d" % (job[0], job[1][n], h))
-            for t in range(4):
-                for m in range(2):
-                    s = BLK * n + P * t
-                    nc.tensor.transpose(out=tp[:, t, P * m:P * (m + 1)], in_=rt[:, 2 * h + m, s:s + P], identity=ident_b[:])
+            tp = t1p.tile([P, BLK], F32, tag="t1", name="tp%d_%d_%d" % (job[0], job[1][n], h))
+            dst = tp[:].rearrange("p (q e u) -> p e u q", e=2, u=2)
+            for e in range(2):
+                words = rt[:, 2 * h + e, BLK * n:BLK * (n + 1)].bitcast(F32)
+                for u in range(2):
+                    nc.tensor.transpose(out=dst[:, e, u, :], in_=words[:, P * u:P * (u + 1)], identity=ident_f[:])
             turned[half] = tp
 
         ag_m = {}
@@ -212,12 +221,19 @@ def tile_simplegcn_pa_t_kernel(tc, x, adjacency, w, b, out):
             job, n, h = half
             a, cols = job
             c = cols[n]
+            products = turned[half][:].bitcast(BF16)
+            if (a, c) in raw:
+                ag = raw[(a, c)]
+                part = ag[:, PANEL * h:PANEL * (h + 1)]
+                nc.vector.tensor_tensor(out=part, in0=part, in1=products, op=ALU.mult)
+                if h == 1:
+                    after(2, lambda: finish(a, c, ag))
+                return
             if h == 0:
                 ag_m[(a, c)] = group_tile(a, c)
             ag = ag_m[(a, c)]
-            u = unit[(a, c)][:, :, 256 * h:256 * (h + 1)]
-            dst = grouped(ag[:, PANEL * h:PANEL * (h + 1)])
-            nc.vector.tensor_tensor(out=dst, in0=columns(u), in1=columns(turned[half][:]), op=ALU.mult)
+            nc.vector.tensor_tensor(out=grouped(ag[:, PANEL * h:PANEL * (h + 1)]), in0=columns(unit[(a, c)][:, :, 256 * h:256 * (h + 1)]),
+                                    in1=grouped(products), op=ALU.mult)
             if h == 1:
                 after(2, lambda: finish(a, c, ag))
 
@@ -226,28 +242,28 @@ def tile_simplegcn_pa_t_kernel(tc, x, adjacency, w, b, out):
         def straight(job, n):
             a, cols = job
             B = cols[n]
-            pl = plain.tile([P, 4, BLK], BF16, tag="pl", name="pl%d_%d" % (B, a))
-            planes[(B, a)] = pl
+            pl = plain.tile([P, 4, BLK], BF16, tag="pl", align_bytes=64, name="pl%d_%d" % (B, a))
             nc.vector.tensor_tensor(out=pl[:], in0=unit[(B, a)], in1=tables[job][:, :, BLK * n:BLK * (n + 1)], op=ALU.mult)
-
-        def interleave(job, n, steps):
-            a, cols = job
-            B = cols[n]
             ag = group_tile(B, a)
-            nc.scalar.copy(out=grouped(ag[:]), in_=columns(planes[(B, a)][:]))
-            after(steps, lambda: finish(B, a, ag))
+            nc.scalar.copy(out=grouped(ag[:]), in_=columns(pl[:]))
+            after(LAG, lambda: finish(B, a, ag))
+
+        def self_loops(a):
+            for k in range(4):
+                s = 256 * (k // 2) + k % 2
+                d = unit[(a, a)][:, k, s:s + 255:2]
+                nc.gpsimd.tensor_tensor(out=d, in0=d, in1=ident_b[:], op=ALU.add)
 
         def diagonal(a):
             u = unit[(a, a)]
-            nc.gpsimd.tensor_tensor(out=loops[(a, a)], in0=loops[(a, a)], in1=ident_b[:].unsqueeze(1).to_broadcast([P, 4, P]), op=ALU.add)
-            pl = plain.tile([P, 4, BLK], BF16, tag="pl", name="pl%d_%d" % (a, a))
+            pl = plain.tile([P, 4, BLK], BF16, tag="pl", align_bytes=64, name="pl%d_%d" % (a, a))
             v0 = BLK * (a % 4)
             for t in range(4):
                 nc.vector.scalar_tensor_tensor(out=pl[:, t, :], in0=u[:, t, :], scalar=dinv[:, 4 * a + t:4 * a + t + 1],
                                                in1=vb[:, v0:v0 + BLK], op0=ALU.mult, op1=ALU.mult)
             ag = group_tile(a, a)
             nc.scalar.copy(out=grouped(ag[:]), in_=columns(pl[:]))
-            after(LAG_D, lambda: finish(a, a, ag))
+            after(LAG, lambda: finish(a, a, ag))
 
         def halves(job):
             a, cols = job
@@ -259,8 +275,8 @@ def tile_simplegcn_pa_t_kernel(tc, x, adjacency, w, b, out):
                 queue.extend(halves(job))
             turns = [0]
 
-            def turn_next(hs):
-                if turns[0] < len(queue) and queue[turns[0]] in hs:
+            def turn_next():
+                if turns[0] < len(queue) and queue[turns[0]][0] in tables:
                     turn(queue[turns[0]])
                     turns[0] += 1
 
@@ -268,11 +284,11 @@ def tile_simplegcn_pa_t_kernel(tc, x, adjacency, w, b, out):
                 job = jobs[i]
                 a, cols = job
                 extra = list(fill.get(job, []))
-                nxt = jobs[i + 1] if i + 1 < len(jobs) else None
 
                 def early():
-                    if nxt is not None and nxt[1] != (nxt[0],) and nxt not in tables and BLK * nxt[1][-1] < ready[0]:
-                        table(nxt)
+                    for nxt in jobs[i:i + 2]:
+                        if nxt[1] != (nxt[0],) and nxt not in tables and nxt[1][-1] < ready[0]:
+                            table(nxt)
 
                 def done():
                     tick()
@@ -288,39 +304,22 @@ def tile_simplegcn_pa_t_kernel(tc, x, adjacency, w, b, out):
                     done()
                 else:
                     hs = halves(job)
-                    turn_next(hs[0:2])
-                    turn_next(hs[0:2])
-                    straight(job, 0)
-                    interleave(job, 0, LAG)
-                    done()
-                    mirrored(hs[0])
-                    turn_next(hs)
-                    done()
-                    if len(cols) == 2:
-                        straight(job, 1)
-                        interleave(job, 1, LAG)
-                        done()
-                    for q in range(1, len(hs)):
-                        mirrored(hs[q])
-                        turn_next(hs)
+                    while_turned = [half in turned for half in hs[0:2]]
+                    for known in while_turned:
+                        if not known:
+                            turn_next()
+                    for n in range(len(cols)):
+                        for h in range(2):
+                            mirrored(hs[2 * n + h])
+                            turn_next()
+                            done()
+                        straight(job, n)
                         done()
                 for e in list(extra):
                     e()
                     early()
 
-        ready = [0]
-
-        def degrees_done(b0, nb):
-            spread(b0, nb)
-            ready[0] = BLK * (b0 + nb)
-
-        def degrees(b):
-            for c in range(NBLK):
-                count(b, 1, c)
-            root(b, 1)
-            degrees_done(b, 1)
-
-        def features():
+        def features(fill):
             w_g = const.tile([P, F, 4], BF16, align_bytes=64)
             nc.vector.tensor_copy(out=w_g[:], in_=w_raw[:].rearrange("q t f -> q f t"))
             w_c = const.tile([P, F], U32, align_bytes=64)
@@ -329,15 +328,15 @@ def tile_simplegcn_pa_t_kernel(tc, x, adjacency, w, b, out):
             nc.vector.tensor_copy(out=b_f[:], in_=b_raw[:])
             xw_g = [grp.tile([P, 4 * BLK], BF16, tag="ag", align_bytes=64, name="xw%d" % hh) for hh in range(2)]
             codes = {}
-            sums_x = {}
+            products = {}
 
             def regroup(c):
-                xg = grp.tile([P, 4 * BLK], BF16, tag="ag", align_bytes=64, name="xg%d" % c)
+                xg = plain.tile([P, 4 * BLK], BF16, tag="pl", align_bytes=64, name="xg%d" % c)
                 xg32 = xg[:].bitcast(F32).rearrange("p (r i u) -> p r i u", r=4, u=2)
                 for k in range(2):
                     tp = accp.tile([P, 2, 2, P], F32, tag="acc", name="xt%d_%d" % (c, k))
                     for e in range(2):
-                        xr = xunits[c // 2][:, 4 * (c % 2) + 2 * k + e, :].bitcast(F32)
+                        xr = xunits[c][:, k, e, :].bitcast(F32)
                         for u2 in range(2):
                             nc.tensor.transpose(out=tp[:, e, u2, :], in_=xr[:, P * u2:P * (u2 + 1)], identity=ident_f[:])
                     if k == 0:
@@ -353,18 +352,16 @@ def tile_simplegcn_pa_t_kernel(tc, x, adjacency, w, b, out):
                     nc.tensor.matmul_mx(out=xwp[:, t, :], lhsT=xc[:, P * t:P * (t + 1)].bitcast(FP8X4),
                                         lhsT_scale=xs[:, P * t:P * (t + 1)], rhs=w_c[:].bitcast(FP8X4), rhs_scale=w_s[:],
                                         start=True, stop=True)
-                sums_x[c] = xwp
+                products[c] = xwp
 
             def collect(c):
                 dst = xw_g[c // 4][:].rearrange("p (c f t) -> p c f t", c=4, t=4)[:, c % 4]
-                nc.scalar.copy(out=dst, in_=sums_x[c][:].rearrange("p t f -> p f t"))
+                nc.scalar.copy(out=dst, in_=products[c][:].rearrange("p t f -> p f t"))
                 if c % 4 == 3:
                     hh = c // 4
                     nc.vector.quantize_mx(out=xw_c[:, BLK * hh:BLK * (hh + 1)].bitcast(FP8X4), scales=xw_s[:, BLK * hh:BLK * (hh + 1)], in_=xw_g[hh][:])
 
             for i in range(NBLK + 3):
-                if i == 3:
-                    diagonal(0)
                 if i < NBLK:
                     regroup(i)
                 if 1 <= i < NBLK + 1:
@@ -373,34 +370,31 @@ def tile_simplegcn_pa_t_kernel(tc, x, adjacency, w, b, out):
                     times_w(i - 2)
                 if i >= 3:
                     collect(i - 3)
-                if 2 <= i < NBLK + 2:
-                    count(1, 1, i - 2)
-                if i == NBLK + 1:
-                    root(1, 1)
-                    degrees_done(1, 1)
+                for e in fill.get(i, ()):
+                    e()
 
-        parts = [load(0, c, True) for c in range(NBLK)]
-        for part in parts:
-            part(0)
+        for c in range(NBLK):
+            load(0, c)
         w_raw = const.tile([P, 4, F], BF16)
         nc.sync.dma_start(out=w_raw[:].rearrange("q (u e) f -> q u e f", u=2), in_=w.rearrange("(u q e) f -> q u e f", u=2, e=2))
         b_raw = const.tile([P, 1], BF16)
         nc.sync.dma_start(out=b_raw[:], in_=b.rearrange("(p o) -> p o", o=1))
         xunits = []
-        for g in range(4):
-            xu = units.tile([P, 8, D], BF16, tag="unit", name="xu%d" % g)
-            nc.sync.dma_start(out=xu[:], in_=x[1024 * g:1024 * (g + 1), :].rearrange("(r p) d -> p r d", p=P))
+        for g in range(NBLK):
+            xu = units.tile([P, 2, 2, D], BF16, tag="unit", align_bytes=64, name="xu%d" % g)
+            nc.sync.dma_start(out=xu[:].rearrange("p r e d -> p r (e d)"),
+                              in_=x[BLK * g:BLK * (g + 1), :].rearrange("(r p e) d -> p r (e d)", p=P, e=2))
             xunits.append(xu)
-        for part in parts:
-            part(1)
-        parts = [load(1, c, True) for c in range(NBLK)]
-        for h in range(2):
-            for part in parts:
-                part(h)
+        for b1 in range(1, 4):
+            for c in range(NBLK):
+                load(b1, c)
+        for b1 in (4, 6):
+            for c in range(NBLK):
+                load(b1, c)
+                load(b1 + 1, c)
 
-        degrees(0)
-        features()
-        tick()
+        def call(f, *args):
+            return lambda: f(*args)
 
         def counts(b0, nb, rows):
             def go():
@@ -408,37 +402,47 @@ def tile_simplegcn_pa_t_kernel(tc, x, adjacency, w, b, out):
                     count(b0, nb, c)
             return go
 
-        def nothing():
-            return None
-
-        for J in (2, 3):
-            for c in range(NBLK):
-                load(J, c, False)
-
         def reload(J, rows):
             def go():
                 for c in rows:
-                    load(J, c, False)
+                    for b in (2 * J, 2 * J + 1):
+                        if (b, c) not in raw:
+                            load(b, c)
             return go
 
+        def nothing():
+            return None
+
+        for c in range(NBLK):
+            count(0, 1, c)
+            if c > 0:
+                regroup_early(0, c, 1 if c % 3 == 0 else 0)
+        root(0, 1)
+        spread(0, 1)
+        features({2: [call(diagonal, 0)],
+                  3: [counts(1, 1, (0, 1))],
+                  4: [counts(1, 1, (2, 3))],
+                  5: [counts(1, 1, (4, 5))],
+                  6: [counts(1, 1, (6, 7)), call(root, 1, 1), call(spread, 1, 1)]})
+        tick()
         run([(1, (1,)), (0, (1,)),
              (2, (2,)), (0, (2,)), (1, (2,)),
              (3, (3,)), (0, (3,)), (1, (3,)), (2, (3,)),
              (4, (4,)), (5, (5,)), (4, (5,))] + [(a, (4, 5)) for a in range(4)]
             + [(6, (6,)), (7, (7,)), (6, (7,))] + [(a, (6, 7)) for a in (4, 5, 0, 1, 2, 3)],
             {(1, (1,)): [counts(2, 1, (0, 1, 2, 3))],
-             (0, (1,)): [counts(2, 1, (4, 5)), counts(2, 1, (6, 7)), lambda: root(2, 1), lambda: degrees_done(2, 1)],
+             (0, (1,)): [counts(2, 1, (4, 5)), counts(2, 1, (6, 7)), call(root, 2, 1), call(spread, 2, 1)],
              (2, (2,)): [counts(3, 1, (0, 1))],
-             (0, (2,)): [counts(3, 1, (2, 3, 4)), counts(3, 1, (5, 6, 7)), lambda: root(3, 1)],
-             (1, (2,)): [lambda: degrees_done(3, 1)],
+             (0, (2,)): [counts(3, 1, (2, 3, 4)), counts(3, 1, (5, 6, 7)), call(root, 3, 1)],
+             (1, (2,)): [call(spread, 3, 1)],
              (0, (3,)): [counts(4, 2, (0,)), counts(4, 2, (1,)), counts(4, 2, (2,))],
              (1, (3,)): [counts(4, 2, (3,)), counts(4, 2, (4,)), counts(4, 2, (5,))],
-             (2, (3,)): [counts(4, 2, (6,)), counts(4, 2, (7,)), lambda: root(4, 2), lambda: degrees_done(4, 2)],
+             (2, (3,)): [counts(4, 2, (6,)), counts(4, 2, (7,)), call(root, 4, 2), call(spread, 4, 2)],
              (4, (4,)): [reload(1, (4, 5))],
              (5, (5,)): [reload(0, (6, 7))],
              (4, (5,)): [counts(6, 2, (0,)), nothing, counts(6, 2, (1,)), reload(1, (6, 7))],
              (0, (4, 5)): [nothing, counts(6, 2, (2,)), counts(6, 2, (3,)), nothing, counts(6, 2, (4,)), counts(6, 2, (5,))],
-             (1, (4, 5)): [counts(6, 2, (6,)), nothing, counts(6, 2, (7,)), nothing, lambda: root(6, 2)],
-             (2, (4, 5)): [lambda: degrees_done(6, 2)]})
+             (1, (4, 5)): [counts(6, 2, (6,)), nothing, counts(6, 2, (7,)), nothing, call(root, 6, 2)],
+             (2, (4, 5)): [call(spread, 6, 2)]})
         for q in range(12):
             tick()

@@ -78,14 +78,12 @@ def tile_simplegcn_pa_t_kernel(tc, x, adjacency, w, b, out):
 
         unit = {}
 
-        def rows_of(c, col0, width, u):
-            return adjacency[BLK * c + 256 * u:BLK * c + 256 * (u + 1), col0:col0 + width].rearrange("(p e) w -> p e w", e=2)
-
         def load(b, c):
             tile = units.tile([P, 4, BLK], BF16, tag="unit", align_bytes=64, name="u%d_%d_%d" % (b, c, len(unit)))
             unit[(b, c)] = tile[:]
             for u in range(2):
-                nc.sync.dma_start(out=tile[:, 2 * u:2 * u + 2, :], in_=rows_of(c, BLK * b, BLK, u))
+                nc.sync.dma_start(out=tile[:, 2 * u:2 * u + 2, :],
+                                  in_=adjacency[BLK * c + 256 * u:BLK * c + 256 * (u + 1), BLK * b:BLK * (b + 1)].rearrange("(p e) w -> p e w", e=2))
 
         cs = {}
 
@@ -121,7 +119,6 @@ def tile_simplegcn_pa_t_kernel(tc, x, adjacency, w, b, out):
                     nc.tensor.transpose(out=vps[:, m, :], in_=dinv[:, 4 * n + m:4 * n + m + 1].to_broadcast([P, P]), identity=ident_f[:])
                 nc.scalar.copy(out=vb[:, BLK * (n % 4):BLK * (n % 4 + 1)].rearrange("p (u k e) -> p u k e", u=2, e=2),
                                in_=vps[:].rearrange("p (u e) k -> p u k e", u=2))
-                self_loops(n)
             ready[0] = b0 + nb
 
         acc = {}
@@ -248,14 +245,14 @@ def tile_simplegcn_pa_t_kernel(tc, x, adjacency, w, b, out):
             nc.scalar.copy(out=grouped(ag[:]), in_=columns(pl[:]))
             after(LAG, lambda: finish(B, a, ag))
 
-        def self_loops(a):
-            for k in range(4):
-                s = 256 * (k // 2) + k % 2
-                d = unit[(a, a)][:, k, s:s + 255:2]
-                nc.gpsimd.tensor_tensor(out=d, in0=d, in1=ident_b[:], op=ALU.add)
-
         def diagonal(a):
             u = unit[(a, a)]
+            flat = u.rearrange("p t n -> p (t n)")
+            for s in (0, 2 * BLK - 2):
+                d = flat[:, s:s + 2 * BLK + 2].rearrange("p (e k) -> p e k", e=2)
+                k0 = 0 if s == 0 else 258
+                d = d[:, :, k0:k0 + 255:2]
+                nc.vector.tensor_tensor(out=d, in0=d, in1=ident_b[:].unsqueeze(1).to_broadcast([P, 2, P]), op=ALU.add)
             pl = plain.tile([P, 4, BLK], BF16, tag="pl", align_bytes=64, name="pl%d_%d" % (a, a))
             v0 = BLK * (a % 4)
             for t in range(4):

@@ -19,11 +19,11 @@ F = 128
 PANEL = 1024
 BLK = 512
 NBLK = N // BLK
-UNIT_BUFS = 27
+UNIT_BUFS = 24
 RAW_BUFS = 7
-AG_BUFS = 5
+AG_BUFS = 8
 COD_BUFS = 6
-LAG = 5
+LAG = 8
 TINY = 1e-30
 
 FLOPS = 2 * N * D * F + 2 * N * N * F
@@ -88,7 +88,7 @@ def tile_simplegcn_pa_t_kernel(tc, x, adjacency, w, b, out):
         cs = {}
 
         def count(b0, nb, c):
-            if c == 0:
+            if b0 not in cs:
                 cs[b0] = csp.tile([P, 4 * nb, NBLK], F32, tag="cs", name="cs%d" % b0)
             for m in range(4 * nb):
                 u = unit[(b0 + m // 4, c)]
@@ -180,13 +180,15 @@ def tile_simplegcn_pa_t_kernel(tc, x, adjacency, w, b, out):
 
         raw = {}
 
-        def regroup_early(B, c, engine):
-            t = raws.tile([P, 4 * BLK], BF16, tag="raw", align_bytes=64, name="raw%d_%d" % (B, c))
+        def regroup(B, c, t, engine):
             if engine == 0:
                 nc.vector.tensor_copy(out=grouped(t[:]), in_=columns(unit[(B, c)]))
             else:
                 nc.scalar.copy(out=grouped(t[:]), in_=columns(unit[(B, c)]))
             raw[(B, c)] = t
+
+        def regroup_early(B, c, engine):
+            regroup(B, c, raws.tile([P, 4 * BLK], BF16, tag="raw", align_bytes=64, name="raw%d_%d" % (B, c)), engine)
 
         tables = {}
 
@@ -212,25 +214,14 @@ def tile_simplegcn_pa_t_kernel(tc, x, adjacency, w, b, out):
                     nc.tensor.transpose(out=dst[:, e, u, :], in_=words[:, P * u:P * (u + 1)], identity=ident_f[:])
             turned[half] = tp
 
-        ag_m = {}
-
         def mirrored(half):
             job, n, h = half
             a, cols = job
             c = cols[n]
             products = turned[half][:].bitcast(BF16)
-            if (a, c) in raw:
-                ag = raw[(a, c)]
-                part = ag[:, PANEL * h:PANEL * (h + 1)]
-                nc.vector.tensor_tensor(out=part, in0=part, in1=products, op=ALU.mult)
-                if h == 1:
-                    after(2, lambda: finish(a, c, ag))
-                return
-            if h == 0:
-                ag_m[(a, c)] = group_tile(a, c)
-            ag = ag_m[(a, c)]
-            nc.vector.tensor_tensor(out=grouped(ag[:, PANEL * h:PANEL * (h + 1)]), in0=columns(unit[(a, c)][:, :, 256 * h:256 * (h + 1)]),
-                                    in1=grouped(products), op=ALU.mult)
+            ag = raw[(a, c)]
+            part = ag[:, PANEL * h:PANEL * (h + 1)]
+            nc.vector.tensor_tensor(out=part, in0=part, in1=products, op=ALU.mult)
             if h == 1:
                 after(2, lambda: finish(a, c, ag))
 
@@ -301,6 +292,9 @@ def tile_simplegcn_pa_t_kernel(tc, x, adjacency, w, b, out):
                     done()
                 else:
                     hs = halves(job)
+                    for n in range(len(cols)):
+                        if (a, cols[n]) not in raw:
+                            regroup(a, cols[n], group_tile(a, cols[n]), 0)
                     while_turned = [half in turned for half in hs[0:2]]
                     for known in while_turned:
                         if not known:
@@ -327,7 +321,7 @@ def tile_simplegcn_pa_t_kernel(tc, x, adjacency, w, b, out):
             codes = {}
             products = {}
 
-            def regroup(c):
+            def regroup_x(c):
                 xg = plain.tile([P, 4 * BLK], BF16, tag="pl", align_bytes=64, name="xg%d" % c)
                 xg32 = xg[:].bitcast(F32).rearrange("p (r i u) -> p r i u", r=4, u=2)
                 for k in range(2):
@@ -360,7 +354,7 @@ def tile_simplegcn_pa_t_kernel(tc, x, adjacency, w, b, out):
 
             for i in range(NBLK + 3):
                 if i < NBLK:
-                    regroup(i)
+                    regroup_x(i)
                 if 1 <= i < NBLK + 1:
                     codes[i - 1] = quantise(codes[i - 1])
                 if 2 <= i < NBLK + 2:
@@ -370,7 +364,10 @@ def tile_simplegcn_pa_t_kernel(tc, x, adjacency, w, b, out):
                 for e in fill.get(i, ()):
                     e()
 
-        for c in range(NBLK):
+        def own_first(b):
+            return [b] + [c for c in range(NBLK) if c != b]
+
+        for c in own_first(0):
             load(0, c)
         w_raw = const.tile([P, 4, F], BF16)
         nc.sync.dma_start(out=w_raw[:].rearrange("q (u e) f -> q u e f", u=2), in_=w.rearrange("(u q e) f -> q u e f", u=2, e=2))
@@ -383,20 +380,20 @@ def tile_simplegcn_pa_t_kernel(tc, x, adjacency, w, b, out):
                               in_=x[BLK * g:BLK * (g + 1), :].rearrange("(r p e) d -> p r (e d)", p=P, e=2))
             xunits.append(xu)
         for b1 in range(1, 4):
-            for c in range(NBLK):
+            for c in own_first(b1):
                 load(b1, c)
         for b1 in (4, 6):
-            for c in range(NBLK):
+            for c in own_first(b1):
                 load(b1, c)
                 load(b1 + 1, c)
 
         def call(f, *args):
             return lambda: f(*args)
 
-        def counts(b0, nb, rows):
+        def counts(b0, nb, places):
             def go():
-                for c in rows:
-                    count(b0, nb, c)
+                for q in places:
+                    count(b0, nb, own_first(b0)[q])
             return go
 
         def reload(J, rows):

@@ -19,10 +19,10 @@ F = 128
 PANEL = 1024
 BLK = 512
 NBLK = N // BLK
-UNIT_BUFS = 24
-RAW_BUFS = 7
-AG_BUFS = 8
-COD_BUFS = 6
+UNIT_BUFS = 11
+RAW_BUFS = 13
+AG_BUFS = 5
+COD_BUFS = 5
 LAG = 8
 TINY = 1e-30
 
@@ -78,12 +78,13 @@ def tile_simplegcn_pa_t_kernel(tc, x, adjacency, w, b, out):
 
         unit = {}
 
-        def load(b, c):
-            tile = units.tile([P, 4, BLK], BF16, tag="unit", align_bytes=64, name="u%d_%d_%d" % (b, c, len(unit)))
-            unit[(b, c)] = tile[:]
+        def load(J, c):
+            tile = units.tile([P, 4, PANEL], BF16, tag="unit", name="u%d_%d_%d" % (J, c, len(unit)))
+            for h in range(2):
+                unit[(2 * J + h, c)] = tile[:, :, BLK * h:BLK * (h + 1)]
             for u in range(2):
                 nc.sync.dma_start(out=tile[:, 2 * u:2 * u + 2, :],
-                                  in_=adjacency[BLK * c + 256 * u:BLK * c + 256 * (u + 1), BLK * b:BLK * (b + 1)].rearrange("(p e) w -> p e w", e=2))
+                                  in_=adjacency[BLK * c + 256 * u:BLK * c + 256 * (u + 1), PANEL * J:PANEL * (J + 1)].rearrange("(p e) w -> p e w", e=2))
 
         cs = {}
 
@@ -238,12 +239,10 @@ def tile_simplegcn_pa_t_kernel(tc, x, adjacency, w, b, out):
 
         def diagonal(a):
             u = unit[(a, a)]
-            flat = u.rearrange("p t n -> p (t n)")
-            for s in (0, 2 * BLK - 2):
-                d = flat[:, s:s + 2 * BLK + 2].rearrange("p (e k) -> p e k", e=2)
-                k0 = 0 if s == 0 else 258
-                d = d[:, :, k0:k0 + 255:2]
-                nc.vector.tensor_tensor(out=d, in0=d, in1=ident_b[:].unsqueeze(1).to_broadcast([P, 2, P]), op=ALU.add)
+            for k in range(4):
+                s = 256 * (k // 2) + k % 2
+                d = u[:, k, s:s + 255:2]
+                nc.vector.tensor_tensor(out=d, in0=d, in1=ident_b[:], op=ALU.add)
             pl = plain.tile([P, 4, BLK], BF16, tag="pl", align_bytes=64, name="pl%d_%d" % (a, a))
             v0 = BLK * (a % 4)
             for t in range(4):
@@ -327,7 +326,7 @@ def tile_simplegcn_pa_t_kernel(tc, x, adjacency, w, b, out):
                 for k in range(2):
                     tp = accp.tile([P, 2, 2, P], F32, tag="acc", name="xt%d_%d" % (c, k))
                     for e in range(2):
-                        xr = xunits[c][:, k, e, :].bitcast(F32)
+                        xr = xunits[c // 2][:, 2 * (c % 2) + k, e, :].bitcast(F32)
                         for u2 in range(2):
                             nc.tensor.transpose(out=tp[:, e, u2, :], in_=xr[:, P * u2:P * (u2 + 1)], identity=ident_f[:])
                     if k == 0:
@@ -364,8 +363,8 @@ def tile_simplegcn_pa_t_kernel(tc, x, adjacency, w, b, out):
                 for e in fill.get(i, ()):
                     e()
 
-        def own_first(b):
-            return [b] + [c for c in range(NBLK) if c != b]
+        def own_first(J):
+            return [2 * J, 2 * J + 1] + [c for c in range(NBLK) if c // 2 != J]
 
         for c in own_first(0):
             load(0, c)
@@ -374,69 +373,56 @@ def tile_simplegcn_pa_t_kernel(tc, x, adjacency, w, b, out):
         b_raw = const.tile([P, 1], BF16)
         nc.sync.dma_start(out=b_raw[:], in_=b.rearrange("(p o) -> p o", o=1))
         xunits = []
-        for g in range(NBLK):
-            xu = units.tile([P, 2, 2, D], BF16, tag="unit", align_bytes=64, name="xu%d" % g)
+        for g in range(4):
+            xu = units.tile([P, 4, 2, D], BF16, tag="unit", name="xu%d" % g)
             nc.sync.dma_start(out=xu[:].rearrange("p r e d -> p r (e d)"),
-                              in_=x[BLK * g:BLK * (g + 1), :].rearrange("(r p e) d -> p r (e d)", p=P, e=2))
+                              in_=x[PANEL * g:PANEL * (g + 1), :].rearrange("(r p e) d -> p r (e d)", p=P, e=2))
             xunits.append(xu)
-        for b1 in range(1, 4):
-            for c in own_first(b1):
-                load(b1, c)
-        for b1 in (4, 6):
-            for c in own_first(b1):
-                load(b1, c)
-                load(b1 + 1, c)
+        for J in range(1, 4):
+            for c in own_first(J):
+                load(J, c)
 
         def call(f, *args):
             return lambda: f(*args)
 
-        def counts(b0, nb, places):
+        def counts(J, places):
             def go():
                 for q in places:
-                    count(b0, nb, own_first(b0)[q])
+                    count(2 * J, 2, own_first(J)[q])
             return go
 
         def reload(J, rows):
             def go():
                 for c in rows:
-                    for b in (2 * J, 2 * J + 1):
-                        if (b, c) not in raw:
-                            load(b, c)
+                    load(J, c)
             return go
 
         def nothing():
             return None
 
-        for c in range(NBLK):
-            count(0, 1, c)
-            if c > 0:
-                regroup_early(0, c, 1 if c % 3 == 0 else 0)
-        root(0, 1)
-        spread(0, 1)
-        features({2: [call(diagonal, 0)],
-                  3: [counts(1, 1, (0, 1))],
-                  4: [counts(1, 1, (2, 3))],
-                  5: [counts(1, 1, (4, 5))],
-                  6: [counts(1, 1, (6, 7)), call(root, 1, 1), call(spread, 1, 1)]})
+        for c in own_first(0):
+            count(0, 2, c)
+            for b1 in range(2):
+                if c > b1:
+                    regroup_early(b1, c, 1 if c % 3 == 0 else 0)
+        root(0, 2)
+        spread(0, 2)
+        features({1: [call(diagonal, 0)],
+                  4: [call(diagonal, 1)],
+                  7: [counts(1, (0,))], 8: [counts(1, (1,))], 9: [counts(1, (2,))], 10: [counts(1, (3,))]})
         tick()
-        run([(1, (1,)), (0, (1,)),
-             (2, (2,)), (0, (2,)), (1, (2,)),
-             (3, (3,)), (0, (3,)), (1, (3,)), (2, (3,)),
+        run([(0, (1,)),
+             (2, (2,)), (3, (3,)), (2, (3,)), (0, (2, 3)), (1, (2, 3)),
              (4, (4,)), (5, (5,)), (4, (5,))] + [(a, (4, 5)) for a in range(4)]
             + [(6, (6,)), (7, (7,)), (6, (7,))] + [(a, (6, 7)) for a in (4, 5, 0, 1, 2, 3)],
-            {(1, (1,)): [counts(2, 1, (0, 1, 2, 3))],
-             (0, (1,)): [counts(2, 1, (4, 5)), counts(2, 1, (6, 7)), call(root, 2, 1), call(spread, 2, 1)],
-             (2, (2,)): [counts(3, 1, (0, 1))],
-             (0, (2,)): [counts(3, 1, (2, 3, 4)), counts(3, 1, (5, 6, 7)), call(root, 3, 1)],
-             (1, (2,)): [call(spread, 3, 1)],
-             (0, (3,)): [counts(4, 2, (0,)), counts(4, 2, (1,)), counts(4, 2, (2,))],
-             (1, (3,)): [counts(4, 2, (3,)), counts(4, 2, (4,)), counts(4, 2, (5,))],
-             (2, (3,)): [counts(4, 2, (6,)), counts(4, 2, (7,)), call(root, 4, 2), call(spread, 4, 2)],
+            {(0, (1,)): [counts(1, (4, 5)), counts(1, (6, 7)), call(root, 2, 2), call(spread, 2, 2)],
+             (2, (3,)): [counts(2, (0,)), counts(2, (1,)), counts(2, (2,))],
+             (0, (2, 3)): [counts(2, (3,)), nothing, counts(2, (4,)), nothing, counts(2, (5,))],
+             (1, (2, 3)): [counts(2, (6,)), nothing, counts(2, (7,)), call(root, 4, 2), nothing, call(spread, 4, 2)],
              (4, (4,)): [reload(1, (4, 5))],
-             (5, (5,)): [reload(0, (6, 7))],
-             (4, (5,)): [counts(6, 2, (0,)), nothing, counts(6, 2, (1,)), reload(1, (6, 7))],
-             (0, (4, 5)): [nothing, counts(6, 2, (2,)), counts(6, 2, (3,)), nothing, counts(6, 2, (4,)), counts(6, 2, (5,))],
-             (1, (4, 5)): [counts(6, 2, (6,)), nothing, counts(6, 2, (7,)), nothing, call(root, 6, 2)],
-             (2, (4, 5)): [call(spread, 6, 2)]})
+             (4, (5,)): [counts(3, (0,)), nothing, counts(3, (1,))],
+             (0, (4, 5)): [counts(3, (2,)), nothing, counts(3, (3,)), nothing, counts(3, (4,)), nothing],
+             (1, (4, 5)): [counts(3, (5,)), nothing, counts(3, (6,)), nothing, counts(3, (7,)), call(root, 6, 2)],
+             (2, (4, 5)): [call(spread, 6, 2), nothing, nothing, reload(2, (6, 7)), reload(1, (6, 7))]})
         for q in range(12):
             tick()

@@ -24,7 +24,6 @@ RAW_BUFS = 13
 AG_BUFS = 5
 COD_BUFS = 5
 LAG = 8
-TINY = 1e-30
 
 FLOPS = 2 * N * D * F + 2 * N * N * F
 
@@ -77,11 +76,23 @@ def tile_simplegcn_pa_t_kernel(tc, x, adjacency, w, b, out):
                     item[1]()
 
         unit = {}
+        wide = {}
+        loops = {}
 
         def load(J, c):
             tile = units.tile([P, 4, PANEL], BF16, tag="unit", name="u%d_%d_%d" % (J, c, len(unit)))
             for h in range(2):
                 unit[(2 * J + h, c)] = tile[:, :, BLK * h:BLK * (h + 1)]
+            wide[(J, c)] = tile
+            if c // 2 == J:
+                flat = tile[:].rearrange("p t w -> p (t w)")
+                h0 = BLK * (c % 2)
+                pair = 2 * PANEL + 2
+                first = flat[:, 0:pair].rearrange("p (e k) -> p e k", e=2)[:, :, h0:h0 + 255:2]
+                start = 4 * PANEL - pair
+                k0 = h0 + 2 * PANEL + 256 - start
+                second = flat[:, start:4 * PANEL].rearrange("p (e k) -> p e k", e=2)[:, :, k0:k0 + 255:2]
+                loops[c] = (first, second)
             for u in range(2):
                 nc.sync.dma_start(out=tile[:, 2 * u:2 * u + 2, :],
                                   in_=adjacency[BLK * c + 256 * u:BLK * c + 256 * (u + 1), PANEL * J:PANEL * (J + 1)].rearrange("(p e) w -> p e w", e=2))
@@ -103,17 +114,13 @@ def tile_simplegcn_pa_t_kernel(tc, x, adjacency, w, b, out):
         def root(b0, nb):
             deg[b0] = small.tile([P, 4 * nb], F32, tag="deg", name="deg%d" % b0)
             nc.vector.tensor_reduce(out=deg[b0][:], in_=cs[b0][:], axis=AX.X, op=ALU.add)
-            dcl = small.tile([P, 4 * nb], F32, tag="dcl")
-            nc.vector.tensor_scalar(out=dcl[:], in0=deg[b0][:], scalar1=1.0, scalar2=TINY, op0=ALU.add, op1=ALU.max)
             sq[b0] = small.tile([P, 4 * nb], F32, tag="sq", name="sq%d" % b0)
-            nc.scalar.activation(out=sq[b0][:], in_=dcl[:], func=ACT.Sqrt)
+            nc.scalar.activation(out=sq[b0][:], in_=deg[b0][:], func=ACT.Sqrt, bias=warm[:, 0:1], scale=1.0)
 
         ready = [0]
 
         def spread(b0, nb):
-            rc = small.tile([P, 4 * nb], F32, tag="rc")
-            nc.vector.reciprocal(out=rc[:], in_=sq[b0][:])
-            nc.vector.scalar_tensor_tensor(out=dinv[:, 4 * b0:4 * (b0 + nb)], in0=deg[b0][:], scalar=-1.0, in1=rc[:], op0=ALU.is_gt, op1=ALU.mult)
+            nc.vector.reciprocal(out=dinv[:, 4 * b0:4 * (b0 + nb)], in_=sq[b0][:])
             for n in range(b0, b0 + nb):
                 vps = t2p.tile([P, 4, P], F32, tag="t2", name="vps%d" % n)
                 for m in range(4):
@@ -146,6 +153,8 @@ def tile_simplegcn_pa_t_kernel(tc, x, adjacency, w, b, out):
                 res = const.tile([P, BLK], F32, name="sum%d" % B)
             if B in sums:
                 nc.vector.tensor_tensor(out=res[:], in0=ps[:], in1=sums[B][:], op=ALU.add)
+            elif last:
+                nc.vector.tensor_scalar_add(out=res[:], in0=ps[:], scalar1=b_f[:, 0:1])
             else:
                 nc.scalar.activation(out=res[:], in_=ps[:], func=ACT.Identity, bias=b_f[:, 0:1], scale=1.0)
                 sums[B] = res
@@ -153,10 +162,13 @@ def tile_simplegcn_pa_t_kernel(tc, x, adjacency, w, b, out):
                 after(1, lambda: store(B, res))
 
         def store(B, res):
-            tq = t2p.tile([P, 4, F], F32, tag="t2")
+            if B % 2 == 0:
+                tq = t2p.tile([P, 4, F], F32, tag="t2", name="tq%d" % B)
+            else:
+                tq = t1p.tile([P, 4, F], F32, tag="t1", name="tq%d" % B)
             for m in range(4):
                 nc.tensor.transpose(out=tq[:, m, :], in_=res[:, P * m:P * (m + 1)], identity=ident_f[:])
-            ot = outp.tile([P, 4, F], F32, tag="ot")
+            ot = outp.tile([P, 4, F], F32, tag="ot", bufs=3)
             nc.scalar.activation(out=ot[:], in_=tq[:], func=ACT.Relu)
             nc.sync.dma_start(out=out[BLK * B:BLK * (B + 1), :].rearrange("(m p) f -> p m f", p=P), in_=ot[:])
 
@@ -228,21 +240,22 @@ def tile_simplegcn_pa_t_kernel(tc, x, adjacency, w, b, out):
 
         planes = {}
 
-        def straight(job, n):
+        def straight(job, n, engine):
             a, cols = job
             B = cols[n]
             pl = plain.tile([P, 4, BLK], BF16, tag="pl", align_bytes=64, name="pl%d_%d" % (B, a))
             nc.vector.tensor_tensor(out=pl[:], in0=unit[(B, a)], in1=tables[job][:, :, BLK * n:BLK * (n + 1)], op=ALU.mult)
             ag = group_tile(B, a)
-            nc.scalar.copy(out=grouped(ag[:]), in_=columns(pl[:]))
+            if engine == 0:
+                nc.vector.tensor_copy(out=grouped(ag[:]), in_=columns(pl[:]))
+            else:
+                nc.scalar.copy(out=grouped(ag[:]), in_=columns(pl[:]))
             after(LAG, lambda: finish(B, a, ag))
 
         def diagonal(a):
             u = unit[(a, a)]
-            for k in range(4):
-                s = 256 * (k // 2) + k % 2
-                d = u[:, k, s:s + 255:2]
-                nc.vector.tensor_tensor(out=d, in0=d, in1=ident_b[:], op=ALU.add)
+            for d in loops[a]:
+                nc.vector.tensor_tensor(out=d, in0=d, in1=ident_b[:].unsqueeze(1).to_broadcast([P, 2, P]), op=ALU.add)
             pl = plain.tile([P, 4, BLK], BF16, tag="pl", align_bytes=64, name="pl%d_%d" % (a, a))
             v0 = BLK * (a % 4)
             for t in range(4):
@@ -303,7 +316,7 @@ def tile_simplegcn_pa_t_kernel(tc, x, adjacency, w, b, out):
                             mirrored(hs[2 * n + h])
                             turn_next()
                             done()
-                        straight(job, n)
+                        straight(job, n, 1)
                         done()
                 for e in list(extra):
                     e()
@@ -416,13 +429,11 @@ def tile_simplegcn_pa_t_kernel(tc, x, adjacency, w, b, out):
              (4, (4,)), (5, (5,)), (4, (5,))] + [(a, (4, 5)) for a in range(4)]
             + [(6, (6,)), (7, (7,)), (6, (7,))] + [(a, (6, 7)) for a in (4, 5, 0, 1, 2, 3)],
             {(0, (1,)): [counts(1, (4, 5)), counts(1, (6, 7)), call(root, 2, 2), call(spread, 2, 2)],
-             (2, (3,)): [counts(2, (0,)), counts(2, (1,)), counts(2, (2,))],
-             (0, (2, 3)): [counts(2, (3,)), nothing, counts(2, (4,)), nothing, counts(2, (5,))],
-             (1, (2, 3)): [counts(2, (6,)), nothing, counts(2, (7,)), call(root, 4, 2), nothing, call(spread, 4, 2)],
+             (2, (3,)): [counts(2, (0, 1, 2)), counts(2, (3, 4)), counts(2, (5, 6))],
+             (0, (2, 3)): [counts(2, (7,)), call(root, 4, 2), call(spread, 4, 2)],
              (4, (4,)): [reload(1, (4, 5))],
-             (4, (5,)): [counts(3, (0,)), nothing, counts(3, (1,))],
-             (0, (4, 5)): [counts(3, (2,)), nothing, counts(3, (3,)), nothing, counts(3, (4,)), nothing],
-             (1, (4, 5)): [counts(3, (5,)), nothing, counts(3, (6,)), nothing, counts(3, (7,)), call(root, 6, 2)],
-             (2, (4, 5)): [call(spread, 6, 2), nothing, nothing, reload(2, (6, 7)), reload(1, (6, 7))]})
+             (4, (5,)): [counts(3, (0, 1)), counts(3, (2, 3)), counts(3, (4, 5))],
+             (0, (4, 5)): [counts(3, (6,)), counts(3, (7,)), call(root, 6, 2), call(spread, 6, 2)],
+             (2, (4, 5)): [nothing, nothing, nothing, reload(2, (6, 7)), reload(1, (6, 7))]})
         for q in range(12):
             tick()

@@ -19,9 +19,9 @@ F = 128
 PANEL = 1024
 BLK = 512
 NBLK = N // BLK
-UNIT_BUFS = 11
-RAW_BUFS = 13
-AG_BUFS = 5
+UNIT_BUFS = 9
+RAW_BUFS = 19
+AG_BUFS = 4
 COD_BUFS = 5
 LAG = 8
 
@@ -112,6 +112,10 @@ def tile_simplegcn_pa_t_kernel(tc, x, adjacency, w, b, out):
         sq = {}
 
         def root(b0, nb):
+            with tc.high_priority():
+                root_now(b0, nb)
+
+        def root_now(b0, nb):
             deg[b0] = small.tile([P, 4 * nb], F32, tag="deg", name="deg%d" % b0)
             nc.vector.tensor_reduce(out=deg[b0][:], in_=cs[b0][:], axis=AX.X, op=ALU.add)
             sq[b0] = small.tile([P, 4 * nb], F32, tag="sq", name="sq%d" % b0)
@@ -120,6 +124,10 @@ def tile_simplegcn_pa_t_kernel(tc, x, adjacency, w, b, out):
         ready = [0]
 
         def spread(b0, nb):
+            with tc.high_priority():
+                spread_now(b0, nb)
+
+        def spread_now(b0, nb):
             nc.vector.reciprocal(out=dinv[:, 4 * b0:4 * (b0 + nb)], in_=sq[b0][:])
             for n in range(b0, b0 + nb):
                 vps = t2p.tile([P, 4, P], F32, tag="t2", name="vps%d" % n)
@@ -145,14 +153,14 @@ def tile_simplegcn_pa_t_kernel(tc, x, adjacency, w, b, out):
                 after(1, lambda: close(B, a[0], J == 3))
 
         def close(B, ps, last):
-            if last:
-                res = outp.tile([P, BLK], F32, tag="res")
-            elif B in sums:
+            if B in sums:
                 res = sums[B]
+            elif last:
+                res = sums[B - 2]
             else:
                 res = const.tile([P, BLK], F32, name="sum%d" % B)
             if B in sums:
-                nc.vector.tensor_tensor(out=res[:], in0=ps[:], in1=sums[B][:], op=ALU.add)
+                nc.vector.tensor_tensor(out=res[:], in0=ps[:], in1=res[:], op=ALU.add)
             elif last:
                 nc.vector.tensor_scalar_add(out=res[:], in0=ps[:], scalar1=b_f[:, 0:1])
             else:
@@ -227,6 +235,10 @@ def tile_simplegcn_pa_t_kernel(tc, x, adjacency, w, b, out):
                     nc.tensor.transpose(out=dst[:, e, u, :], in_=words[:, P * u:P * (u + 1)], identity=ident_f[:])
             turned[half] = tp
 
+        def turn_first(half):
+            with tc.high_priority():
+                turn(half)
+
         def mirrored(half):
             job, n, h = half
             a, cols = job
@@ -277,7 +289,7 @@ def tile_simplegcn_pa_t_kernel(tc, x, adjacency, w, b, out):
 
             def turn_next():
                 if turns[0] < len(queue) and queue[turns[0]][0] in tables:
-                    turn(queue[turns[0]])
+                    turn_first(queue[turns[0]])
                     turns[0] += 1
 
             for i in range(len(jobs)):
@@ -428,12 +440,11 @@ def tile_simplegcn_pa_t_kernel(tc, x, adjacency, w, b, out):
              (2, (2,)), (3, (3,)), (2, (3,)), (0, (2, 3)), (1, (2, 3)),
              (4, (4,)), (5, (5,)), (4, (5,))] + [(a, (4, 5)) for a in range(4)]
             + [(6, (6,)), (7, (7,)), (6, (7,))] + [(a, (6, 7)) for a in (4, 5, 0, 1, 2, 3)],
-            {(0, (1,)): [counts(1, (4, 5)), counts(1, (6, 7)), call(root, 2, 2), call(spread, 2, 2)],
+            {(0, (1,)): [counts(1, (4, 5)), counts(1, (6, 7)), call(root, 2, 2), call(spread, 2, 2), call(regroup_early, 2, 4, 0), call(regroup_early, 2, 5, 1), call(regroup_early, 2, 6, 0), call(regroup_early, 3, 4, 0), call(regroup_early, 3, 5, 1), call(regroup_early, 3, 6, 1)],
              (2, (3,)): [counts(2, (0, 1, 2)), counts(2, (3, 4)), counts(2, (5, 6))],
              (0, (2, 3)): [counts(2, (7,)), call(root, 4, 2), call(spread, 4, 2)],
-             (4, (4,)): [reload(1, (4, 5))],
              (4, (5,)): [counts(3, (0, 1)), counts(3, (2, 3)), counts(3, (4, 5))],
              (0, (4, 5)): [counts(3, (6,)), counts(3, (7,)), call(root, 6, 2), call(spread, 6, 2)],
-             (2, (4, 5)): [nothing, nothing, nothing, reload(2, (6, 7)), reload(1, (6, 7))]})
+             (2, (4, 5)): [nothing, nothing, nothing, reload(2, (6, 7)), reload(1, (7,))]})
         for q in range(12):
             tick()

from contextlib import ExitStack

import concourse.mybir as mybir
from concourse.masks import make_identity

F32 = mybir.dt.float32
BF16 = mybir.dt.bfloat16
U32 = mybir.dt.uint32
U8 = mybir.dt.uint8
FP8X4 = mybir.dt.float8_e4m3fn_x4
ALU = mybir.AluOpType
ACT = mybir.ActivationFunctionType
AX = mybir.AxisListType

P = 128
N = 4096
D = 512
F = 128
PANEL = 1024
BLK = 512
NBLK = N // BLK
UNIT_BUFS = 9
RAW_BUFS = 19
AG_BUFS = 4
COD_BUFS = 5
LAG = 8

FLOPS = 2 * N * D * F + 2 * N * N * F


def tile_simplegcn_pa_t_kernel(tc, x, adjacency, w, b, out):
    nc = tc.nc
    with ExitStack() as ctx:
        const = ctx.enter_context(tc.tile_pool(name="const", bufs=1))
        units = ctx.enter_context(tc.tile_pool(name="units", bufs=UNIT_BUFS))
        raws = ctx.enter_context(tc.tile_pool(name="raws", bufs=RAW_BUFS))
        grp = ctx.enter_context(tc.tile_pool(name="grp", bufs=AG_BUFS))
        rpool = ctx.enter_context(tc.tile_pool(name="rpool", bufs=2))
        plain = ctx.enter_context(tc.tile_pool(name="plain", bufs=3))
        cod = ctx.enter_context(tc.tile_pool(name="cod", bufs=COD_BUFS))
        small = ctx.enter_context(tc.tile_pool(name="small", bufs=2))
        outp = ctx.enter_context(tc.tile_pool(name="outp", bufs=2))
        t1p = ctx.enter_context(tc.psum_pool(name="t1p", bufs=2))
        t2p = ctx.enter_context(tc.psum_pool(name="t2p", bufs=1))
        csp = ctx.enter_context(tc.psum_pool(name="csp", bufs=1))
        accp = ctx.enter_context(tc.psum_pool(name="accp", bufs=4))

        ident_f = const.tile([P, P], F32)
        make_identity(nc, ident_f[:])
        ident_b = const.tile([P, P], BF16)
        nc.vector.tensor_copy(out=ident_b[:], in_=ident_f[:])
        ones = const.tile([P, 2], BF16)
        nc.vector.memset(ones[:], 1.0)
        warm = const.tile([P, 1], F32)
        nc.vector.memset(warm[:], 1.0)
        warm2 = const.tile([P, 1], F32)
        nc.scalar.activation(out=warm2[:], in_=warm[:], func=ACT.Sqrt)

        vb = const.tile([P, 2 * PANEL], F32)
        dinv = const.tile([P, 4 * NBLK], F32)
        xw_c = const.tile([P, NBLK * F], U32, align_bytes=64)
        xw_s = const.tile([P, NBLK * F], U8, align_bytes=64)
        b_f = const.tile([P, 1], F32)

        later = []
        step = [0]

        def after(steps, action):
            later.append((step[0] + steps, action))

        def tick():
            step[0] += 1
            for item in list(later):
                if item[0] <= step[0]:
                    later.remove(item)
                    item[1]()

        unit = {}
        wide = {}
        loops = {}

        def load(J, c):
            tile = units.tile([P, 4, PANEL], BF16, tag="unit", name="u%d_%d_%d" % (J, c, len(unit)))
            for h in range(2):
                unit[(2 * J + h, c)] = tile[:, :, BLK * h:BLK * (h + 1)]
            wide[(J, c)] = tile
            if c // 2 == J:
                flat = tile[:].rearrange("p t w -> p (t w)")
                h0 = BLK * (c % 2)
                pair = 2 * PANEL + 2
                first = flat[:, 0:pair].rearrange("p (e k) -> p e k", e=2)[:, :, h0:h0 + 255:2]
                start = 4 * PANEL - pair
                k0 = h0 + 2 * PANEL + 256 - start
                second = flat[:, start:4 * PANEL].rearrange("p (e k) -> p e k", e=2)[:, :, k0:k0 + 255:2]
                loops[c] = (first, second)
            for u in range(2):
                nc.sync.dma_start(out=tile[:, 2 * u:2 * u + 2, :],
                                  in_=adjacency[BLK * c + 256 * u:BLK * c + 256 * (u + 1), PANEL * J:PANEL * (J + 1)].rearrange("(p e) w -> p e w", e=2))

        cs = {}

        def count(b0, nb, c):
            if b0 not in cs:
                cs[b0] = csp.tile([P, 4 * nb, NBLK], F32, tag="cs", name="cs%d" % b0)
            for m in range(4 * nb):
                u = unit[(b0 + m // 4, c)]
                s = 256 * (m % 4 // 2) + m % 2
                for t in range(4):
                    nc.tensor.matmul(out=cs[b0][:, m, c:c + 1], lhsT=u[:, t, s:s + 255:2], rhs=ones[:, 0:1], start=(t == 0), stop=(t == 3))

        deg = {}
        sq = {}

        def root(b0, nb):
            with tc.high_priority():
                root_now(b0, nb)

        def root_now(b0, nb):
            deg[b0] = small.tile([P, 4 * nb], F32, tag="deg", name="deg%d" % b0)
            nc.vector.tensor_reduce(out=deg[b0][:], in_=cs[b0][:], axis=AX.X, op=ALU.add)
            sq[b0] = small.tile([P, 4 * nb], F32, tag="sq", name="sq%d" % b0)
            nc.scalar.activation(out=sq[b0][:], in_=deg[b0][:], func=ACT.Sqrt, bias=warm[:, 0:1], scale=1.0)

        ready = [0]

        def spread(b0, nb):
            with tc.high_priority():
                spread_now(b0, nb)

        def spread_now(b0, nb):
            nc.vector.reciprocal(out=dinv[:, 4 * b0:4 * (b0 + nb)], in_=sq[b0][:])
            for n in range(b0, b0 + nb):
                vps = t2p.tile([P, 4, P], F32, tag="t2", name="vps%d" % n)
                for m in range(4):
                    nc.tensor.transpose(out=vps[:, m, :], in_=dinv[:, 4 * n + m:4 * n + m + 1].to_broadcast([P, P]), identity=ident_f[:])
                nc.scalar.copy(out=vb[:, BLK * (n % 4):BLK * (n % 4 + 1)].rearrange("p (u k e) -> p u k e", u=2, e=2),
                               in_=vps[:].rearrange("p (u e) k -> p u k e", u=2))
            ready[0] = b0 + nb

        acc = {}
        sums = {}

        def multiply(B, c, pair):
            J = max(B, c) // 2
            passes = 2 * J + 2 if J == B // 2 else 2
            if (B, J) not in acc:
                acc[(B, J)] = [accp.tile([P, BLK], F32, tag="acc", name="acc%d_%d" % (B, J)), 0]
            a = acc[(B, J)]
            a[1] += 1
            nc.tensor.matmul_mx(out=a[0][:], lhsT=xw_c[:, F * c:F * (c + 1)].bitcast(FP8X4), lhsT_scale=xw_s[:, F * c:F * (c + 1)],
                                rhs=pair[0][:].bitcast(FP8X4), rhs_scale=pair[1][:], start=(a[1] == 1), stop=(a[1] == passes))
            if a[1] == passes:
                after(1, lambda: close(B, a[0], J == 3))

        def close(B, ps, last):
            if B in sums:
                res = sums[B]
            elif last:
                res = sums[B - 2]
            else:
                res = const.tile([P, BLK], F32, name="sum%d" % B)
            if B in sums:
                nc.vector.tensor_tensor(out=res[:], in0=ps[:], in1=res[:], op=ALU.add)
            elif last:
                nc.vector.tensor_scalar_add(out=res[:], in0=ps[:], scalar1=b_f[:, 0:1])
            else:
                nc.scalar.activation(out=res[:], in_=ps[:], func=ACT.Identity, bias=b_f[:, 0:1], scale=1.0)
                sums[B] = res
            if last:
                after(1, lambda: store(B, res))

        def store(B, res):
            if B % 2 == 0:
                tq = t2p.tile([P, 4, F], F32, tag="t2", name="tq%d" % B)
            else:
                tq = t1p.tile([P, 4, F], F32, tag="t1", name="tq%d" % B)
            for m in range(4):
                nc.tensor.transpose(out=tq[:, m, :], in_=res[:, P * m:P * (m + 1)], identity=ident_f[:])
            ot = outp.tile([P, 4, F], F32, tag="ot", bufs=3)
            nc.scalar.activation(out=ot[:], in_=tq[:], func=ACT.Relu)
            nc.sync.dma_start(out=out[BLK * B:BLK * (B + 1), :].rearrange("(m p) f -> p m f", p=P), in_=ot[:])

        def quantise(ag):
            cd = cod.tile([P, BLK], U32, tag="cd", align_bytes=64)
            sc = cod.tile([P, BLK], U8, tag="sc", align_bytes=64)
            nc.vector.quantize_mx(out=cd[:].bitcast(FP8X4), scales=sc[:], in_=ag[:])
            return cd, sc

        def finish(B, c, ag):
            pair = quantise(ag)
            after(1, lambda: multiply(B, c, pair))

        def columns(ap):
            return ap.rearrange("p t (n i) -> p n t i", i=4)

        def grouped(ap):
            return ap.rearrange("p (n i t) -> p n t i", i=4, t=4)

        def group_tile(B, c):
            return grp.tile([P, 4 * BLK], BF16, tag="ag", align_bytes=64, name="ag%d_%d" % (B, c))

        raw = {}

        def regroup(B, c, t, engine):
            if engine == 0:
                nc.vector.tensor_copy(out=grouped(t[:]), in_=columns(unit[(B, c)]))
            else:
                nc.scalar.copy(out=grouped(t[:]), in_=columns(unit[(B, c)]))
            raw[(B, c)] = t

        def regroup_early(B, c, engine):
            regroup(B, c, raws.tile([P, 4 * BLK], BF16, tag="raw", align_bytes=64, name="raw%d_%d" % (B, c)), engine)

        tables = {}

        def table(job):
            a, cols = job
            rt = rpool.tile([P, 4, PANEL], BF16, tag="rt", name="rt%d_%d" % (a, cols[0]))
            tables[job] = rt
            col0 = BLK * (cols[0] % 4)
            width = BLK * len(cols)
            for k in range(4):
                nc.scalar.activation(out=rt[:, k, 0:width], in_=vb[:, col0:col0 + width], func=ACT.Copy, scale=dinv[:, 4 * a + k:4 * a + k + 1])

        turned = {}

        def turn(half):
            job, n, h = half
            rt = tables[job]
            tp = t1p.tile([P, BLK], F32, tag="t1", name="tp%d_%d_%d" % (job[0], job[1][n], h))
            dst = tp[:].rearrange("p (q e u) -> p e u q", e=2, u=2)
            for e in range(2):
                words = rt[:, 2 * h + e, BLK * n:BLK * (n + 1)].bitcast(F32)
                for u in range(2):
                    nc.tensor.transpose(out=dst[:, e, u, :], in_=words[:, P * u:P * (u + 1)], identity=ident_f[:])
            turned[half] = tp

        def turn_first(half):
            with tc.high_priority():
                turn(half)

        def mirrored(half):
            job, n, h = half
            a, cols = job
            c = cols[n]
            products = turned[half][:].bitcast(BF16)
            ag = raw[(a, c)]
            part = ag[:, PANEL * h:PANEL * (h + 1)]
            nc.vector.tensor_tensor(out=part, in0=part, in1=products, op=ALU.mult)
            if h == 1:
                after(2, lambda: finish(a, c, ag))

        planes = {}

        def straight(job, n, engine):
            a, cols = job
            B = cols[n]
            pl = plain.tile([P, 4, BLK], BF16, tag="pl", align_bytes=64, name="pl%d_%d" % (B, a))
            nc.vector.tensor_tensor(out=pl[:], in0=unit[(B, a)], in1=tables[job][:, :, BLK * n:BLK * (n + 1)], op=ALU.mult)
            ag = group_tile(B, a)
            if engine == 0:
                nc.vector.tensor_copy(out=grouped(ag[:]), in_=columns(pl[:]))
            else:
                nc.scalar.copy(out=grouped(ag[:]), in_=columns(pl[:]))
            after(LAG, lambda: finish(B, a, ag))

        def diagonal(a):
            u = unit[(a, a)]
            for d in loops[a]:
                nc.vector.tensor_tensor(out=d, in0=d, in1=ident_b[:].unsqueeze(1).to_broadcast([P, 2, P]), op=ALU.add)
            pl = plain.tile([P, 4, BLK], BF16, tag="pl", align_bytes=64, name="pl%d_%d" % (a, a))
            v0 = BLK * (a % 4)
            for t in range(4):
                nc.vector.scalar_tensor_tensor(out=pl[:, t, :], in0=u[:, t, :], scalar=dinv[:, 4 * a + t:4 * a + t + 1],
                                               in1=vb[:, v0:v0 + BLK], op0=ALU.mult, op1=ALU.mult)
            ag = group_tile(a, a)
            nc.scalar.copy(out=grouped(ag[:]), in_=columns(pl[:]))
            after(LAG, lambda: finish(a, a, ag))

        def halves(job):
            a, cols = job
            return [] if cols == (a,) else [(job, n, h) for n in range(len(cols)) for h in range(2)]

        def run(jobs, fill):
            queue = []
            for job in jobs:
                queue.extend(halves(job))
            turns = [0]

            def turn_next():
                if turns[0] < len(queue) and queue[turns[0]][0] in tables:
                    turn_first(queue[turns[0]])
                    turns[0] += 1

            for i in range(len(jobs)):
                job = jobs[i]
                a, cols = job
                extra = list(fill.get(job, []))

                def early():
                    for nxt in jobs[i:i + 2]:
                        if nxt[1] != (nxt[0],) and nxt not in tables and nxt[1][-1] < ready[0]:
                            table(nxt)

                def done():
                    tick()
                    if extra:
                        e = extra[0]
                        extra.remove(e)
                        e()
                    early()

                early()
                if cols == (a,):
                    diagonal(a)
                    done()
                else:
                    hs = halves(job)
                    for n in range(len(cols)):
                        if (a, cols[n]) not in raw:
                            regroup(a, cols[n], group_tile(a, cols[n]), 0)
                    while_turned = [half in turned for half in hs[0:2]]
                    for known in while_turned:
                        if not known:
                            turn_next()
                    for n in range(len(cols)):
                        for h in range(2):
                            mirrored(hs[2 * n + h])
                            turn_next()
                            done()
                        straight(job, n, 1)
                        done()
                for e in list(extra):
                    e()
                    early()

        def features(fill):
            w_g = const.tile([P, F, 4], BF16, align_bytes=64)
            nc.vector.tensor_copy(out=w_g[:], in_=w_raw[:].rearrange("q t f -> q f t"))
            w_c = const.tile([P, F], U32, align_bytes=64)
            w_s = const.tile([P, F], U8, align_bytes=64)
            nc.vector.quantize_mx(out=w_c[:].bitcast(FP8X4), scales=w_s[:], in_=w_g[:].rearrange("q f t -> q (f t)"))
            nc.vector.tensor_copy(out=b_f[:], in_=b_raw[:])
            xw_g = [grp.tile([P, 4 * BLK], BF16, tag="ag", align_bytes=64, name="xw%d" % hh) for hh in range(2)]
            codes = {}
            products = {}

            def regroup_x(c):
                xg = plain.tile([P, 4 * BLK], BF16, tag="pl", align_bytes=64, name="xg%d" % c)
                xg32 = xg[:].bitcast(F32).rearrange("p (r i u) -> p r i u", r=4, u=2)
                for k in range(2):
                    tp = accp.tile([P, 2, 2, P], F32, tag="acc", name="xt%d_%d" % (c, k))
                    for e in range(2):
                        xr = xunits[c // 2][:, 2 * (c % 2) + k, e, :].bitcast(F32)
                        for u2 in range(2):
                            nc.tensor.transpose(out=tp[:, e, u2, :], in_=xr[:, P * u2:P * (u2 + 1)], identity=ident_f[:])
                    if k == 0:
                        nc.scalar.copy(out=xg32[:, 0:2], in_=tp[:].rearrange("p e u i -> p e i u"))
                    else:
                        nc.vector.tensor_copy(out=xg32[:, 2:4], in_=tp[:].rearrange("p e u i -> p e i u"))
                codes[c] = xg

            def times_w(c):
                xc, xs = codes[c]
                xwp = t1p.tile([P, 4, F], F32, tag="t1", name="xwp%d" % c)
                for t in range(4):
                    nc.tensor.matmul_mx(out=xwp[:, t, :], lhsT=xc[:, P * t:P * (t + 1)].bitcast(FP8X4),
                                        lhsT_scale=xs[:, P * t:P * (t + 1)], rhs=w_c[:].bitcast(FP8X4), rhs_scale=w_s[:],
                                        start=True, stop=True)
                products[c] = xwp

            def collect(c):
                dst = xw_g[c // 4][:].rearrange("p (c f t) -> p c f t", c=4, t=4)[:, c % 4]
                nc.scalar.copy(out=dst, in_=products[c][:].rearrange("p t f -> p f t"))
                if c % 4 == 3:
                    hh = c // 4
                    nc.vector.quantize_mx(out=xw_c[:, BLK * hh:BLK * (hh + 1)].bitcast(FP8X4), scales=xw_s[:, BLK * hh:BLK * (hh + 1)], in_=xw_g[hh][:])

            for i in range(NBLK + 3):
                if i < NBLK:
                    regroup_x(i)
                if 1 <= i < NBLK + 1:
                    codes[i - 1] = quantise(codes[i - 1])
                if 2 <= i < NBLK + 2:
                    times_w(i - 2)
                if i >= 3:
                    collect(i - 3)
                for e in fill.get(i, ()):
                    e()

        def own_first(J):
            return [2 * J, 2 * J + 1] + [c for c in range(NBLK) if c // 2 != J]

        for c in own_first(0):
            load(0, c)
        w_raw = const.tile([P, 4, F], BF16)
        nc.sync.dma_start(out=w_raw[:].rearrange("q (u e) f -> q u e f", u=2), in_=w.rearrange("(u q e) f -> q u e f", u=2, e=2))
        b_raw = const.tile([P, 1], BF16)
        nc.sync.dma_start(out=b_raw[:], in_=b.rearrange("(p o) -> p o", o=1))
        xunits = []
        for g in range(4):
            xu = units.tile([P, 4, 2, D], BF16, tag="unit", name="xu%d" % g)
            nc.sync.dma_start(out=xu[:].rearrange("p r e d -> p r (e d)"),
                              in_=x[PANEL * g:PANEL * (g + 1), :].rearrange("(r p e) d -> p r (e d)", p=P, e=2))
            xunits.append(xu)
        for J in range(1, 4):
            for c in own_first(J):
                load(J, c)

        def call(f, *args):
            return lambda: f(*args)

        def counts(J, places):
            def go():
                for q in places:
                    count(2 * J, 2, own_first(J)[q])
            return go

        def reload(J, rows):
            def go():
                for c in rows:
                    load(J, c)
            return go

        def nothing():
            return None

        for c in own_first(0):
            count(0, 2, c)
            for b1 in range(2):
                if c > b1:
                    regroup_early(b1, c, 1 if c % 3 == 0 else 0)
        root(0, 2)
        spread(0, 2)
        features({1: [call(diagonal, 0)],
                  4: [call(diagonal, 1)],
                  7: [counts(1, (0,))], 8: [counts(1, (1,))], 9: [counts(1, (2,))], 10: [counts(1, (3,))]})
        tick()
        run([(0, (1,)),
             (2, (2,)), (3, (3,)), (2, (3,)), (0, (2, 3)), (1, (2, 3)),
             (4, (4,)), (5, (5,)), (4, (5,))] + [(a, (4, 5)) for a in range(4)]
            + [(6, (6,)), (7, (7,)), (6, (7,))] + [(a, (6, 7)) for a in (4, 5, 0, 1, 2, 3)],
            {(0, (1,)): [counts(1, (4, 5)), counts(1, (6, 7)), call(root, 2, 2), call(spread, 2, 2), call(regroup_early, 2, 4, 0), call(regroup_early, 2, 5, 1), call(regroup_early, 2, 6, 0), call(regroup_early, 3, 4, 0), call(regroup_early, 3, 5, 1), call(regroup_early, 3, 6, 1)],
             (2, (3,)): [counts(2, (0, 1, 2)), counts(2, (3, 4)), counts(2, (5, 6))],
             (0, (2, 3)): [counts(2, (7,)), call(root, 4, 2), call(spread, 4, 2)],
             (4, (5,)): [counts(3, (0, 1)), counts(3, (2, 3)), counts(3, (4, 5))],
             (0, (4, 5)): [counts(3, (6,)), counts(3, (7,)), call(root, 6, 2), call(spread, 6, 2)],
             (2, (4, 5)): [nothing, nothing, nothing, reload(2, (6, 7)), reload(1, (7,))]})
        for q in range(12):
            tick()
